import numpy as np
import ml_dtypes


def mxq(x, axis, fmt="e4m3"):
    dtype, down = {"e4m3": (ml_dtypes.float8_e4m3fn, 7), "e5m2": (ml_dtypes.float8_e5m2, 14)}[fmt]
    v = np.moveaxis(np.asarray(x, np.float32).astype(ml_dtypes.bfloat16).astype(np.float64), axis, -1)
    blocks = v.reshape(v.shape[:-1] + (-1, 32))
    amax = np.abs(blocks).max(-1, keepdims=True)
    byte = np.maximum(np.where(amax > 0, np.frexp(amax)[1] - 1 + 127, 0) - down, 1)
    scale = np.exp2(byte - 127.0)
    codes = (blocks / scale).astype(np.float32).astype(dtype).astype(np.float64)
    return np.moveaxis((codes * scale).reshape(v.shape), -1, axis)


WIDE = False


def mx_kscale(k):
    if not WIDE:
        return np.ones(k)
    levels = np.array([10, -10, 5, -5, 0])
    a = np.random.permutation(np.resize(levels, k // 512 * 4)).reshape(k // 512, 4)
    idx = np.arange(k)
    return np.exp2(a[idx // 512, idx % 128 // 32])


BF16 = ml_dtypes.bfloat16


def bf(x):
    return np.asarray(x, np.float32).astype(BF16)


def f64(x):
    return np.asarray(x).astype(np.float64)


B, S, E, H, G, P, K3, K5, K7 = 2, 512, 1024, 16, 4, 3, 3, 5, 7
D = E // H
HK = H // G


def dwconv_causal(x, w, b):
    k = w.shape[1]
    xp = np.pad(x, ((0, 0), (0, 0), (k - 1, 0), (0, 0)))
    y = b
    for i in range(k):
        y = y + xp[:, :, i:i + S, :] * w[:, i]
    return y


def split_heads(t):
    return t.reshape(B, S, H, D).swapaxes(1, 2)


def tranception_mix(t, ws_bs):
    parts = [t[:, :HK]]
    for g, (w, b) in enumerate(ws_bs):
        parts.append(dwconv_causal(t[:, (g + 1) * HK:(g + 2) * HK], w, b))
    return np.concatenate(parts, axis=1)


def setup_inputs():
    s = mx_kscale(E)
    inp = {'hidden_states': bf(np.random.standard_normal((B, S, E)) * s),
           'c_attn_w': bf(np.random.standard_normal((E, P * E)) / np.sqrt(E) / s[:, None]),
           'c_attn_b': bf(np.random.standard_normal(P * E) * 0.3)}
    for pre in ('q', 'k', 'v'):
        for kern in (K3, K5, K7):
            inp[pre + 'w' + str(kern)] = bf(np.random.standard_normal((D, kern)) / kern)
            inp[pre + 'b' + str(kern)] = bf(np.random.standard_normal(D) * 0.2)
    return inp


def reference(hidden_states, c_attn_w, c_attn_b,
              qw3, qb3, qw5, qb5, qw7, qb7,
              kw3, kb3, kw5, kb5, kw7, kb7,
              vw3, vb3, vw5, vb5, vw7, vb7):
    qkv = (mxq(f64(hidden_states), 2, 'e4m3') @ mxq(f64(c_attn_w), 0, 'e4m3')) + f64(c_attn_b)
    q, k, v = np.split(qkv, P, axis=-1)
    q, k, v = split_heads(q), split_heads(k), split_heads(v)
    q = tranception_mix(q, [(f64(qw3), f64(qb3)), (f64(qw5), f64(qb5)), (f64(qw7), f64(qb7))])
    k = tranception_mix(k, [(f64(kw3), f64(kb3)), (f64(kw5), f64(kb5)), (f64(kw7), f64(kb7))])
    v = tranception_mix(v, [(f64(vw3), f64(vb3)), (f64(vw5), f64(vb5)), (f64(vw7), f64(vb7))])
    return q, k, v

@@ -1,0 +1,278 @@
+import concourse.mybir as mybir
+from concourse.masks import make_identity
+
+F32 = mybir.dt.float32
+BF16 = mybir.dt.bfloat16
+U32 = mybir.dt.uint32
+U8 = mybir.dt.uint8
+FP8X4 = mybir.dt.float8_e4m3fn_x4
+ADD = mybir.AluOpType.add
+SUB = mybir.AluOpType.subtract
+MULT = mybir.AluOpType.mult
+IDENTITY = mybir.ActivationFunctionType.Identity
+
+P = 128
+PACK = 4
+K_PASS = P * PACK
+B, S, E, D = 2, 512, 1024, 64
+PASSES = E // K_PASS
+PROJ = 3
+GROUPS = 4
+TAPS = (1, 3, 5, 7)
+GROUP_COLS = E // GROUPS
+TILES = GROUP_COLS // P
+TOKEN_TILES = S // P
+EDGE = 8
+SLOT = 16
+GROUP_ORDER = (3, 0, 2, 1)
+AHEAD = 2
+
+FLOPS = 2 * B * S * E * PROJ * E + 2 * B * S * PROJ * GROUP_COLS * sum(TAPS[1:])
+
+
+def tile_tranceptionblockattention_pa_kernel(
+    tc, hidden_states, c_attn_w, c_attn_b,
+    qw3, qb3, qw5, qb5, qw7, qb7,
+    kw3, kb3, kw5, kb5, kw7, kb7,
+    vw3, vb3, vw5, vb5, vw7, vb7,
+    out_0, out_1, out_2,
+):
+    nc = tc.nc
+    conv_w = ((qw3, qw5, qw7), (kw3, kw5, kw7), (vw3, vw5, vw7))
+    conv_b = ((qb3, qb5, qb7), (kb3, kb5, kb7), (vb3, vb5, vb7))
+    outs = (out_0, out_1, out_2)
+
+    group_seq = []
+    steps = []
+    for pr in range(PROJ):
+        for g in GROUP_ORDER:
+            group_seq.append((pr, g))
+        for pair in range(GROUPS // 2):
+            for f in range(TILES):
+                for g in GROUP_ORDER[2 * pair:2 * pair + 2]:
+                    steps.append((pr, g, f))
+
+    with tc.tile_pool(name="keep", bufs=1) as keep, \
+            tc.tile_pool(name="wg_pool", bufs=3) as wg_pool, \
+            tc.tile_pool(name="acc_pool", bufs=AHEAD + 2) as acc_pool, \
+            tc.tile_pool(name="out_pool", bufs=4) as out_pool, \
+            tc.psum_pool(name="psum", bufs=2) as psum, \
+            tc.manual_schedule():
+
+        bias_rows = keep.tile([P, P], BF16)
+        nc.vector.memset(bias_rows[:], 0.0)
+        par_in = keep.tile([P, GROUPS, 4, 2, SLOT], BF16)
+        nc.vector.memset(par_in[:], 0.0)
+        ident_f32 = keep.tile([P, P], F32)
+        make_identity(nc, ident_f32[:])
+        ident_bf = keep.tile([P, P], BF16)
+        make_identity(nc, ident_bf[:])
+        twice = keep.tile([P, 2, D], BF16)
+        nc.vector.tensor_copy(out=twice[:], in_=ident_bf[:, 0:D].unsqueeze(1).to_broadcast([P, 2, D]))
+
+        nc.sync.dma_start(out=bias_rows[0:PROJ * E // P, :], in_=c_attn_b.rearrange("(n m) -> n m", m=P))
+
+        w_raw = []
+        for pr in range(PROJ):
+            w_raw_pr = keep.tile([P, PASSES, PACK, E], BF16, name="w_raw%d" % pr)
+            w_raw.append(w_raw_pr)
+
+        def load_w(pr, first_col, n_cols):
+            for c in range(PASSES):
+                nc.sync.dma_start(
+                    out=w_raw[pr][:, c, :, first_col:first_col + n_cols],
+                    in_=c_attn_w[c * K_PASS:(c + 1) * K_PASS, pr * E + first_col:pr * E + first_col + n_cols]
+                    .rearrange("(p j) n -> p j n", j=PACK),
+                )
+
+        x_raw = keep.tile([P, B * TOKEN_TILES, E], BF16)
+        load_w(0, GROUP_ORDER[0] * GROUP_COLS, GROUP_COLS)
+        for b in range(B):
+            nc.sync.dma_start(
+                out=x_raw[:, b * TOKEN_TILES:(b + 1) * TOKEN_TILES, :],
+                in_=hidden_states[b].rearrange("(t p) k -> p t k", p=P),
+            )
+        for g in GROUP_ORDER[1:]:
+            load_w(0, g * GROUP_COLS, GROUP_COLS)
+        for pr in range(1, PROJ):
+            load_w(pr, 0, E)
+
+        for g in GROUP_ORDER:
+            if g > 0:
+                for pr in range(PROJ):
+                    nc.gpsimd.dma_start(out=par_in[0:D, g, pr, 0, 0:TAPS[g]], in_=conv_w[pr][g - 1])
+                    nc.gpsimd.dma_start(out=par_in[0:D, g, pr, 1, 0:1], in_=conv_b[pr][g - 1].rearrange("(d o) -> d o", o=1))
+
+        w_codes = keep.tile([P, PROJ * GROUPS, PASSES, GROUP_COLS], U32, align_bytes=64)
+        w_scales = keep.tile([P, PROJ * GROUPS, PASSES, GROUP_COLS], U8, align_bytes=64)
+
+        def regroup(n, copy):
+            pr, g = group_seq[n]
+            wg = wg_pool.tile([P, PASSES, GROUP_COLS, PACK], BF16, name="wg", align_bytes=64)
+            for c in range(PASSES):
+                copy(
+                    out=wg[:, c].rearrange("p (n i) j -> p n j i", i=4),
+                    in_=w_raw[pr][:, c, :, g * GROUP_COLS:(g + 1) * GROUP_COLS].rearrange("p j (n i) -> p n j i", i=4),
+                )
+            return wg
+
+        def quantise(n, wg):
+            pr, g = group_seq[n]
+            nc.vector.quantize_mx(
+                out=w_codes[:, pr * GROUPS + g].rearrange("p c n -> p (c n)").bitcast(FP8X4),
+                scales=w_scales[:, pr * GROUPS + g].rearrange("p c n -> p (c n)"),
+                in_=wg[:].rearrange("p c n j -> p (c n j)"),
+            )
+
+        attn_bias = keep.tile([P, 4, GROUPS, TILES], F32)
+        par = keep.tile([P, GROUPS, 4, 2, SLOT], F32)
+        total = keep.tile([P, GROUPS, 4], F32)
+        short = keep.tile([P, GROUPS, 4, EDGE], F32)
+        beta = keep.tile([P, GROUPS, 4, TILES], F32)
+        corr = keep.tile([P, GROUPS, 4, TILES, EDGE], F32)
+        nc.vector.memset(par[:, 0], 0.0)
+        nc.vector.memset(par[:, 0, :, 0, 0:1], 1.0)
+        nc.vector.memset(short[:], 0.0)
+
+        def spread_attn_bias():
+            bias_ps = psum.tile([P, P], F32, name="bias_ps", tag="y")
+            nc.tensor.matmul(out=bias_ps[:], lhsT=bias_rows[:], rhs=ident_bf[:], start=True, stop=True)
+            nc.vector.tensor_copy(out=attn_bias[:].rearrange("p r g f -> p (r g f)"), in_=bias_ps[:, 0:4 * GROUPS * TILES])
+
+        def prepare_parameters(g):
+            taps = TAPS[g]
+            if g > 0:
+                par_ps = psum.tile([P, 4 * 2 * SLOT], F32, name="par_ps", tag="y")
+                nc.tensor.matmul(
+                    out=par_ps[:], lhsT=twice[:].rearrange("p a d -> p (a d)"),
+                    rhs=par_in[:, g].rearrange("p r k i -> p (r k i)"), start=True, stop=True,
+                )
+                nc.vector.tensor_copy(out=par[:, g].rearrange("p r k i -> p (r k i)"), in_=par_ps[:])
+            nc.vector.tensor_reduce(out=total[:, g, :], in_=par[:, g, :, 0, :], axis=mybir.AxisListType.X, op=ADD)
+            for t in range(1, taps):
+                nc.vector.tensor_tensor(
+                    out=short[:, g, :, 0:t], in0=short[:, g, :, 0:t],
+                    in1=par[:, g, :, 0, taps - 1 - t:taps - t].to_broadcast([P, 4, t]), op=SUB,
+                )
+            nc.vector.tensor_tensor(
+                out=beta[:, g], in0=attn_bias[:, :, g, :],
+                in1=total[:, g, :].unsqueeze(2).to_broadcast([P, 4, TILES]), op=MULT,
+            )
+            nc.vector.tensor_tensor(
+                out=beta[:, g], in0=beta[:, g],
+                in1=par[:, g, :, 1, 0:1].to_broadcast([P, 4, TILES]), op=ADD,
+            )
+            nc.vector.tensor_tensor(
+                out=corr[:, g], in0=short[:, g].unsqueeze(2).to_broadcast([P, 4, TILES, EDGE]),
+                in1=attn_bias[:, :, g, :].unsqueeze(3).to_broadcast([P, 4, TILES, EDGE]), op=MULT,
+            )
+
+        x_words = x_raw[:].bitcast(F32)
+        x_grouped = keep.tile([P, PASSES, B * S, PACK], BF16, align_bytes=64)
+        x_grouped_words = x_grouped[:].bitcast(F32)
+        x_codes = keep.tile([P, PASSES, B * S], U32, align_bytes=64)
+        x_scales = keep.tile([P, PASSES, B * S], U8, align_bytes=64)
+        words = K_PASS // 2
+
+        def transpose_x(b):
+            for t in range(TOKEN_TILES):
+                tt = b * TOKEN_TILES + t
+                xt = psum.tile([P, PASSES, 2, P], F32, name="xt", tag="y")
+                for c in range(PASSES):
+                    for u in range(2):
+                        nc.tensor.transpose(xt[:, c, u, :], x_words[:, tt, c * words + u:(c + 1) * words:2], ident_f32[:])
+                copy = nc.scalar.copy if t % 2 == 0 else nc.vector.tensor_copy
+                copy(out=x_grouped_words[:, :, tt * P:(tt + 1) * P, :], in_=xt[:].rearrange("p c u t -> p c t u"))
+
+        def quantise_x(b):
+            for c in range(PASSES):
+                nc.vector.quantize_mx(
+                    out=x_codes[:, c, b * S:(b + 1) * S].bitcast(FP8X4),
+                    scales=x_scales[:, c, b * S:(b + 1) * S],
+                    in_=x_grouped[:, c, b * S:(b + 1) * S, :].rearrange("p t j -> p (t j)"),
+                )
+
+        x_ps = {}
+        acc = {}
+
+        def project(i):
+            pr, g, f = steps[i]
+            taps = TAPS[g]
+            pg = pr * GROUPS + g
+            cols = slice(f * P, (f + 1) * P)
+            acc[i] = acc_pool.tile([P, B, S], F32, name="acc")
+            for b in range(B):
+                if taps > 3:
+                    x_b = psum.tile([P, S], F32, name="x_b", tag="x_many", bufs=4)
+                else:
+                    x_b = psum.tile([P, S], F32, name="x_b", tag="x_few", bufs=2)
+                x_ps[(i, b)] = x_b
+                for c in range(PASSES):
+                    nc.tensor.matmul_mx(
+                        out=x_b[:],
+                        lhsT=w_codes[:, pg, c, cols].bitcast(FP8X4), lhsT_scale=w_scales[:, pg, c, cols],
+                        rhs=x_codes[:, c, b * S:(b + 1) * S].bitcast(FP8X4), rhs_scale=x_scales[:, c, b * S:(b + 1) * S],
+                        start=(c == 0), stop=(c == PASSES - 1),
+                    )
+            for b in range(B):
+                nc.scalar.activation(
+                    out=acc[i][:, b, :], in_=x_ps[(i, b)][:], func=IDENTITY,
+                    scale=par[:, g, pr, 0, taps - 1:taps], bias=beta[:, g, pr, f:f + 1],
+                )
+
+        def convolve(i):
+            pr, g, f = steps[i]
+            taps = TAPS[g]
+            if taps > 1:
+                nc.vector.tensor_tensor(
+                    out=acc[i][:, :, 0:EDGE], in0=acc[i][:, :, 0:EDGE],
+                    in1=corr[:, g, pr, f, :].unsqueeze(1).to_broadcast([P, B, EDGE]), op=ADD,
+                )
+            for t in range(1, taps):
+                for b in range(B):
+                    nc.vector.scalar_tensor_tensor(
+                        out=acc[i][:, b, t:], in0=x_ps[(i, b)][:, 0:S - t], scalar=par[:, g, pr, 0, taps - 1 - t:taps - t],
+                        in1=acc[i][:, b, t:], op0=MULT, op1=ADD,
+                    )
+
+        def transpose_and_store(i):
+            pr, g, f = steps[i]
+            o_sb = out_pool.tile([P, B, TOKEN_TILES, P], F32, name="o_sb")
+            for b in range(B):
+                y_ps = psum.tile([P, TOKEN_TILES, P], F32, name="y_ps", tag="y")
+                for t in range(TOKEN_TILES):
+                    nc.tensor.transpose(y_ps[:, t, :], acc[i][:, b, t * P:(t + 1) * P], ident_f32[:])
+                nc.scalar.copy(out=o_sb[:, b], in_=y_ps[:])
+                for h in range(P // D):
+                    head = (g * TILES + f) * (P // D) + h
+                    nc.sync.dma_start(
+                        out=outs[pr][b, head].rearrange("(t p) d -> p t d", p=P),
+                        in_=o_sb[:, b, :, h * D:(h + 1) * D],
+                    )
+
+        spread_attn_bias()
+        wg = {}
+        wg[0] = regroup(0, nc.vector.tensor_copy)
+        transpose_x(0)
+        quantise(0, wg[0])
+        quantise_x(0)
+        transpose_x(1)
+        quantise_x(1)
+        prepare_parameters(GROUP_ORDER[0])
+        wg[1] = regroup(1, nc.vector.tensor_copy)
+        prepare_parameters(GROUP_ORDER[1])
+        quantise(1, wg[1])
+
+        for i in range(-AHEAD, len(steps) + 1):
+            if 0 <= i < len(steps):
+                convolve(i)
+            if i % 2 == 0 and 2 <= (i + 4) // 2 < len(group_seq):
+                quantise((i + 4) // 2, wg[(i + 4) // 2])
+            if 0 <= i - 1:
+                transpose_and_store(i - 1)
+            if i + AHEAD < len(steps):
+                project(i + AHEAD)
+            if i % 2 != 0 and 2 <= (i + 5) // 2 < len(group_seq):
+                wg[(i + 5) // 2] = regroup((i + 5) // 2, nc.scalar.copy)
+            if i in (0, 2):
+                prepare_parameters(GROUP_ORDER[2 + i // 2])

@@ -10,6 +10,7 @@ ADD = mybir.AluOpType.add
 SUB = mybir.AluOpType.subtract
 MULT = mybir.AluOpType.mult
 IDENTITY = mybir.ActivationFunctionType.Identity
+COPY = mybir.ActivationFunctionType.Copy
 
 P = 128
 PACK = 4
@@ -26,6 +27,9 @@ EDGE = 8
 SLOT = 16
 GROUP_ORDER = (3, 0, 2, 1)
 AHEAD = 2
+SCALAR_TAPS = (1, 1, 2, 3)
+HALO = 8
+SIDE_SLOTS = 6
 
 FLOPS = 2 * B * S * E * PROJ * E + 2 * B * S * PROJ * GROUP_COLS * sum(TAPS[1:])
 
@@ -116,6 +120,9 @@ def tile_tranceptionblockattention_pa_kernel(
                 )
             return wg
 
+        def gpsimd_copy(out, in_):
+            nc.gpsimd.tensor_scalar(out=out, in0=in_, scalar1=1.0, scalar2=0.0, op0=MULT, op1=ADD)
+
         def quantise(n, wg):
             pr, g = group_seq[n]
             nc.vector.quantize_mx(
@@ -194,6 +201,9 @@ def tile_tranceptionblockattention_pa_kernel(
 
         x_ps = {}
         acc = {}
+        side = keep.tile([P, SIDE_SLOTS, B, HALO + S], F32)
+        nc.vector.memset(side[:, :, :, 0:HALO], 0.0)
+        side_slot = {}
 
         def project(i):
             pr, g, f = steps[i]
@@ -214,6 +224,13 @@ def tile_tranceptionblockattention_pa_kernel(
                         rhs=x_codes[:, c, b * S:(b + 1) * S].bitcast(FP8X4), rhs_scale=x_scales[:, c, b * S:(b + 1) * S],
                         start=(c == 0), stop=(c == PASSES - 1),
                     )
+            for t in range(taps - SCALAR_TAPS[g] + 1, taps):
+                side_slot[(i, t)] = len(side_slot) % SIDE_SLOTS
+                for b in range(B):
+                    nc.scalar.activation(
+                        out=side[:, side_slot[(i, t)], b, HALO:], in_=x_ps[(i, b)][:], func=COPY,
+                        scale=par[:, g, pr, 0, taps - 1 - t:taps - t],
+                    )
             for b in range(B):
                 nc.scalar.activation(
                     out=acc[i][:, b, :], in_=x_ps[(i, b)][:], func=IDENTITY,
@@ -228,7 +245,7 @@ def tile_tranceptionblockattention_pa_kernel(
                     out=acc[i][:, :, 0:EDGE], in0=acc[i][:, :, 0:EDGE],
                     in1=corr[:, g, pr, f, :].unsqueeze(1).to_broadcast([P, B, EDGE]), op=ADD,
                 )
-            for t in range(1, taps):
+            for t in range(1, taps - SCALAR_TAPS[g] + 1):
                 for b in range(B):
                     nc.vector.scalar_tensor_tensor(
                         out=acc[i][:, b, t:], in0=x_ps[(i, b)][:, 0:S - t], scalar=par[:, g, pr, 0, taps - 1 - t:taps - t],
@@ -240,8 +257,15 @@ def tile_tranceptionblockattention_pa_kernel(
             o_sb = out_pool.tile([P, B, TOKEN_TILES, P], F32, name="o_sb")
             for b in range(B):
                 y_ps = psum.tile([P, TOKEN_TILES, P], F32, name="y_ps", tag="y")
-                for t in range(TOKEN_TILES):
-                    nc.tensor.transpose(y_ps[:, t, :], acc[i][:, b, t * P:(t + 1) * P], ident_f32[:])
+                for tt in range(TOKEN_TILES):
+                    parts = [acc[i][:, b, tt * P:(tt + 1) * P]]
+                    for t in range(TAPS[g] - SCALAR_TAPS[g] + 1, TAPS[g]):
+                        parts.append(side[:, side_slot[(i, t)], b, HALO + tt * P - t:HALO + (tt + 1) * P - t])
+                    for k in range(len(parts)):
+                        nc.tensor.matmul(
+                            out=y_ps[:, tt, :], lhsT=parts[k], rhs=ident_f32[:], is_transpose=True,
+                            start=(k == 0), stop=(k == len(parts) - 1),
+                        )
                 nc.scalar.copy(out=o_sb[:, b], in_=y_ps[:])
                 for h in range(P // D):
                     head = (g * TILES + f) * (P // D) + h
@@ -273,6 +297,7 @@ def tile_tranceptionblockattention_pa_kernel(
             if i + AHEAD < len(steps):
                 project(i + AHEAD)
             if i % 2 != 0 and 2 <= (i + 5) // 2 < len(group_seq):
-                wg[(i + 5) // 2] = regroup((i + 5) // 2, nc.scalar.copy)
+                n = (i + 5) // 2
+                wg[n] = regroup(n, gpsimd_copy if n >= GROUPS else nc.scalar.copy)
             if i in (0, 2):
                 prepare_parameters(GROUP_ORDER[2 + i // 2])

@@ -114,10 +114,16 @@ def tile_tranceptionblockattention_pa_kernel(
             pr, g = group_seq[n]
             wg = wg_pool.tile([P, PASSES, GROUP_COLS, PACK], BF16, name="wg", align_bytes=64)
             for c in range(PASSES):
-                copy(
-                    out=wg[:, c].rearrange("p (n i) j -> p n j i", i=4),
-                    in_=w_raw[pr][:, c, :, g * GROUP_COLS:(g + 1) * GROUP_COLS].rearrange("p j (n i) -> p n j i", i=4),
-                )
+                if copy == gpsimd_copy:
+                    copy(
+                        out=wg[:, c],
+                        in_=w_raw[pr][:, c, :, g * GROUP_COLS:(g + 1) * GROUP_COLS].rearrange("p j n -> p n j"),
+                    )
+                else:
+                    copy(
+                        out=wg[:, c].rearrange("p (n i) j -> p n j i", i=4),
+                        in_=w_raw[pr][:, c, :, g * GROUP_COLS:(g + 1) * GROUP_COLS].rearrange("p j (n i) -> p n j i", i=4),
+                    )
             return wg
 
         def gpsimd_copy(out, in_):

@@ -20,16 +20,21 @@ PASSES = E // K_PASS
 PROJ = 3
 GROUPS = 4
 TAPS = (1, 3, 5, 7)
+MAX_TAPS = 7
+CONV_GROUPS = GROUPS - 1
 GROUP_COLS = E // GROUPS
 TILES = GROUP_COLS // P
 TOKEN_TILES = S // P
 EDGE = 8
 SLOT = 16
-GROUP_ORDER = (3, 0, 2, 1)
-AHEAD = 2
-SCALAR_TAPS = (1, 1, 2, 3)
 HALO = 8
-SIDE_SLOTS = 6
+CONV_ORDER = (3, 2, 1)
+SCALAR_SIDES = (0, 1, 1, 2)
+PE_LEAD = 3
+ACT_LEAD = 2
+X_BANKS = PE_LEAD + 1
+SIDE_SLOTS = 10
+WG_BUFS = 4
 
 FLOPS = 2 * B * S * E * PROJ * E + 2 * B * S * PROJ * GROUP_COLS * sum(TAPS[1:])
 
@@ -46,26 +51,42 @@ def tile_tranceptionblockattention_pa_kernel(
     conv_b = ((qb3, qb5, qb7), (kb3, kb5, kb7), (vb3, vb5, vb7))
     outs = (out_0, out_1, out_2)
 
-    group_seq = []
-    steps = []
+    units = []
     for pr in range(PROJ):
-        for g in GROUP_ORDER:
+        for g in CONV_ORDER:
+            for b in range(B):
+                for f in range(TILES):
+                    units.append((pr, g, f, b))
+    plain_units = []
+    for pr in range(PROJ):
+        for b in range(B):
+            for half in range(2):
+                plain_units.append((pr, b, half))
+    plain_at = {}
+    for n in range(len(units)):
+        if units[n][1] == 1:
+            plain_at[n] = len(plain_at)
+    group_seq = []
+    for pr in range(PROJ):
+        for g in CONV_ORDER + (0,):
             group_seq.append((pr, g))
-        for pair in range(GROUPS // 2):
-            for f in range(TILES):
-                for g in GROUP_ORDER[2 * pair:2 * pair + 2]:
-                    steps.append((pr, g, f))
+    quantise_at = {}
+    for j in range(1, len(group_seq)):
+        pr, g = group_seq[j]
+        first = units.index((pr, max(g, 1), 0, 0))
+        use = first - PE_LEAD if g > 0 else first
+        quantise_at.setdefault(max(use - 2, 0), []).append(j)
 
     with tc.tile_pool(name="keep", bufs=1) as keep, \
-            tc.tile_pool(name="wg_pool", bufs=3) as wg_pool, \
-            tc.tile_pool(name="acc_pool", bufs=AHEAD + 2) as acc_pool, \
+            tc.tile_pool(name="wg_pool", bufs=WG_BUFS) as wg_pool, \
+            tc.tile_pool(name="acc_pool", bufs=6) as acc_pool, \
             tc.tile_pool(name="out_pool", bufs=4) as out_pool, \
             tc.psum_pool(name="psum", bufs=2) as psum, \
             tc.manual_schedule():
 
         bias_rows = keep.tile([P, P], BF16)
         nc.vector.memset(bias_rows[:], 0.0)
-        par_in = keep.tile([P, GROUPS, 4, 2, SLOT], BF16)
+        par_in = keep.tile([P, PROJ * CONV_GROUPS, 2, SLOT], BF16)
         nc.vector.memset(par_in[:], 0.0)
         ident_f32 = keep.tile([P, P], F32)
         make_identity(nc, ident_f32[:])
@@ -74,7 +95,12 @@ def tile_tranceptionblockattention_pa_kernel(
         twice = keep.tile([P, 2, D], BF16)
         nc.vector.tensor_copy(out=twice[:], in_=ident_bf[:, 0:D].unsqueeze(1).to_broadcast([P, 2, D]))
 
-        nc.sync.dma_start(out=bias_rows[0:PROJ * E // P, :], in_=c_attn_b.rearrange("(n m) -> n m", m=P))
+        def block(pr, g):
+            return pr * CONV_GROUPS + g - 1
+
+        def load_parameters(pr, g):
+            nc.sync.dma_start(out=par_in[0:D, block(pr, g), 0, MAX_TAPS - TAPS[g]:MAX_TAPS], in_=conv_w[pr][g - 1])
+            nc.sync.dma_start(out=par_in[0:D, block(pr, g), 1, 0:1], in_=conv_b[pr][g - 1].rearrange("(d o) -> d o", o=1))
 
         w_raw = []
         for pr in range(PROJ):
@@ -90,95 +116,117 @@ def tile_tranceptionblockattention_pa_kernel(
                 )
 
         x_raw = keep.tile([P, B * TOKEN_TILES, E], BF16)
-        load_w(0, GROUP_ORDER[0] * GROUP_COLS, GROUP_COLS)
+        nc.sync.dma_start(out=bias_rows[0:PROJ * E // P, :], in_=c_attn_b.rearrange("(n m) -> n m", m=P))
+        load_parameters(0, CONV_ORDER[0])
+        load_w(0, CONV_ORDER[0] * GROUP_COLS, GROUP_COLS)
         for b in range(B):
-            nc.sync.dma_start(
-                out=x_raw[:, b * TOKEN_TILES:(b + 1) * TOKEN_TILES, :],
-                in_=hidden_states[b].rearrange("(t p) k -> p t k", p=P),
-            )
-        for g in GROUP_ORDER[1:]:
+            for t in range(TOKEN_TILES):
+                nc.sync.dma_start(out=x_raw[:, b * TOKEN_TILES + t, :], in_=hidden_states[b, t * P:(t + 1) * P, :])
+        for g in CONV_ORDER[1:]:
+            load_parameters(0, g)
+        for g in CONV_ORDER[1:] + (0,):
             load_w(0, g * GROUP_COLS, GROUP_COLS)
+        load_w(1, 0, E)
         for pr in range(1, PROJ):
-            load_w(pr, 0, E)
-
-        for g in GROUP_ORDER:
-            if g > 0:
-                for pr in range(PROJ):
-                    nc.gpsimd.dma_start(out=par_in[0:D, g, pr, 0, 0:TAPS[g]], in_=conv_w[pr][g - 1])
-                    nc.gpsimd.dma_start(out=par_in[0:D, g, pr, 1, 0:1], in_=conv_b[pr][g - 1].rearrange("(d o) -> d o", o=1))
+            for g in CONV_ORDER:
+                load_parameters(pr, g)
+        load_w(2, 0, E)
 
         w_codes = keep.tile([P, PROJ * GROUPS, PASSES, GROUP_COLS], U32, align_bytes=64)
         w_scales = keep.tile([P, PROJ * GROUPS, PASSES, GROUP_COLS], U8, align_bytes=64)
+        wg = {}
 
-        def regroup(n, copy):
-            pr, g = group_seq[n]
-            wg = wg_pool.tile([P, PASSES, GROUP_COLS, PACK], BF16, name="wg", align_bytes=64)
+        def regroup_on_vector(j):
+            pr, g = group_seq[j]
+            wg[j] = wg_pool.tile([P, PASSES, GROUP_COLS, PACK], BF16, name="wg", align_bytes=64)
             for c in range(PASSES):
-                if copy == gpsimd_copy:
-                    copy(
-                        out=wg[:, c],
-                        in_=w_raw[pr][:, c, :, g * GROUP_COLS:(g + 1) * GROUP_COLS].rearrange("p j n -> p n j"),
-                    )
-                else:
-                    copy(
-                        out=wg[:, c].rearrange("p (n i) j -> p n j i", i=4),
-                        in_=w_raw[pr][:, c, :, g * GROUP_COLS:(g + 1) * GROUP_COLS].rearrange("p j (n i) -> p n j i", i=4),
-                    )
-            return wg
+                nc.vector.tensor_copy(
+                    out=wg[j][:, c].rearrange("p (n i) j -> p n j i", i=4),
+                    in_=w_raw[pr][:, c, :, g * GROUP_COLS:(g + 1) * GROUP_COLS].rearrange("p j (n i) -> p n j i", i=4),
+                )
 
-        def gpsimd_copy(out, in_):
-            nc.gpsimd.tensor_scalar(out=out, in0=in_, scalar1=1.0, scalar2=0.0, op0=MULT, op1=ADD)
+        def regroup_on_gpsimd(j):
+            pr, g = group_seq[j]
+            wg[j] = wg_pool.tile([P, PASSES, GROUP_COLS, PACK], BF16, name="wg", align_bytes=64)
+            for c in range(PASSES):
+                nc.gpsimd.tensor_scalar(
+                    out=wg[j][:, c],
+                    in0=w_raw[pr][:, c, :, g * GROUP_COLS:(g + 1) * GROUP_COLS].rearrange("p j n -> p n j"),
+                    scalar1=1.0, scalar2=0.0, op0=MULT, op1=ADD,
+                )
 
-        def quantise(n, wg):
-            pr, g = group_seq[n]
+        def quantise(j):
+            pr, g = group_seq[j]
             nc.vector.quantize_mx(
                 out=w_codes[:, pr * GROUPS + g].rearrange("p c n -> p (c n)").bitcast(FP8X4),
                 scales=w_scales[:, pr * GROUPS + g].rearrange("p c n -> p (c n)"),
-                in_=wg[:].rearrange("p c n j -> p (c n j)"),
+                in_=wg[j][:].rearrange("p c n j -> p (c n j)"),
             )
 
         attn_bias = keep.tile([P, 4, GROUPS, TILES], F32)
-        par = keep.tile([P, GROUPS, 4, 2, SLOT], F32)
-        total = keep.tile([P, GROUPS, 4], F32)
-        short = keep.tile([P, GROUPS, 4, EDGE], F32)
-        beta = keep.tile([P, GROUPS, 4, TILES], F32)
-        corr = keep.tile([P, GROUPS, 4, TILES, EDGE], F32)
-        nc.vector.memset(par[:, 0], 0.0)
-        nc.vector.memset(par[:, 0, :, 0, 0:1], 1.0)
+        plain_bias = keep.tile([P, PROJ * TILES, P], F32)
+        par = keep.tile([P, PROJ * CONV_GROUPS, 2, SLOT], F32)
+        total = keep.tile([P, PROJ * CONV_GROUPS], F32)
+        short = keep.tile([P, PROJ * CONV_GROUPS, EDGE], F32)
+        beta = keep.tile([P, PROJ * CONV_GROUPS, TILES], F32)
+        corr = keep.tile([P, PROJ * CONV_GROUPS, TILES, P], F32)
+        side = keep.tile([P, SIDE_SLOTS, HALO + S], F32)
         nc.vector.memset(short[:], 0.0)
+        nc.vector.memset(corr[:], 0.0)
+        nc.vector.memset(side[:, :, 0:HALO], 0.0)
 
         def spread_attn_bias():
             bias_ps = psum.tile([P, P], F32, name="bias_ps", tag="y")
             nc.tensor.matmul(out=bias_ps[:], lhsT=bias_rows[:], rhs=ident_bf[:], start=True, stop=True)
-            nc.vector.tensor_copy(out=attn_bias[:].rearrange("p r g f -> p (r g f)"), in_=bias_ps[:, 0:4 * GROUPS * TILES])
+            nc.scalar.copy(out=attn_bias[:].rearrange("p r g f -> p (r g f)"), in_=bias_ps[:, 0:4 * GROUPS * TILES])
+            for first in range(0, PROJ * TILES, 4):
+                n_rows = min(4, PROJ * TILES - first)
+                rows_ps = psum.tile([P, 4, P], F32, name="rows_ps", tag="y")
+                for i in range(n_rows):
+                    r = ((first + i) // TILES) * GROUPS * TILES + (first + i) % TILES
+                    nc.tensor.matmul(
+                        out=rows_ps[:, i, :], lhsT=ident_bf[:, r:r + 1].to_broadcast([P, P]), rhs=bias_rows[:],
+                        start=True, stop=True,
+                    )
+                nc.scalar.copy(out=plain_bias[:, first:first + n_rows, :], in_=rows_ps[:, 0:n_rows, :])
 
-        def prepare_parameters(g):
-            taps = TAPS[g]
-            if g > 0:
-                par_ps = psum.tile([P, 4 * 2 * SLOT], F32, name="par_ps", tag="y")
-                nc.tensor.matmul(
-                    out=par_ps[:], lhsT=twice[:].rearrange("p a d -> p (a d)"),
-                    rhs=par_in[:, g].rearrange("p r k i -> p (r k i)"), start=True, stop=True,
-                )
-                nc.vector.tensor_copy(out=par[:, g].rearrange("p r k i -> p (r k i)"), in_=par_ps[:])
-            nc.vector.tensor_reduce(out=total[:, g, :], in_=par[:, g, :, 0, :], axis=mybir.AxisListType.X, op=ADD)
-            for t in range(1, taps):
+        def spread_parameters(pr, g_lo, g_hi):
+            blocks = slice(block(pr, g_lo), block(pr, g_hi))
+            n_g = g_hi - g_lo
+            par_ps = psum.tile([P, CONV_GROUPS * 2 * SLOT], F32, name="par_ps", tag="y")
+            nc.tensor.matmul(
+                out=par_ps[:, 0:n_g * 2 * SLOT], lhsT=twice[:].rearrange("p a d -> p (a d)"),
+                rhs=par_in[:, blocks].rearrange("p n k i -> p (n k i)"), start=True, stop=True,
+            )
+            nc.scalar.copy(out=par[:, blocks].rearrange("p n k i -> p (n k i)"), in_=par_ps[:, 0:n_g * 2 * SLOT])
+
+        def derive_parameters(pr, g_lo, g_hi):
+            blocks = slice(block(pr, g_lo), block(pr, g_hi))
+            n_g = g_hi - g_lo
+            last = MAX_TAPS - 1
+            for t in range(1, TAPS[g_hi - 1]):
                 nc.vector.tensor_tensor(
-                    out=short[:, g, :, 0:t], in0=short[:, g, :, 0:t],
-                    in1=par[:, g, :, 0, taps - 1 - t:taps - t].to_broadcast([P, 4, t]), op=SUB,
+                    out=short[:, blocks, 0:t], in0=short[:, blocks, 0:t],
+                    in1=par[:, blocks, 0, last - t:last - t + 1].to_broadcast([P, n_g, t]), op=SUB,
                 )
             nc.vector.tensor_tensor(
-                out=beta[:, g], in0=attn_bias[:, :, g, :],
-                in1=total[:, g, :].unsqueeze(2).to_broadcast([P, 4, TILES]), op=MULT,
+                out=total[:, blocks].unsqueeze(2), in0=par[:, blocks, 0, last:last + 1], in1=short[:, blocks, 0:1], op=SUB,
             )
             nc.vector.tensor_tensor(
-                out=beta[:, g], in0=beta[:, g],
-                in1=par[:, g, :, 1, 0:1].to_broadcast([P, 4, TILES]), op=ADD,
+                out=beta[:, blocks], in0=attn_bias[:, pr, g_lo:g_hi, :],
+                in1=total[:, blocks].unsqueeze(2).to_broadcast([P, n_g, TILES]), op=MULT,
             )
             nc.vector.tensor_tensor(
-                out=corr[:, g], in0=short[:, g].unsqueeze(2).to_broadcast([P, 4, TILES, EDGE]),
-                in1=attn_bias[:, :, g, :].unsqueeze(3).to_broadcast([P, 4, TILES, EDGE]), op=MULT,
+                out=beta[:, blocks], in0=beta[:, blocks],
+                in1=par[:, blocks, 1, 0:1].to_broadcast([P, n_g, TILES]), op=ADD,
             )
+            nc.vector.tensor_tensor(
+                out=corr[:, blocks, :, 0:EDGE], in0=short[:, blocks].unsqueeze(2).to_broadcast([P, n_g, TILES, EDGE]),
+                in1=attn_bias[:, pr, g_lo:g_hi, :].unsqueeze(3).to_broadcast([P, n_g, TILES, EDGE]), op=MULT,
+            )
+
+        def weight(pr, g, t):
+            return par[:, block(pr, g), 0, MAX_TAPS - 1 - t:MAX_TAPS - t]
 
         x_words = x_raw[:].bitcast(F32)
         x_grouped = keep.tile([P, PASSES, B * S, PACK], BF16, align_bytes=64)
@@ -187,15 +235,13 @@ def tile_tranceptionblockattention_pa_kernel(
         x_scales = keep.tile([P, PASSES, B * S], U8, align_bytes=64)
         words = K_PASS // 2
 
-        def transpose_x(b):
-            for t in range(TOKEN_TILES):
-                tt = b * TOKEN_TILES + t
-                xt = psum.tile([P, PASSES, 2, P], F32, name="xt", tag="y")
-                for c in range(PASSES):
-                    for u in range(2):
-                        nc.tensor.transpose(xt[:, c, u, :], x_words[:, tt, c * words + u:(c + 1) * words:2], ident_f32[:])
-                copy = nc.scalar.copy if t % 2 == 0 else nc.vector.tensor_copy
-                copy(out=x_grouped_words[:, :, tt * P:(tt + 1) * P, :], in_=xt[:].rearrange("p c u t -> p c t u"))
+        def transpose_x(tt):
+            xt = psum.tile([P, PASSES, 2, P], F32, name="xt", tag="x", bufs=X_BANKS)
+            for c in range(PASSES):
+                for u in range(2):
+                    nc.tensor.transpose(xt[:, c, u, :], x_words[:, tt, c * words + u:(c + 1) * words:2], ident_f32[:])
+            copy = nc.scalar.copy if tt % 2 == 0 else nc.vector.tensor_copy
+            copy(out=x_grouped_words[:, :, tt * P:(tt + 1) * P, :], in_=xt[:].rearrange("p c u t -> p c t u"))
 
         def quantise_x(b):
             for c in range(PASSES):
@@ -207,103 +253,141 @@ def tile_tranceptionblockattention_pa_kernel(
 
         x_ps = {}
         acc = {}
-        side = keep.tile([P, SIDE_SLOTS, B, HALO + S], F32)
-        nc.vector.memset(side[:, :, :, 0:HALO], 0.0)
+        y_ps = {}
         side_slot = {}
 
-        def project(i):
-            pr, g, f = steps[i]
-            taps = TAPS[g]
+        def side_taps(g):
+            return range(TAPS[g] - SCALAR_SIDES[g], TAPS[g])
+
+        def project(n):
+            pr, g, f, b = units[n]
             pg = pr * GROUPS + g
             cols = slice(f * P, (f + 1) * P)
-            acc[i] = acc_pool.tile([P, B, S], F32, name="acc")
-            for b in range(B):
-                if taps > 3:
-                    x_b = psum.tile([P, S], F32, name="x_b", tag="x_many", bufs=4)
-                else:
-                    x_b = psum.tile([P, S], F32, name="x_b", tag="x_few", bufs=2)
-                x_ps[(i, b)] = x_b
+            x_ps[n] = psum.tile([P, S], F32, name="x_b", tag="x", bufs=X_BANKS)
+            for c in range(PASSES):
+                nc.tensor.matmul_mx(
+                    out=x_ps[n][:],
+                    lhsT=w_codes[:, pg, c, cols].bitcast(FP8X4), lhsT_scale=w_scales[:, pg, c, cols],
+                    rhs=x_codes[:, c, b * S:(b + 1) * S].bitcast(FP8X4), rhs_scale=x_scales[:, c, b * S:(b + 1) * S],
+                    start=(c == 0), stop=(c == PASSES - 1),
+                )
+
+        def scalar_taps(n):
+            pr, g, f, b = units[n]
+            acc[n] = acc_pool.tile([P, S], F32, name="acc")
+            nc.scalar.activation(
+                out=acc[n][:], in_=x_ps[n][:], func=IDENTITY,
+                scale=weight(pr, g, 0), bias=beta[:, block(pr, g), f:f + 1],
+            )
+            for t in side_taps(g):
+                side_slot[(n, t)] = len(side_slot) % SIDE_SLOTS
+                nc.scalar.activation(out=side[:, side_slot[(n, t)], HALO:], in_=x_ps[n][:], func=COPY, scale=weight(pr, g, t))
+
+        def convolve(n):
+            pr, g, f, b = units[n]
+            for t in range(1, TAPS[g] - SCALAR_SIDES[g]):
+                nc.vector.scalar_tensor_tensor(
+                    out=acc[n][:, t:], in0=x_ps[n][:, 0:S - t], scalar=weight(pr, g, t),
+                    in1=acc[n][:, t:], op0=MULT, op1=ADD,
+                )
+
+        def transposes(n):
+            pr, g, f, b = units[n]
+            y_ps[n] = psum.tile([P, TOKEN_TILES, P], F32, name="y_b", tag="y")
+            for tt in range(TOKEN_TILES):
+                parts = [acc[n][:, tt * P:(tt + 1) * P]]
+                for t in side_taps(g):
+                    parts.append(side[:, side_slot[(n, t)], HALO + tt * P - t:HALO + (tt + 1) * P - t])
+                if tt == 0:
+                    parts.append(corr[:, block(pr, g), f, :])
+                for k in range(len(parts)):
+                    nc.tensor.matmul(
+                        out=y_ps[n][:, tt, :], lhsT=parts[k], rhs=ident_f32[:], is_transpose=True,
+                        start=(k == 0), stop=(k == len(parts) - 1),
+                    )
+
+        def evacuate(n):
+            pr, g, f, b = units[n]
+            o_sb = out_pool.tile([P, TOKEN_TILES, P], F32, name="o_sb")
+            nc.scalar.copy(out=o_sb[:], in_=y_ps[n][:])
+            for h in range(P // D):
+                head = (g * TILES + f) * (P // D) + h
+                nc.sync.dma_start(
+                    out=outs[pr][b, head].rearrange("(t p) d -> p t d", p=P),
+                    in_=o_sb[:, :, h * D:(h + 1) * D],
+                )
+
+        z_ps = {}
+
+        def project_plain(k):
+            pr, b, half = plain_units[k]
+            pg = pr * GROUPS
+            z_ps[k] = psum.tile([P, 2, GROUP_COLS], F32, name="z_b", tag="z")
+            for i in range(2):
+                tokens = slice(b * S + (2 * half + i) * P, b * S + (2 * half + i + 1) * P)
                 for c in range(PASSES):
                     nc.tensor.matmul_mx(
-                        out=x_b[:],
-                        lhsT=w_codes[:, pg, c, cols].bitcast(FP8X4), lhsT_scale=w_scales[:, pg, c, cols],
-                        rhs=x_codes[:, c, b * S:(b + 1) * S].bitcast(FP8X4), rhs_scale=x_scales[:, c, b * S:(b + 1) * S],
+                        out=z_ps[k][:, i, :],
+                        lhsT=x_codes[:, c, tokens].bitcast(FP8X4), lhsT_scale=x_scales[:, c, tokens],
+                        rhs=w_codes[:, pg, c, :].bitcast(FP8X4), rhs_scale=w_scales[:, pg, c, :],
                         start=(c == 0), stop=(c == PASSES - 1),
                     )
-            for t in range(taps - SCALAR_TAPS[g] + 1, taps):
-                side_slot[(i, t)] = len(side_slot) % SIDE_SLOTS
-                for b in range(B):
-                    nc.scalar.activation(
-                        out=side[:, side_slot[(i, t)], b, HALO:], in_=x_ps[(i, b)][:], func=COPY,
-                        scale=par[:, g, pr, 0, taps - 1 - t:taps - t],
-                    )
-            for b in range(B):
-                nc.scalar.activation(
-                    out=acc[i][:, b, :], in_=x_ps[(i, b)][:], func=IDENTITY,
-                    scale=par[:, g, pr, 0, taps - 1:taps], bias=beta[:, g, pr, f:f + 1],
-                )
 
-        def convolve(i):
-            pr, g, f = steps[i]
-            taps = TAPS[g]
-            if taps > 1:
-                nc.vector.tensor_tensor(
-                    out=acc[i][:, :, 0:EDGE], in0=acc[i][:, :, 0:EDGE],
-                    in1=corr[:, g, pr, f, :].unsqueeze(1).to_broadcast([P, B, EDGE]), op=ADD,
+        def finish_plain(k):
+            pr, b, half = plain_units[k]
+            o_plain = out_pool.tile([P, 2, GROUP_COLS], F32, name="o_plain")
+            nc.vector.tensor_tensor(
+                out=o_plain[:], in0=z_ps[k][:],
+                in1=plain_bias[:, pr * TILES:(pr + 1) * TILES, :].rearrange("p a m -> p (a m)")
+                .unsqueeze(1).to_broadcast([P, 2, GROUP_COLS]),
+                op=ADD,
+            )
+            for i in range(2):
+                first = (2 * half + i) * P
+                nc.sync.dma_start(
+                    out=outs[pr][b, 0:GROUP_COLS // D, first:first + P, :].rearrange("h p d -> p h d"),
+                    in_=o_plain[:, i, :].rearrange("p (h d) -> p h d", d=D),
                 )
-            for t in range(1, taps - SCALAR_TAPS[g] + 1):
-                for b in range(B):
-                    nc.vector.scalar_tensor_tensor(
-                        out=acc[i][:, b, t:], in0=x_ps[(i, b)][:, 0:S - t], scalar=par[:, g, pr, 0, taps - 1 - t:taps - t],
-                        in1=acc[i][:, b, t:], op0=MULT, op1=ADD,
-                    )
-
-        def transpose_and_store(i):
-            pr, g, f = steps[i]
-            o_sb = out_pool.tile([P, B, TOKEN_TILES, P], F32, name="o_sb")
-            for b in range(B):
-                y_ps = psum.tile([P, TOKEN_TILES, P], F32, name="y_ps", tag="y")
-                for tt in range(TOKEN_TILES):
-                    parts = [acc[i][:, b, tt * P:(tt + 1) * P]]
-                    for t in range(TAPS[g] - SCALAR_TAPS[g] + 1, TAPS[g]):
-                        parts.append(side[:, side_slot[(i, t)], b, HALO + tt * P - t:HALO + (tt + 1) * P - t])
-                    for k in range(len(parts)):
-                        nc.tensor.matmul(
-                            out=y_ps[:, tt, :], lhsT=parts[k], rhs=ident_f32[:], is_transpose=True,
-                            start=(k == 0), stop=(k == len(parts) - 1),
-                        )
-                nc.scalar.copy(out=o_sb[:, b], in_=y_ps[:])
-                for h in range(P // D):
-                    head = (g * TILES + f) * (P // D) + h
-                    nc.sync.dma_start(
-                        out=outs[pr][b, head].rearrange("(t p) d -> p t d", p=P),
-                        in_=o_sb[:, b, :, h * D:(h + 1) * D],
-                    )
 
         spread_attn_bias()
-        wg = {}
-        wg[0] = regroup(0, nc.vector.tensor_copy)
+        spread_parameters(0, CONV_ORDER[0], CONV_ORDER[0] + 1)
+        derive_parameters(0, CONV_ORDER[0], CONV_ORDER[0] + 1)
+        regroup_on_vector(0)
+        for j in range(1, WG_BUFS):
+            regroup_on_gpsimd(j)
         transpose_x(0)
-        quantise(0, wg[0])
-        quantise_x(0)
         transpose_x(1)
+        quantise(0)
+        regroup_on_gpsimd(WG_BUFS)
+        transpose_x(2)
+        transpose_x(3)
+        quantise_x(0)
+        for tt in range(TOKEN_TILES, 2 * TOKEN_TILES):
+            transpose_x(tt)
         quantise_x(1)
-        prepare_parameters(GROUP_ORDER[0])
-        wg[1] = regroup(1, nc.vector.tensor_copy)
-        prepare_parameters(GROUP_ORDER[1])
-        quantise(1, wg[1])
 
-        for i in range(-AHEAD, len(steps) + 1):
-            if 0 <= i < len(steps):
-                convolve(i)
-            if i % 2 == 0 and 2 <= (i + 4) // 2 < len(group_seq):
-                quantise((i + 4) // 2, wg[(i + 4) // 2])
-            if 0 <= i - 1:
-                transpose_and_store(i - 1)
-            if i + AHEAD < len(steps):
-                project(i + AHEAD)
-            if i % 2 != 0 and 2 <= (i + 5) // 2 < len(group_seq):
-                n = (i + 5) // 2
-                wg[n] = regroup(n, gpsimd_copy if n >= GROUPS else nc.scalar.copy)
-            if i in (0, 2):
-                prepare_parameters(GROUP_ORDER[2 + i // 2])
+        for n in range(-PE_LEAD, len(units) + 1):
+            if 0 <= n - 1:
+                transposes(n - 1)
+            if n + PE_LEAD < len(units):
+                project(n + PE_LEAD)
+            if n in plain_at:
+                project_plain(plain_at[n])
+            if 0 <= n + ACT_LEAD < len(units):
+                scalar_taps(n + ACT_LEAD)
+            if 0 <= n - 1:
+                evacuate(n - 1)
+            if 0 <= n < len(units):
+                convolve(n)
+            if n - 1 in plain_at:
+                finish_plain(plain_at[n - 1])
+            for j in quantise_at.get(n, []):
+                quantise(j)
+                if j + WG_BUFS < len(group_seq):
+                    regroup_on_gpsimd(j + WG_BUFS)
+            if n == 0:
+                spread_parameters(0, 1, CONV_ORDER[0])
+                derive_parameters(0, 1, CONV_ORDER[0])
+            if n in plain_at and plain_at[n] % 4 == 0 and units[n][0] + 1 < PROJ:
+                spread_parameters(units[n][0] + 1, 1, GROUPS)
+                derive_parameters(units[n][0] + 1, 1, GROUPS)

@@ -30,11 +30,13 @@ SLOT = 16
 HALO = 8
 CONV_ORDER = (3, 2, 1)
 SCALAR_SIDES = (0, 1, 1, 2)
-PE_LEAD = 3
-ACT_LEAD = 2
-X_BANKS = PE_LEAD + 1
-SIDE_SLOTS = 10
+X_BANKS = 4
+ACT_LEAD = 3
+PLAIN_LEAD = 2
+SKEW = 2
+SIDE_SLOTS = 12
 WG_BUFS = 4
+PLAIN = 0
 
 FLOPS = 2 * B * S * E * PROJ * E + 2 * B * S * PROJ * GROUP_COLS * sum(TAPS[1:])
 
@@ -74,8 +76,22 @@ def tile_tranceptionblockattention_pa_kernel(
     for j in range(1, len(group_seq)):
         pr, g = group_seq[j]
         first = units.index((pr, max(g, 1), 0, 0))
-        use = first - PE_LEAD if g > 0 else first
+        use = first - X_BANKS if g > 0 else first - PLAIN_LEAD
         quantise_at.setdefault(max(use - 2, 0), []).append(j)
+    lanes = ([], [])
+    for n in range(len(units)):
+        for t in range(1, TAPS[units[n][1]] - SCALAR_SIDES[units[n][1]]):
+            lanes[n % 2].append((n, t))
+        if n in plain_at:
+            lanes[n % 2].append((n, PLAIN))
+    vector_order = lanes[0][0:SKEW]
+    for i in range(len(lanes[1])):
+        vector_order.append(lanes[1][i])
+        if SKEW + i < len(lanes[0]):
+            vector_order.append(lanes[0][SKEW + i])
+    left = {}
+    for n, t in vector_order:
+        left[n] = left.get(n, 0) + 1
 
     with tc.tile_pool(name="keep", bufs=1) as keep, \
             tc.tile_pool(name="wg_pool", bufs=WG_BUFS) as wg_pool, \
@@ -122,8 +138,9 @@ def tile_tranceptionblockattention_pa_kernel(
         for b in range(B):
             for t in range(TOKEN_TILES):
                 nc.sync.dma_start(out=x_raw[:, b * TOKEN_TILES + t, :], in_=hidden_states[b, t * P:(t + 1) * P, :])
-        for g in CONV_ORDER[1:]:
-            load_parameters(0, g)
+            if b == 0:
+                for g in CONV_ORDER[1:]:
+                    load_parameters(0, g)
         for g in CONV_ORDER[1:] + (0,):
             load_w(0, g * GROUP_COLS, GROUP_COLS)
         load_w(1, 0, E)
@@ -144,6 +161,7 @@ def tile_tranceptionblockattention_pa_kernel(
                     out=wg[j][:, c].rearrange("p (n i) j -> p n j i", i=4),
                     in_=w_raw[pr][:, c, :, g * GROUP_COLS:(g + 1) * GROUP_COLS].rearrange("p j (n i) -> p n j i", i=4),
                 )
+                fill()
 
         def regroup_on_gpsimd(j):
             pr, g = group_seq[j]
@@ -176,12 +194,12 @@ def tile_tranceptionblockattention_pa_kernel(
         nc.vector.memset(side[:, :, 0:HALO], 0.0)
 
         def spread_attn_bias():
-            bias_ps = psum.tile([P, P], F32, name="bias_ps", tag="y")
+            bias_ps = psum.tile([P, P], F32, name="bias_ps", tag="z")
             nc.tensor.matmul(out=bias_ps[:], lhsT=bias_rows[:], rhs=ident_bf[:], start=True, stop=True)
             nc.scalar.copy(out=attn_bias[:].rearrange("p r g f -> p (r g f)"), in_=bias_ps[:, 0:4 * GROUPS * TILES])
             for first in range(0, PROJ * TILES, 4):
                 n_rows = min(4, PROJ * TILES - first)
-                rows_ps = psum.tile([P, 4, P], F32, name="rows_ps", tag="y")
+                rows_ps = psum.tile([P, 4, P], F32, name="rows_ps", tag="z")
                 for i in range(n_rows):
                     r = ((first + i) // TILES) * GROUPS * TILES + (first + i) % TILES
                     nc.tensor.matmul(
@@ -193,37 +211,60 @@ def tile_tranceptionblockattention_pa_kernel(
         def spread_parameters(pr, g_lo, g_hi):
             blocks = slice(block(pr, g_lo), block(pr, g_hi))
             n_g = g_hi - g_lo
-            par_ps = psum.tile([P, CONV_GROUPS * 2 * SLOT], F32, name="par_ps", tag="y")
+            par_ps = psum.tile([P, CONV_GROUPS * 2 * SLOT], F32, name="par_ps", tag="z")
             nc.tensor.matmul(
                 out=par_ps[:, 0:n_g * 2 * SLOT], lhsT=twice[:].rearrange("p a d -> p (a d)"),
                 rhs=par_in[:, blocks].rearrange("p n k i -> p (n k i)"), start=True, stop=True,
             )
             nc.scalar.copy(out=par[:, blocks].rearrange("p n k i -> p (n k i)"), in_=par_ps[:, 0:n_g * 2 * SLOT])
 
-        def derive_parameters(pr, g_lo, g_hi):
+        def derive_step(pr, g_lo, g_hi, step):
             blocks = slice(block(pr, g_lo), block(pr, g_hi))
             n_g = g_hi - g_lo
             last = MAX_TAPS - 1
-            for t in range(1, TAPS[g_hi - 1]):
+            n_taps = TAPS[g_hi - 1]
+            if step < n_taps - 1:
+                t = step + 1
                 nc.vector.tensor_tensor(
                     out=short[:, blocks, 0:t], in0=short[:, blocks, 0:t],
                     in1=par[:, blocks, 0, last - t:last - t + 1].to_broadcast([P, n_g, t]), op=SUB,
                 )
-            nc.vector.tensor_tensor(
-                out=total[:, blocks].unsqueeze(2), in0=par[:, blocks, 0, last:last + 1], in1=short[:, blocks, 0:1], op=SUB,
-            )
-            nc.vector.tensor_tensor(
-                out=beta[:, blocks], in0=attn_bias[:, pr, g_lo:g_hi, :],
-                in1=total[:, blocks].unsqueeze(2).to_broadcast([P, n_g, TILES]), op=MULT,
-            )
-            nc.vector.tensor_tensor(
-                out=beta[:, blocks], in0=beta[:, blocks],
-                in1=par[:, blocks, 1, 0:1].to_broadcast([P, n_g, TILES]), op=ADD,
-            )
-            nc.vector.tensor_tensor(
-                out=corr[:, blocks, :, 0:EDGE], in0=short[:, blocks].unsqueeze(2).to_broadcast([P, n_g, TILES, EDGE]),
-                in1=attn_bias[:, pr, g_lo:g_hi, :].unsqueeze(3).to_broadcast([P, n_g, TILES, EDGE]), op=MULT,
-            )
+            elif step == n_taps - 1:
+                nc.vector.tensor_tensor(
+                    out=total[:, blocks].unsqueeze(2), in0=par[:, blocks, 0, last:last + 1], in1=short[:, blocks, 0:1], op=SUB,
+                )
+            elif step == n_taps:
+                nc.vector.tensor_tensor(
+                    out=beta[:, blocks], in0=attn_bias[:, pr, g_lo:g_hi, :],
+                    in1=total[:, blocks].unsqueeze(2).to_broadcast([P, n_g, TILES]), op=MULT,
+                )
+            elif step == n_taps + 1:
+                nc.vector.tensor_tensor(
+                    out=beta[:, blocks], in0=beta[:, blocks],
+                    in1=par[:, blocks, 1, 0:1].to_broadcast([P, n_g, TILES]), op=ADD,
+                )
+            else:
+                nc.vector.tensor_tensor(
+                    out=corr[:, blocks, :, 0:EDGE], in0=short[:, blocks].unsqueeze(2).to_broadcast([P, n_g, TILES, EDGE]),
+                    in1=attn_bias[:, pr, g_lo:g_hi, :].unsqueeze(3).to_broadcast([P, n_g, TILES, EDGE]), op=MULT,
+                )
+
+        fillers = []
+        taken = {"count": 0}
+
+        def fill():
+            if taken["count"] < len(fillers):
+                step, arguments = fillers[taken["count"]]
+                taken["count"] += 1
+                step(*arguments)
+
+        def flush():
+            for i in range(len(fillers) - taken["count"]):
+                fill()
+
+        def derive_parameters(pr, g_lo, g_hi):
+            for step in range(TAPS[g_hi - 1] + 3):
+                fillers.append((derive_step, (pr, g_lo, g_hi, step)))
 
         def weight(pr, g, t):
             return par[:, block(pr, g), 0, MAX_TAPS - 1 - t:MAX_TAPS - t]
@@ -240,8 +281,7 @@ def tile_tranceptionblockattention_pa_kernel(
             for c in range(PASSES):
                 for u in range(2):
                     nc.tensor.transpose(xt[:, c, u, :], x_words[:, tt, c * words + u:(c + 1) * words:2], ident_f32[:])
-            copy = nc.scalar.copy if tt % 2 == 0 else nc.vector.tensor_copy
-            copy(out=x_grouped_words[:, :, tt * P:(tt + 1) * P, :], in_=xt[:].rearrange("p c u t -> p c t u"))
+            nc.scalar.copy(out=x_grouped_words[:, :, tt * P:(tt + 1) * P, :], in_=xt[:].rearrange("p c u t -> p c t u"))
 
         def quantise_x(b):
             for c in range(PASSES):
@@ -250,6 +290,7 @@ def tile_tranceptionblockattention_pa_kernel(
                     scales=x_scales[:, c, b * S:(b + 1) * S],
                     in_=x_grouped[:, c, b * S:(b + 1) * S, :].rearrange("p t j -> p (t j)"),
                 )
+                fill()
 
         x_ps = {}
         acc = {}
@@ -274,6 +315,8 @@ def tile_tranceptionblockattention_pa_kernel(
 
         def scalar_taps(n):
             pr, g, f, b = units[n]
+            if (f, b) == (0, 0) and (g == CONV_ORDER[0] or (pr, g) == (0, CONV_ORDER[1])):
+                flush()
             acc[n] = acc_pool.tile([P, S], F32, name="acc")
             nc.scalar.activation(
                 out=acc[n][:], in_=x_ps[n][:], func=IDENTITY,
@@ -283,13 +326,12 @@ def tile_tranceptionblockattention_pa_kernel(
                 side_slot[(n, t)] = len(side_slot) % SIDE_SLOTS
                 nc.scalar.activation(out=side[:, side_slot[(n, t)], HALO:], in_=x_ps[n][:], func=COPY, scale=weight(pr, g, t))
 
-        def convolve(n):
+        def vector_tap(n, t):
             pr, g, f, b = units[n]
-            for t in range(1, TAPS[g] - SCALAR_SIDES[g]):
-                nc.vector.scalar_tensor_tensor(
-                    out=acc[n][:, t:], in0=x_ps[n][:, 0:S - t], scalar=weight(pr, g, t),
-                    in1=acc[n][:, t:], op0=MULT, op1=ADD,
-                )
+            nc.vector.scalar_tensor_tensor(
+                out=acc[n][:, t:], in0=x_ps[n][:, 0:S - t], scalar=weight(pr, g, t),
+                in1=acc[n][:, t:], op0=MULT, op1=ADD,
+            )
 
         def transposes(n):
             pr, g, f, b = units[n]
@@ -355,39 +397,49 @@ def tile_tranceptionblockattention_pa_kernel(
         regroup_on_vector(0)
         for j in range(1, WG_BUFS):
             regroup_on_gpsimd(j)
-        transpose_x(0)
-        transpose_x(1)
+        for tt in range(TOKEN_TILES):
+            transpose_x(tt)
+        spread_parameters(0, 1, CONV_ORDER[0])
         quantise(0)
         regroup_on_gpsimd(WG_BUFS)
-        transpose_x(2)
-        transpose_x(3)
+        for i in range(len(fillers) // 2):
+            fill()
         quantise_x(0)
         for tt in range(TOKEN_TILES, 2 * TOKEN_TILES):
             transpose_x(tt)
+        flush()
         quantise_x(1)
 
-        for n in range(-PE_LEAD, len(units) + 1):
-            if 0 <= n - 1:
-                transposes(n - 1)
-            if n + PE_LEAD < len(units):
-                project(n + PE_LEAD)
-            if n in plain_at:
-                project_plain(plain_at[n])
-            if 0 <= n + ACT_LEAD < len(units):
-                scalar_taps(n + ACT_LEAD)
-            if 0 <= n - 1:
-                evacuate(n - 1)
-            if 0 <= n < len(units):
-                convolve(n)
-            if n - 1 in plain_at:
-                finish_plain(plain_at[n - 1])
+        def unit_done(n):
             for j in quantise_at.get(n, []):
                 quantise(j)
                 if j + WG_BUFS < len(group_seq):
                     regroup_on_gpsimd(j + WG_BUFS)
-            if n == 0:
-                spread_parameters(0, 1, CONV_ORDER[0])
-                derive_parameters(0, 1, CONV_ORDER[0])
-            if n in plain_at and plain_at[n] % 4 == 0 and units[n][0] + 1 < PROJ:
+            if units[n][1:] == (2, 0, 0) and units[n][0] + 1 < PROJ:
                 spread_parameters(units[n][0] + 1, 1, GROUPS)
                 derive_parameters(units[n][0] + 1, 1, GROUPS)
+            if n + PLAIN_LEAD in plain_at:
+                project_plain(plain_at[n + PLAIN_LEAD])
+            if n + X_BANKS < len(units):
+                project(n + X_BANKS)
+            transposes(n)
+            if n + ACT_LEAD < len(units):
+                scalar_taps(n + ACT_LEAD)
+            if n >= 1:
+                evacuate(n - 1)
+
+        for n in range(X_BANKS):
+            project(n)
+        for n in range(ACT_LEAD):
+            scalar_taps(n)
+        derive_parameters(0, 1, CONV_ORDER[0])
+        for n, t in vector_order:
+            if t == PLAIN:
+                finish_plain(plain_at[n])
+            else:
+                vector_tap(n, t)
+            fill()
+            left[n] -= 1
+            if left[n] == 0:
+                unit_done(n)
+        evacuate(len(units) - 1)

@@ -161,7 +161,6 @@ def tile_tranceptionblockattention_pa_kernel(
                     out=wg[j][:, c].rearrange("p (n i) j -> p n j i", i=4),
                     in_=w_raw[pr][:, c, :, g * GROUP_COLS:(g + 1) * GROUP_COLS].rearrange("p j (n i) -> p n j i", i=4),
                 )
-                fill()
 
         def regroup_on_gpsimd(j):
             pr, g = group_seq[j]
@@ -225,46 +224,33 @@ def tile_tranceptionblockattention_pa_kernel(
             n_taps = TAPS[g_hi - 1]
             if step < n_taps - 1:
                 t = step + 1
-                nc.vector.tensor_tensor(
+                nc.gpsimd.tensor_tensor(
                     out=short[:, blocks, 0:t], in0=short[:, blocks, 0:t],
                     in1=par[:, blocks, 0, last - t:last - t + 1].to_broadcast([P, n_g, t]), op=SUB,
                 )
             elif step == n_taps - 1:
-                nc.vector.tensor_tensor(
+                nc.gpsimd.tensor_tensor(
                     out=total[:, blocks].unsqueeze(2), in0=par[:, blocks, 0, last:last + 1], in1=short[:, blocks, 0:1], op=SUB,
                 )
             elif step == n_taps:
-                nc.vector.tensor_tensor(
+                nc.gpsimd.tensor_tensor(
                     out=beta[:, blocks], in0=attn_bias[:, pr, g_lo:g_hi, :],
                     in1=total[:, blocks].unsqueeze(2).to_broadcast([P, n_g, TILES]), op=MULT,
                 )
             elif step == n_taps + 1:
-                nc.vector.tensor_tensor(
+                nc.gpsimd.tensor_tensor(
                     out=beta[:, blocks], in0=beta[:, blocks],
                     in1=par[:, blocks, 1, 0:1].to_broadcast([P, n_g, TILES]), op=ADD,
                 )
             else:
-                nc.vector.tensor_tensor(
+                nc.gpsimd.tensor_tensor(
                     out=corr[:, blocks, :, 0:EDGE], in0=short[:, blocks].unsqueeze(2).to_broadcast([P, n_g, TILES, EDGE]),
                     in1=attn_bias[:, pr, g_lo:g_hi, :].unsqueeze(3).to_broadcast([P, n_g, TILES, EDGE]), op=MULT,
                 )
 
-        fillers = []
-        taken = {"count": 0}
-
-        def fill():
-            if taken["count"] < len(fillers):
-                step, arguments = fillers[taken["count"]]
-                taken["count"] += 1
-                step(*arguments)
-
-        def flush():
-            for i in range(len(fillers) - taken["count"]):
-                fill()
-
         def derive_parameters(pr, g_lo, g_hi):
             for step in range(TAPS[g_hi - 1] + 3):
-                fillers.append((derive_step, (pr, g_lo, g_hi, step)))
+                derive_step(pr, g_lo, g_hi, step)
 
         def weight(pr, g, t):
             return par[:, block(pr, g), 0, MAX_TAPS - 1 - t:MAX_TAPS - t]
@@ -290,7 +276,6 @@ def tile_tranceptionblockattention_pa_kernel(
                     scales=x_scales[:, c, b * S:(b + 1) * S],
                     in_=x_grouped[:, c, b * S:(b + 1) * S, :].rearrange("p t j -> p (t j)"),
                 )
-                fill()
 
         x_ps = {}
         acc = {}
@@ -315,8 +300,6 @@ def tile_tranceptionblockattention_pa_kernel(
 
         def scalar_taps(n):
             pr, g, f, b = units[n]
-            if (f, b) == (0, 0) and (g == CONV_ORDER[0] or (pr, g) == (0, CONV_ORDER[1])):
-                flush()
             acc[n] = acc_pool.tile([P, S], F32, name="acc")
             nc.scalar.activation(
                 out=acc[n][:], in_=x_ps[n][:], func=IDENTITY,
@@ -395,19 +378,17 @@ def tile_tranceptionblockattention_pa_kernel(
         spread_parameters(0, CONV_ORDER[0], CONV_ORDER[0] + 1)
         derive_parameters(0, CONV_ORDER[0], CONV_ORDER[0] + 1)
         regroup_on_vector(0)
-        for j in range(1, WG_BUFS):
-            regroup_on_gpsimd(j)
         for tt in range(TOKEN_TILES):
             transpose_x(tt)
         spread_parameters(0, 1, CONV_ORDER[0])
+        derive_parameters(0, 1, CONV_ORDER[0])
+        for j in range(1, WG_BUFS):
+            regroup_on_gpsimd(j)
         quantise(0)
         regroup_on_gpsimd(WG_BUFS)
-        for i in range(len(fillers) // 2):
-            fill()
         quantise_x(0)
         for tt in range(TOKEN_TILES, 2 * TOKEN_TILES):
             transpose_x(tt)
-        flush()
         quantise_x(1)
 
         def unit_done(n):
@@ -432,13 +413,11 @@ def tile_tranceptionblockattention_pa_kernel(
             project(n)
         for n in range(ACT_LEAD):
             scalar_taps(n)
-        derive_parameters(0, 1, CONV_ORDER[0])
         for n, t in vector_order:
             if t == PLAIN:
                 finish_plain(plain_at[n])
             else:
                 vector_tap(n, t)
-            fill()
             left[n] -= 1
             if left[n] == 0:
                 unit_done(n)

@@ -29,6 +29,7 @@ EDGE = 8
 SLOT = 16
 HALO = 8
 CONV_ORDER = (3, 2, 1)
+LAST_ORDER = (3, 1, 2)
 SCALAR_SIDES = (0, 1, 1, 2)
 X_BANKS = 4
 ACT_LEAD = 3
@@ -55,7 +56,7 @@ def tile_tranceptionblockattention_pa_kernel(
 
     units = []
     for pr in range(PROJ):
-        for g in CONV_ORDER:
+        for g in (LAST_ORDER if pr == PROJ - 1 else CONV_ORDER):
             for b in range(B):
                 for f in range(TILES):
                     units.append((pr, g, f, b))
@@ -70,7 +71,7 @@ def tile_tranceptionblockattention_pa_kernel(
             plain_at[n] = len(plain_at)
     group_seq = []
     for pr in range(PROJ):
-        for g in CONV_ORDER + (0,):
+        for g in ((3, 1, 0, 2) if pr == PROJ - 1 else (3, 2, 1, 0)):
             group_seq.append((pr, g))
     quantise_at = {}
     for j in range(1, len(group_seq)):

@@ -97,7 +97,7 @@ def tile_tranceptionblockattention_pa_kernel(
     with tc.tile_pool(name="keep", bufs=1) as keep, \
             tc.tile_pool(name="wg_pool", bufs=WG_BUFS) as wg_pool, \
             tc.tile_pool(name="acc_pool", bufs=6) as acc_pool, \
-            tc.tile_pool(name="out_pool", bufs=4) as out_pool, \
+            tc.tile_pool(name="out_pool", bufs=8) as out_pool, \
             tc.psum_pool(name="psum", bufs=2) as psum, \
             tc.manual_schedule():
 
@@ -400,10 +400,10 @@ def tile_tranceptionblockattention_pa_kernel(
             if units[n][1:] == (2, 0, 0) and units[n][0] + 1 < PROJ:
                 spread_parameters(units[n][0] + 1, 1, GROUPS)
                 derive_parameters(units[n][0] + 1, 1, GROUPS)
-            if n + PLAIN_LEAD in plain_at:
-                project_plain(plain_at[n + PLAIN_LEAD])
             if n + X_BANKS < len(units):
                 project(n + X_BANKS)
+            if n + PLAIN_LEAD in plain_at:
+                project_plain(plain_at[n + PLAIN_LEAD])
             transposes(n)
             if n + ACT_LEAD < len(units):
                 scalar_taps(n + ACT_LEAD)

@@ -24,20 +24,18 @@ MAX_TAPS = 7
 CONV_GROUPS = GROUPS - 1
 GROUP_COLS = E // GROUPS
 TILES = GROUP_COLS // P
-TOKEN_TILES = S // P
-EDGE = 8
+PHASES = 2
+HALF = S // PHASES
+BLOCKS = HALF // P
+HEADS = P // D
 SLOT = 16
 HALO = 8
 CONV_ORDER = (3, 2, 1)
 LAST_ORDER = (3, 1, 2)
 SCALAR_SIDES = (0, 1, 1, 2)
-X_BANKS = 4
-ACT_LEAD = 3
-PLAIN_LEAD = 2
-SKEW = 2
-SIDE_SLOTS = 12
 WG_BUFS = 4
-PLAIN = 0
+PLAIN_FIRST = (4, 2, 0)
+LEAD = 2
 
 FLOPS = 2 * B * S * E * PROJ * E + 2 * B * S * PROJ * GROUP_COLS * sum(TAPS[1:])
 
@@ -57,47 +55,34 @@ def tile_tranceptionblockattention_pa_kernel(
     units = []
     for pr in range(PROJ):
         for g in (LAST_ORDER if pr == PROJ - 1 else CONV_ORDER):
-            for b in range(B):
-                for f in range(TILES):
-                    units.append((pr, g, f, b))
+            for f in range(TILES):
+                units.append((pr, g, f))
+    n_units = len(units)
     plain_units = []
     for pr in range(PROJ):
         for b in range(B):
-            for half in range(2):
-                plain_units.append((pr, b, half))
+            for blk in range(BLOCKS):
+                plain_units.append((pr, b, blk))
     plain_at = {}
-    for n in range(len(units)):
-        if units[n][1] == 1:
-            plain_at[n] = len(plain_at)
-    group_seq = []
     for pr in range(PROJ):
-        for g in ((3, 1, 0, 2) if pr == PROJ - 1 else (3, 2, 1, 0)):
+        for i in range(B * BLOCKS):
+            plain_at[pr * n_units // PROJ + PLAIN_FIRST[pr] + i] = len(plain_at)
+    group_seq = []
+    needed = []
+    for pr in range(PROJ):
+        uses = [(units.index((pr, g, 0)) - LEAD, g) for g in (LAST_ORDER if pr == PROJ - 1 else CONV_ORDER)]
+        uses.append((min(n for n in plain_at if plain_at[n] >= pr * B * BLOCKS) - LEAD, 0))
+        for n, g in sorted(uses):
             group_seq.append((pr, g))
+            needed.append(n)
     quantise_at = {}
-    for j in range(1, len(group_seq)):
-        pr, g = group_seq[j]
-        first = units.index((pr, max(g, 1), 0, 0))
-        use = first - X_BANKS if g > 0 else first - PLAIN_LEAD
-        quantise_at.setdefault(max(use - 2, 0), []).append(j)
-    lanes = ([], [])
-    for n in range(len(units)):
-        for t in range(1, TAPS[units[n][1]] - SCALAR_SIDES[units[n][1]]):
-            lanes[n % 2].append((n, t))
-        if n in plain_at:
-            lanes[n % 2].append((n, PLAIN))
-    vector_order = lanes[0][0:SKEW]
-    for i in range(len(lanes[1])):
-        vector_order.append(lanes[1][i])
-        if SKEW + i < len(lanes[0]):
-            vector_order.append(lanes[0][SKEW + i])
-    left = {}
-    for n, t in vector_order:
-        left[n] = left.get(n, 0) + 1
+    for j in range(2, len(group_seq)):
+        quantise_at.setdefault(needed[j], []).append(j)
 
     with tc.tile_pool(name="keep", bufs=1) as keep, \
             tc.tile_pool(name="wg_pool", bufs=WG_BUFS) as wg_pool, \
             tc.tile_pool(name="acc_pool", bufs=6) as acc_pool, \
-            tc.tile_pool(name="out_pool", bufs=8) as out_pool, \
+            tc.tile_pool(name="out_pool", bufs=5) as out_pool, \
             tc.psum_pool(name="psum", bufs=2) as psum, \
             tc.manual_schedule():
 
@@ -132,22 +117,25 @@ def tile_tranceptionblockattention_pa_kernel(
                     .rearrange("(p j) n -> p j n", j=PACK),
                 )
 
-        x_raw = keep.tile([P, B * TOKEN_TILES, E], BF16)
+        x_raw = keep.tile([P, PHASES, B, BLOCKS, E], BF16)
+        load_w(0, CONV_ORDER[0] * GROUP_COLS, GROUP_COLS)
         nc.sync.dma_start(out=bias_rows[0:PROJ * E // P, :], in_=c_attn_b.rearrange("(n m) -> n m", m=P))
         load_parameters(0, CONV_ORDER[0])
-        load_w(0, CONV_ORDER[0] * GROUP_COLS, GROUP_COLS)
-        for b in range(B):
-            for t in range(TOKEN_TILES):
-                nc.sync.dma_start(out=x_raw[:, b * TOKEN_TILES + t, :], in_=hidden_states[b, t * P:(t + 1) * P, :])
-            if b == 0:
-                for g in CONV_ORDER[1:]:
-                    load_parameters(0, g)
-        for g in CONV_ORDER[1:] + (0,):
-            load_w(0, g * GROUP_COLS, GROUP_COLS)
-        load_w(1, 0, E)
+        for ph in range(PHASES):
+            for b in range(B):
+                nc.sync.dma_start(
+                    out=x_raw[:, ph, b],
+                    in_=hidden_states[b].rearrange("(k p a) e -> p a k e", p=P, a=PHASES)[:, ph],
+                )
+        for g in CONV_ORDER[1:]:
+            load_parameters(0, g)
+        load_w(0, CONV_ORDER[1] * GROUP_COLS, GROUP_COLS)
+        load_w(0, 0, GROUP_COLS)
         for pr in range(1, PROJ):
             for g in CONV_ORDER:
                 load_parameters(pr, g)
+        load_w(0, CONV_ORDER[2] * GROUP_COLS, GROUP_COLS)
+        load_w(1, 0, E)
         load_w(2, 0, E)
 
         w_codes = keep.tile([P, PROJ * GROUPS, PASSES, GROUP_COLS], U32, align_bytes=64)
@@ -181,22 +169,33 @@ def tile_tranceptionblockattention_pa_kernel(
                 in_=wg[j][:].rearrange("p c n j -> p (c n j)"),
             )
 
-        attn_bias = keep.tile([P, 4, GROUPS, TILES], F32)
+        conv_bias = keep.tile([P, PROJ * CONV_GROUPS, TILES], F32)
         plain_bias = keep.tile([P, PROJ * TILES, P], F32)
         par = keep.tile([P, PROJ * CONV_GROUPS, 2, SLOT], F32)
         total = keep.tile([P, PROJ * CONV_GROUPS], F32)
-        short = keep.tile([P, PROJ * CONV_GROUPS, EDGE], F32)
+        short = keep.tile([P, PROJ * CONV_GROUPS, HALO], F32)
         beta = keep.tile([P, PROJ * CONV_GROUPS, TILES], F32)
-        corr = keep.tile([P, PROJ * CONV_GROUPS, TILES, P], F32)
-        side = keep.tile([P, SIDE_SLOTS, HALO + S], F32)
+        far = [None]
+        for g in range(1, GROUPS):
+            far_g = []
+            for f in range(TILES):
+                far_gf = keep.tile([P, PHASES, B, HALO + HALF], F32, name="far%d%d" % (g, f))
+                far_g.append(far_gf)
+            far.append(far_g)
+        near = []
+        for f in range(TILES):
+            near_f = keep.tile([P, PHASES + 1, B, HALO + HALF], F32, name="near%d" % f)
+            near.append(near_f)
+            nc.vector.memset(near_f[:, :, :, 0:HALO], 0.0)
         nc.vector.memset(short[:], 0.0)
-        nc.vector.memset(corr[:], 0.0)
-        nc.vector.memset(side[:, :, 0:HALO], 0.0)
 
         def spread_attn_bias():
             bias_ps = psum.tile([P, P], F32, name="bias_ps", tag="z")
             nc.tensor.matmul(out=bias_ps[:], lhsT=bias_rows[:], rhs=ident_bf[:], start=True, stop=True)
-            nc.scalar.copy(out=attn_bias[:].rearrange("p r g f -> p (r g f)"), in_=bias_ps[:, 0:4 * GROUPS * TILES])
+            nc.scalar.copy(
+                out=conv_bias[:].rearrange("p (r g) f -> p r (g f)", r=PROJ),
+                in_=bias_ps[:, 0:PROJ * GROUPS * TILES].rearrange("p (r g) -> p r g", r=PROJ)[:, :, TILES:],
+            )
             for first in range(0, PROJ * TILES, 4):
                 n_rows = min(4, PROJ * TILES - first)
                 rows_ps = psum.tile([P, 4, P], F32, name="rows_ps", tag="z")
@@ -208,218 +207,268 @@ def tile_tranceptionblockattention_pa_kernel(
                     )
                 nc.scalar.copy(out=plain_bias[:, first:first + n_rows, :], in_=rows_ps[:, 0:n_rows, :])
 
-        def spread_parameters(pr, g_lo, g_hi):
-            blocks = slice(block(pr, g_lo), block(pr, g_hi))
-            n_g = g_hi - g_lo
-            par_ps = psum.tile([P, CONV_GROUPS * 2 * SLOT], F32, name="par_ps", tag="z")
+        par_ps = {}
+
+        def spread_parameters(lo, hi):
+            par_ps[lo] = psum.tile([P, PROJ * CONV_GROUPS * 2 * SLOT], F32, name="par_b", tag="z")
             nc.tensor.matmul(
-                out=par_ps[:, 0:n_g * 2 * SLOT], lhsT=twice[:].rearrange("p a d -> p (a d)"),
-                rhs=par_in[:, blocks].rearrange("p n k i -> p (n k i)"), start=True, stop=True,
+                out=par_ps[lo][:, 0:(hi - lo) * 2 * SLOT], lhsT=twice[:].rearrange("p a d -> p (a d)"),
+                rhs=par_in[:, lo:hi].rearrange("p n k i -> p (n k i)"), start=True, stop=True,
             )
-            nc.scalar.copy(out=par[:, blocks].rearrange("p n k i -> p (n k i)"), in_=par_ps[:, 0:n_g * 2 * SLOT])
 
-        def derive_step(pr, g_lo, g_hi, step):
-            blocks = slice(block(pr, g_lo), block(pr, g_hi))
-            n_g = g_hi - g_lo
+        def take_parameters(lo, hi):
+            nc.scalar.copy(out=par[:, lo:hi].rearrange("p n k i -> p (n k i)"), in_=par_ps[lo][:, 0:(hi - lo) * 2 * SLOT])
+
+        def derive_parameters(lo, hi, n_taps):
+            n = hi - lo
             last = MAX_TAPS - 1
-            n_taps = TAPS[g_hi - 1]
-            if step < n_taps - 1:
-                t = step + 1
+            for t in range(1, n_taps):
                 nc.gpsimd.tensor_tensor(
-                    out=short[:, blocks, 0:t], in0=short[:, blocks, 0:t],
-                    in1=par[:, blocks, 0, last - t:last - t + 1].to_broadcast([P, n_g, t]), op=SUB,
+                    out=short[:, lo:hi, 0:t], in0=short[:, lo:hi, 0:t],
+                    in1=par[:, lo:hi, 0, last - t:last - t + 1].to_broadcast([P, n, t]), op=SUB,
                 )
-            elif step == n_taps - 1:
-                nc.gpsimd.tensor_tensor(
-                    out=total[:, blocks].unsqueeze(2), in0=par[:, blocks, 0, last:last + 1], in1=short[:, blocks, 0:1], op=SUB,
-                )
-            elif step == n_taps:
-                nc.gpsimd.tensor_tensor(
-                    out=beta[:, blocks], in0=attn_bias[:, pr, g_lo:g_hi, :],
-                    in1=total[:, blocks].unsqueeze(2).to_broadcast([P, n_g, TILES]), op=MULT,
-                )
-            elif step == n_taps + 1:
-                nc.gpsimd.tensor_tensor(
-                    out=beta[:, blocks], in0=beta[:, blocks],
-                    in1=par[:, blocks, 1, 0:1].to_broadcast([P, n_g, TILES]), op=ADD,
-                )
-            else:
-                nc.gpsimd.tensor_tensor(
-                    out=corr[:, blocks, :, 0:EDGE], in0=short[:, blocks].unsqueeze(2).to_broadcast([P, n_g, TILES, EDGE]),
-                    in1=attn_bias[:, pr, g_lo:g_hi, :].unsqueeze(3).to_broadcast([P, n_g, TILES, EDGE]), op=MULT,
-                )
+            nc.gpsimd.tensor_tensor(
+                out=total[:, lo:hi].unsqueeze(2), in0=par[:, lo:hi, 0, last:last + 1], in1=short[:, lo:hi, 0:1], op=SUB,
+            )
+            nc.gpsimd.tensor_tensor(
+                out=beta[:, lo:hi], in0=conv_bias[:, lo:hi], in1=total[:, lo:hi].unsqueeze(2).to_broadcast([P, n, TILES]), op=MULT,
+            )
+            nc.gpsimd.tensor_tensor(
+                out=beta[:, lo:hi], in0=beta[:, lo:hi], in1=par[:, lo:hi, 1, 0:1].to_broadcast([P, n, TILES]), op=ADD,
+            )
 
-        def derive_parameters(pr, g_lo, g_hi):
-            for step in range(TAPS[g_hi - 1] + 3):
-                derive_step(pr, g_lo, g_hi, step)
+        def correct_edge(pr, g):
+            u = (TAPS[g] - 1) // PHASES
+            for f in range(TILES):
+                nc.gpsimd.tensor_tensor(
+                    out=far[g][f][:, :, :, HALO - u:HALO],
+                    in0=short[:, block(pr, g), 0:PHASES * u].rearrange("p (i a) -> p a i", a=PHASES)
+                    .unsqueeze(2).to_broadcast([P, PHASES, B, u]),
+                    in1=conv_bias[:, block(pr, g), f:f + 1].unsqueeze(2).unsqueeze(3).to_broadcast([P, PHASES, B, u]), op=MULT,
+                )
 
         def weight(pr, g, t):
             return par[:, block(pr, g), 0, MAX_TAPS - 1 - t:MAX_TAPS - t]
 
         x_words = x_raw[:].bitcast(F32)
-        x_grouped = keep.tile([P, PASSES, B * S, PACK], BF16, align_bytes=64)
-        x_grouped_words = x_grouped[:].bitcast(F32)
-        x_codes = keep.tile([P, PASSES, B * S], U32, align_bytes=64)
-        x_scales = keep.tile([P, PASSES, B * S], U8, align_bytes=64)
+        x_grouped = []
+        for c in range(PASSES):
+            x_grouped_c = keep.tile([P, PHASES, B, HALF, PACK], BF16, name="x_grouped%d" % c, align_bytes=64)
+            x_grouped.append(x_grouped_c)
+        x_codes = keep.tile([P, PASSES, PHASES, B * HALF], U32, align_bytes=64)
+        x_scales = keep.tile([P, PASSES, PHASES, B * HALF], U8, align_bytes=64)
         words = K_PASS // 2
 
-        def transpose_x(tt):
-            xt = psum.tile([P, PASSES, 2, P], F32, name="xt", tag="x", bufs=X_BANKS)
+        def transpose_x(ph, b, copy_out):
             for c in range(PASSES):
-                for u in range(2):
-                    nc.tensor.transpose(xt[:, c, u, :], x_words[:, tt, c * words + u:(c + 1) * words:2], ident_f32[:])
-            nc.scalar.copy(out=x_grouped_words[:, :, tt * P:(tt + 1) * P, :], in_=xt[:].rearrange("p c u t -> p c t u"))
+                xt = psum.tile([P, BLOCKS, 2, P], F32, name="xt", tag="x", bufs=LEAD * PHASES)
+                for blk in range(BLOCKS):
+                    for u in range(2):
+                        nc.tensor.transpose(
+                            xt[:, blk, u, :], x_words[:, ph, b, blk, c * words + u:(c + 1) * words:2], ident_f32[:])
+                copy_out[c](
+                    out=x_grouped[c][:].bitcast(F32)[:, ph, b].rearrange("p (k t) u -> p k t u", t=P),
+                    in_=xt[:].rearrange("p k u t -> p k t u"),
+                )
 
-        def quantise_x(b):
+        def quantise_x(ph, b):
             for c in range(PASSES):
                 nc.vector.quantize_mx(
-                    out=x_codes[:, c, b * S:(b + 1) * S].bitcast(FP8X4),
-                    scales=x_scales[:, c, b * S:(b + 1) * S],
-                    in_=x_grouped[:, c, b * S:(b + 1) * S, :].rearrange("p t j -> p (t j)"),
+                    out=x_codes[:, c, ph, b * HALF:(b + 1) * HALF].bitcast(FP8X4),
+                    scales=x_scales[:, c, ph, b * HALF:(b + 1) * HALF],
+                    in_=x_grouped[c][:, ph, b].rearrange("p t j -> p (t j)"),
                 )
 
         x_ps = {}
         acc = {}
         y_ps = {}
-        side_slot = {}
 
-        def side_taps(g):
-            return range(TAPS[g] - SCALAR_SIDES[g], TAPS[g])
+        def source(ph, t):
+            src = (ph - t) % PHASES
+            return src, (t + src - ph) // PHASES
+
+        def sides(n):
+            g = units[n][1]
+            pairs = [(t, ph) for t in range(TAPS[g] - SCALAR_SIDES[g], TAPS[g]) for ph in range(PHASES)]
+            if n in plain_at and g > 1:
+                pairs.append((TAPS[g] - SCALAR_SIDES[g] - 1, 0))
+            return pairs
+
+        def vector_sides(n):
+            if units[n][1] != 1:
+                return ()
+            return (1,) if n in plain_at else (0, 1)
+
+        def side(n, t, ph):
+            pr, g, f = units[n]
+            if t == TAPS[g] - 1:
+                return far[g][f][:, ph]
+            return near[f][:, ph if t >= TAPS[g] - SCALAR_SIDES[g] else PHASES]
 
         def project(n):
-            pr, g, f, b = units[n]
+            pr, g, f = units[n]
             pg = pr * GROUPS + g
             cols = slice(f * P, (f + 1) * P)
-            x_ps[n] = psum.tile([P, S], F32, name="x_b", tag="x", bufs=X_BANKS)
-            for c in range(PASSES):
-                nc.tensor.matmul_mx(
-                    out=x_ps[n][:],
-                    lhsT=w_codes[:, pg, c, cols].bitcast(FP8X4), lhsT_scale=w_scales[:, pg, c, cols],
-                    rhs=x_codes[:, c, b * S:(b + 1) * S].bitcast(FP8X4), rhs_scale=x_scales[:, c, b * S:(b + 1) * S],
-                    start=(c == 0), stop=(c == PASSES - 1),
-                )
+            for ph in range(PHASES):
+                x_ps[(n, ph)] = psum.tile([P, B, HALF], F32, name="x_b", tag="x", bufs=LEAD * PHASES)
+                for c in range(PASSES):
+                    nc.tensor.matmul_mx(
+                        out=x_ps[(n, ph)][:].rearrange("p b i -> p (b i)"),
+                        lhsT=w_codes[:, pg, c, cols].bitcast(FP8X4), lhsT_scale=w_scales[:, pg, c, cols],
+                        rhs=x_codes[:, c, ph, :].bitcast(FP8X4), rhs_scale=x_scales[:, c, ph, :],
+                        start=(c == 0), stop=(c == PASSES - 1),
+                    )
 
         def scalar_taps(n):
-            pr, g, f, b = units[n]
-            acc[n] = acc_pool.tile([P, S], F32, name="acc")
-            nc.scalar.activation(
-                out=acc[n][:], in_=x_ps[n][:], func=IDENTITY,
-                scale=weight(pr, g, 0), bias=beta[:, block(pr, g), f:f + 1],
-            )
-            for t in side_taps(g):
-                side_slot[(n, t)] = len(side_slot) % SIDE_SLOTS
-                nc.scalar.activation(out=side[:, side_slot[(n, t)], HALO:], in_=x_ps[n][:], func=COPY, scale=weight(pr, g, t))
+            pr, g, f = units[n]
+            for src in range(PHASES):
+                acc[(n, src)] = acc_pool.tile([P, B, HALF], F32, name="acc")
+                nc.scalar.activation(
+                    out=acc[(n, src)][:], in_=x_ps[(n, src)][:], func=IDENTITY,
+                    scale=weight(pr, g, 0), bias=beta[:, block(pr, g), f:f + 1],
+                )
+                for t, ph in sides(n):
+                    if source(ph, t)[0] == src and ph not in vector_sides(n):
+                        nc.scalar.activation(
+                            out=side(n, t, ph)[:, :, HALO:], in_=x_ps[(n, src)][:], func=COPY, scale=weight(pr, g, t),
+                        )
 
-        def vector_tap(n, t):
-            pr, g, f, b = units[n]
+        def vector_taps(n, src):
+            pr, g, f = units[n]
+            by_phase = [
+                [t for t in range(1, TAPS[g]) if source(ph, t)[0] == src and (t, ph) not in sides(n)] for ph in range(PHASES)]
+            order = (0, 1) if len(by_phase[0]) > len(by_phase[1]) else (1, 0)
+            for i in range(max(len(taps) for taps in by_phase)):
+                for ph in order:
+                    if i < len(by_phase[ph]):
+                        vector_tap(n, by_phase[ph][i], ph)
+            t = TAPS[g] - 1
+            for ph in vector_sides(n):
+                if source(ph, t)[0] == src:
+                    nc.vector.tensor_scalar(
+                        out=side(n, t, ph)[:, :, HALO:], in0=x_ps[(n, src)][:], scalar1=weight(pr, g, t), scalar2=None, op0=MULT,
+                    )
+
+        def vector_tap(n, t, ph):
+            pr, g, f = units[n]
+            src, u = source(ph, t)
             nc.vector.scalar_tensor_tensor(
-                out=acc[n][:, t:], in0=x_ps[n][:, 0:S - t], scalar=weight(pr, g, t),
-                in1=acc[n][:, t:], op0=MULT, op1=ADD,
+                out=acc[(n, ph)][:, :, u:], in0=x_ps[(n, src)][:, :, 0:HALF - u], scalar=weight(pr, g, t),
+                in1=acc[(n, ph)][:, :, u:], op0=MULT, op1=ADD,
             )
 
         def transposes(n):
-            pr, g, f, b = units[n]
-            y_ps[n] = psum.tile([P, TOKEN_TILES, P], F32, name="y_b", tag="y")
-            for tt in range(TOKEN_TILES):
-                parts = [acc[n][:, tt * P:(tt + 1) * P]]
-                for t in side_taps(g):
-                    parts.append(side[:, side_slot[(n, t)], HALO + tt * P - t:HALO + (tt + 1) * P - t])
-                if tt == 0:
-                    parts.append(corr[:, block(pr, g), f, :])
-                for k in range(len(parts)):
-                    nc.tensor.matmul(
-                        out=y_ps[n][:, tt, :], lhsT=parts[k], rhs=ident_f32[:], is_transpose=True,
-                        start=(k == 0), stop=(k == len(parts) - 1),
-                    )
+            pr, g, f = units[n]
+            for ph in range(PHASES):
+                y_ps[(n, ph)] = psum.tile([P, B * BLOCKS, P], F32, name="y_b", tag="y")
+                for b in range(B):
+                    for blk in range(BLOCKS):
+                        parts = [acc[(n, ph)][:, b, blk * P:(blk + 1) * P]]
+                        for t, to in sides(n):
+                            if to == ph:
+                                first = HALO + blk * P - source(ph, t)[1]
+                                parts.append(side(n, t, ph)[:, b, first:first + P])
+                        for k in range(len(parts)):
+                            nc.tensor.matmul(
+                                out=y_ps[(n, ph)][:, b * BLOCKS + blk, :], lhsT=parts[k], rhs=ident_f32[:], is_transpose=True,
+                                start=(k == 0), stop=(k == len(parts) - 1),
+                            )
 
         def evacuate(n):
-            pr, g, f, b = units[n]
-            o_sb = out_pool.tile([P, TOKEN_TILES, P], F32, name="o_sb")
-            nc.scalar.copy(out=o_sb[:], in_=y_ps[n][:])
-            for h in range(P // D):
-                head = (g * TILES + f) * (P // D) + h
-                nc.sync.dma_start(
-                    out=outs[pr][b, head].rearrange("(t p) d -> p t d", p=P),
-                    in_=o_sb[:, :, h * D:(h + 1) * D],
-                )
+            pr, g, f = units[n]
+            o_sb = out_pool.tile([P, B * BLOCKS, HEADS, PHASES, D], F32, name="o_sb")
+            for ph in range(PHASES):
+                nc.scalar.copy(out=o_sb[:, :, :, ph, :], in_=y_ps[(n, ph)][:].rearrange("p k (h d) -> p k h d", d=D))
+            for b in range(B):
+                for h in range(HEADS):
+                    nc.sync.dma_start(
+                        out=outs[pr][b, (g * TILES + f) * HEADS + h].rearrange("(k p a) d -> p k (a d)", p=P, a=PHASES),
+                        in_=o_sb[:, b * BLOCKS:(b + 1) * BLOCKS, h].rearrange("p k a d -> p k (a d)"),
+                    )
 
         z_ps = {}
 
         def project_plain(k):
-            pr, b, half = plain_units[k]
+            pr, b, blk = plain_units[k]
             pg = pr * GROUPS
-            z_ps[k] = psum.tile([P, 2, GROUP_COLS], F32, name="z_b", tag="z")
-            for i in range(2):
-                tokens = slice(b * S + (2 * half + i) * P, b * S + (2 * half + i + 1) * P)
+            z_ps[k] = psum.tile([P, PHASES, GROUP_COLS], F32, name="z_b", tag="z")
+            first = b * HALF + blk * P
+            for ph in range(PHASES):
                 for c in range(PASSES):
                     nc.tensor.matmul_mx(
-                        out=z_ps[k][:, i, :],
-                        lhsT=x_codes[:, c, tokens].bitcast(FP8X4), lhsT_scale=x_scales[:, c, tokens],
+                        out=z_ps[k][:, ph, :],
+                        lhsT=x_codes[:, c, ph, first:first + P].bitcast(FP8X4), lhsT_scale=x_scales[:, c, ph, first:first + P],
                         rhs=w_codes[:, pg, c, :].bitcast(FP8X4), rhs_scale=w_scales[:, pg, c, :],
                         start=(c == 0), stop=(c == PASSES - 1),
                     )
 
         def finish_plain(k):
-            pr, b, half = plain_units[k]
-            o_plain = out_pool.tile([P, 2, GROUP_COLS], F32, name="o_plain")
+            pr, b, blk = plain_units[k]
+            o_plain = out_pool.tile([P, GROUP_COLS // D, PHASES, D], F32, name="o_plain")
             nc.vector.tensor_tensor(
-                out=o_plain[:], in0=z_ps[k][:],
-                in1=plain_bias[:, pr * TILES:(pr + 1) * TILES, :].rearrange("p a m -> p (a m)")
-                .unsqueeze(1).to_broadcast([P, 2, GROUP_COLS]),
+                out=o_plain[:].rearrange("p h a d -> p a h d"), in0=z_ps[k][:].rearrange("p a (h d) -> p a h d", d=D),
+                in1=plain_bias[:, pr * TILES:(pr + 1) * TILES, :].rearrange("p f (h d) -> p (f h) d", d=D)
+                .unsqueeze(1).to_broadcast([P, PHASES, GROUP_COLS // D, D]),
                 op=ADD,
             )
-            for i in range(2):
-                first = (2 * half + i) * P
-                nc.sync.dma_start(
-                    out=outs[pr][b, 0:GROUP_COLS // D, first:first + P, :].rearrange("h p d -> p h d"),
-                    in_=o_plain[:, i, :].rearrange("p (h d) -> p h d", d=D),
-                )
+            nc.sync.dma_start(
+                out=outs[pr][b, 0:GROUP_COLS // D, blk * P * PHASES:(blk + 1) * P * PHASES, :]
+                .rearrange("h (p a) d -> p h (a d)", a=PHASES),
+                in_=o_plain[:].rearrange("p h a d -> p h (a d)"),
+            )
 
         spread_attn_bias()
-        spread_parameters(0, CONV_ORDER[0], CONV_ORDER[0] + 1)
-        derive_parameters(0, CONV_ORDER[0], CONV_ORDER[0] + 1)
+        first_g = CONV_ORDER[0]
+        lead = block(0, first_g)
+        spread_parameters(lead, lead + 1)
+        take_parameters(lead, lead + 1)
+        derive_parameters(lead, lead + 1, TAPS[first_g])
+        correct_edge(0, first_g)
         regroup_on_vector(0)
-        for tt in range(TOKEN_TILES):
-            transpose_x(tt)
-        spread_parameters(0, 1, CONV_ORDER[0])
-        derive_parameters(0, 1, CONV_ORDER[0])
-        for j in range(1, WG_BUFS):
-            regroup_on_gpsimd(j)
         quantise(0)
-        regroup_on_gpsimd(WG_BUFS)
-        quantise_x(0)
-        for tt in range(TOKEN_TILES, 2 * TOKEN_TILES):
-            transpose_x(tt)
-        quantise_x(1)
+        for ph in range(PHASES):
+            for b in range(B):
+                last = ph == PHASES - 1 and b == B - 1
+                transpose_x(ph, b, (nc.scalar.copy, nc.vector.tensor_copy if last else nc.scalar.copy))
+                quantise_x(ph, b)
+        regroup_on_gpsimd(1)
+        quantise(1)
+        for n in range(LEAD):
+            project(n)
+        spread_parameters(0, lead)
+        spread_parameters(lead + 1, PROJ * CONV_GROUPS)
+        scalar_taps(0)
+        take_parameters(0, lead)
+        derive_parameters(0, lead, TAPS[first_g - 1])
+        for g in range(1, first_g):
+            correct_edge(0, g)
+        scalar_taps(1)
+        take_parameters(lead + 1, PROJ * CONV_GROUPS)
+        for j in range(2, WG_BUFS):
+            regroup_on_gpsimd(j)
+        derive_parameters(lead + 1, PROJ * CONV_GROUPS, MAX_TAPS)
+        for j in range(WG_BUFS, 2 + WG_BUFS):
+            regroup_on_gpsimd(j)
 
-        def unit_done(n):
+        for n in range(n_units):
+            if n in plain_at:
+                finish_plain(plain_at[n])
+            vector_taps(n, 0)
             for j in quantise_at.get(n, []):
                 quantise(j)
                 if j + WG_BUFS < len(group_seq):
                     regroup_on_gpsimd(j + WG_BUFS)
-            if units[n][1:] == (2, 0, 0) and units[n][0] + 1 < PROJ:
-                spread_parameters(units[n][0] + 1, 1, GROUPS)
-                derive_parameters(units[n][0] + 1, 1, GROUPS)
-            if n + X_BANKS < len(units):
-                project(n + X_BANKS)
-            if n + PLAIN_LEAD in plain_at:
-                project_plain(plain_at[n + PLAIN_LEAD])
-            transposes(n)
-            if n + ACT_LEAD < len(units):
-                scalar_taps(n + ACT_LEAD)
+            vector_taps(n, 1)
+            if n + LEAD < n_units:
+                project(n + LEAD)
+            if n + LEAD in plain_at:
+                project_plain(plain_at[n + LEAD])
             if n >= 1:
                 evacuate(n - 1)
-
-        for n in range(X_BANKS):
-            project(n)
-        for n in range(ACT_LEAD):
-            scalar_taps(n)
-        for n, t in vector_order:
-            if t == PLAIN:
-                finish_plain(plain_at[n])
-            else:
-                vector_tap(n, t)
-            left[n] -= 1
-            if left[n] == 0:
-                unit_done(n)
-        evacuate(len(units) - 1)
+            transposes(n)
+            pr, g, f = units[n]
+            if f == TILES - 1 and pr + 1 < PROJ:
+                correct_edge(pr + 1, g)
+            if n + LEAD < n_units:
+                scalar_taps(n + LEAD)
+        evacuate(n_units - 1)

@@ -14,6 +14,8 @@ COPY = mybir.ActivationFunctionType.Copy
 
 P = 128
 PACK = 4
+PAIR = 2
+WORDS = PACK // PAIR
 K_PASS = P * PACK
 B, S, E, D = 2, 512, 1024, 64
 PASSES = E // K_PASS
@@ -76,8 +78,9 @@ def tile_tranceptionblockattention_pa_kernel(
             group_seq.append((pr, g))
             needed.append(n)
     quantise_at = {}
-    for j in range(2, len(group_seq)):
-        quantise_at.setdefault(needed[j], []).append(j)
+    for j in range(1, len(group_seq)):
+        early = 1 if group_seq[j][1] == 0 and group_seq[j][0] > 0 else 0
+        quantise_at.setdefault(needed[j] - early, []).append(j)
 
     with tc.tile_pool(name="keep", bufs=1) as keep, \
             tc.tile_pool(name="wg_pool", bufs=WG_BUFS) as wg_pool, \
@@ -109,24 +112,32 @@ def tile_tranceptionblockattention_pa_kernel(
             w_raw_pr = keep.tile([P, PASSES, PACK, E], BF16, name="w_raw%d" % pr)
             w_raw.append(w_raw_pr)
 
-        def load_w(pr, first_col, n_cols):
-            for c in range(PASSES):
-                nc.sync.dma_start(
-                    out=w_raw[pr][:, c, :, first_col:first_col + n_cols],
-                    in_=c_attn_w[c * K_PASS:(c + 1) * K_PASS, pr * E + first_col:pr * E + first_col + n_cols]
-                    .rearrange("(p j) n -> p j n", j=PACK),
-                )
+        def load_w(pr, first_col, n_cols, passes=range(PASSES)):
+            for c in passes:
+                for u in range(WORDS):
+                    first_row = c * K_PASS + u * K_PASS // WORDS
+                    nc.sync.dma_start(
+                        out=w_raw[pr][:, c, u * PAIR:(u + 1) * PAIR, first_col:first_col + n_cols],
+                        in_=c_attn_w[first_row:first_row + K_PASS // WORDS, pr * E + first_col:pr * E + first_col + n_cols]
+                        .rearrange("(p e) n -> p e n", e=PAIR),
+                    )
+
+        def load_x(ph, b):
+            nc.sync.dma_start(
+                out=x_raw[:, ph, b],
+                in_=hidden_states[b].rearrange("(k p a) e -> p a k e", p=P, a=PHASES)[:, ph],
+            )
 
         x_raw = keep.tile([P, PHASES, B, BLOCKS, E], BF16)
-        load_w(0, CONV_ORDER[0] * GROUP_COLS, GROUP_COLS)
+        first_col = CONV_ORDER[0] * GROUP_COLS
+        load_w(0, first_col, GROUP_COLS, (0,))
         nc.sync.dma_start(out=bias_rows[0:PROJ * E // P, :], in_=c_attn_b.rearrange("(n m) -> n m", m=P))
         load_parameters(0, CONV_ORDER[0])
-        for ph in range(PHASES):
-            for b in range(B):
-                nc.sync.dma_start(
-                    out=x_raw[:, ph, b],
-                    in_=hidden_states[b].rearrange("(k p a) e -> p a k e", p=P, a=PHASES)[:, ph],
-                )
+        load_x(0, 0)
+        load_x(0, 1)
+        load_w(0, first_col, GROUP_COLS, (1,))
+        load_x(1, 0)
+        load_x(1, 1)
         for g in CONV_ORDER[1:]:
             load_parameters(0, g)
         load_w(0, CONV_ORDER[1] * GROUP_COLS, GROUP_COLS)
@@ -142,14 +153,21 @@ def tile_tranceptionblockattention_pa_kernel(
         w_scales = keep.tile([P, PROJ * GROUPS, PASSES, GROUP_COLS], U8, align_bytes=64)
         wg = {}
 
-        def regroup_on_vector(j):
-            pr, g = group_seq[j]
-            wg[j] = wg_pool.tile([P, PASSES, GROUP_COLS, PACK], BF16, name="wg", align_bytes=64)
-            for c in range(PASSES):
-                nc.vector.tensor_copy(
-                    out=wg[j][:, c].rearrange("p (n i) j -> p n j i", i=4),
-                    in_=w_raw[pr][:, c, :, g * GROUP_COLS:(g + 1) * GROUP_COLS].rearrange("p j (n i) -> p n j i", i=4),
-                )
+        def prepare_first_group(c):
+            pr, g = group_seq[0]
+            if c == 0:
+                wg[0] = wg_pool.tile([P, PASSES, GROUP_COLS, PACK], BF16, name="wg", align_bytes=64)
+            nc.vector.tensor_copy(
+                out=wg[0][:, c].rearrange("p (n i) j -> p n j i", i=4),
+                in_=w_raw[pr][:, c, :, g * GROUP_COLS:(g + 1) * GROUP_COLS].rearrange("p j (n i) -> p n j i", i=4),
+            )
+
+        def quantise_first_group(c):
+            pr, g = group_seq[0]
+            nc.vector.quantize_mx(
+                out=w_codes[:, pr * GROUPS + g, c].bitcast(FP8X4), scales=w_scales[:, pr * GROUPS + g, c],
+                in_=wg[0][:, c].rearrange("p n j -> p (n j)"),
+            )
 
         def regroup_on_gpsimd(j):
             pr, g = group_seq[j]
@@ -255,17 +273,22 @@ def tile_tranceptionblockattention_pa_kernel(
         for c in range(PASSES):
             x_grouped_c = keep.tile([P, PHASES, B, HALF, PACK], BF16, name="x_grouped%d" % c, align_bytes=64)
             x_grouped.append(x_grouped_c)
+        held = keep.tile([P, 1], U8)
         x_codes = keep.tile([P, PASSES, PHASES, B * HALF], U32, align_bytes=64)
         x_scales = keep.tile([P, PASSES, PHASES, B * HALF], U8, align_bytes=64)
         words = K_PASS // 2
 
         def transpose_x(ph, b, copy_out):
+            last = (ph, b) == (PHASES - 1, B - 1)
             for c in range(PASSES):
-                xt = psum.tile([P, BLOCKS, 2, P], F32, name="xt", tag="x", bufs=LEAD * PHASES)
+                if last:
+                    xt = psum.tile([P, BLOCKS, 2, P], F32, name="xt_last", tag="y")
+                else:
+                    xt = psum.tile([P, BLOCKS, 2, P], F32, name="xt", tag="x", bufs=LEAD * PHASES)
                 for blk in range(BLOCKS):
                     for u in range(2):
                         nc.tensor.transpose(
-                            xt[:, blk, u, :], x_words[:, ph, b, blk, c * words + u:(c + 1) * words:2], ident_f32[:])
+                            xt[:, blk, u, :], x_words[:, ph, b, blk, c * words + u * P:c * words + (u + 1) * P], ident_f32[:])
                 copy_out[c](
                     out=x_grouped[c][:].bitcast(F32)[:, ph, b].rearrange("p (k t) u -> p k t u", t=P),
                     in_=xt[:].rearrange("p k u t -> p k t u"),
@@ -287,17 +310,20 @@ def tile_tranceptionblockattention_pa_kernel(
             src = (ph - t) % PHASES
             return src, (t + src - ph) // PHASES
 
+        def busy(n):
+            return (1 if n in plain_at else 0) + len(quantise_at.get(n, [])) >= 2
+
         def sides(n):
             g = units[n][1]
             pairs = [(t, ph) for t in range(TAPS[g] - SCALAR_SIDES[g], TAPS[g]) for ph in range(PHASES)]
-            if n in plain_at and g > 1:
+            if g > 1 and busy(n):
                 pairs.append((TAPS[g] - SCALAR_SIDES[g] - 1, 0))
             return pairs
 
         def vector_sides(n):
             if units[n][1] != 1:
                 return ()
-            return (1,) if n in plain_at else (0, 1)
+            return (1,) if busy(n) else (0, 1)
 
         def side(n, t, ph):
             pr, g, f = units[n]
@@ -305,11 +331,11 @@ def tile_tranceptionblockattention_pa_kernel(
                 return far[g][f][:, ph]
             return near[f][:, ph if t >= TAPS[g] - SCALAR_SIDES[g] else PHASES]
 
-        def project(n):
+        def project(n, phases=range(PHASES)):
             pr, g, f = units[n]
             pg = pr * GROUPS + g
             cols = slice(f * P, (f + 1) * P)
-            for ph in range(PHASES):
+            for ph in phases:
                 x_ps[(n, ph)] = psum.tile([P, B, HALF], F32, name="x_b", tag="x", bufs=LEAD * PHASES)
                 for c in range(PASSES):
                     nc.tensor.matmul_mx(
@@ -337,11 +363,14 @@ def tile_tranceptionblockattention_pa_kernel(
             pr, g, f = units[n]
             by_phase = [
                 [t for t in range(1, TAPS[g]) if source(ph, t)[0] == src and (t, ph) not in sides(n)] for ph in range(PHASES)]
-            order = (0, 1) if len(by_phase[0]) > len(by_phase[1]) else (1, 0)
-            for i in range(max(len(taps) for taps in by_phase)):
-                for ph in order:
-                    if i < len(by_phase[ph]):
-                        vector_tap(n, by_phase[ph][i], ph)
+            order = (1, 0) if len(by_phase[1]) > len(by_phase[0]) else (0, 1)
+            if (n, src) == (0, 0):
+                turns = [(i, ph) for ph in order for i in range(max(len(taps) for taps in by_phase))]
+            else:
+                turns = [(i, ph) for i in range(max(len(taps) for taps in by_phase)) for ph in order]
+            for i, ph in turns:
+                if i < len(by_phase[ph]):
+                    vector_tap(n, by_phase[ph][i], ph)
             t = TAPS[g] - 1
             for ph in vector_sides(n):
                 if source(ph, t)[0] == src:
@@ -378,7 +407,8 @@ def tile_tranceptionblockattention_pa_kernel(
             pr, g, f = units[n]
             o_sb = out_pool.tile([P, B * BLOCKS, HEADS, PHASES, D], F32, name="o_sb")
             for ph in range(PHASES):
-                nc.scalar.copy(out=o_sb[:, :, :, ph, :], in_=y_ps[(n, ph)][:].rearrange("p k (h d) -> p k h d", d=D))
+                copy_out = nc.vector.tensor_copy if n == n_units - 1 and ph == 1 else nc.scalar.copy
+                copy_out(out=o_sb[:, :, :, ph, :], in_=y_ps[(n, ph)][:].rearrange("p k (h d) -> p k h d", d=D))
             for b in range(B):
                 for h in range(HEADS):
                     nc.sync.dma_start(
@@ -424,17 +454,24 @@ def tile_tranceptionblockattention_pa_kernel(
         take_parameters(lead, lead + 1)
         derive_parameters(lead, lead + 1, TAPS[first_g])
         correct_edge(0, first_g)
-        regroup_on_vector(0)
-        quantise(0)
-        for ph in range(PHASES):
-            for b in range(B):
-                last = ph == PHASES - 1 and b == B - 1
-                transpose_x(ph, b, (nc.scalar.copy, nc.vector.tensor_copy if last else nc.scalar.copy))
-                quantise_x(ph, b)
+        prepare_first_group(0)
+        copies = (nc.scalar.copy, nc.scalar.copy)
+        transpose_x(0, 0, copies)
+        quantise_first_group(0)
+        quantise_x(0, 0)
+        transpose_x(0, 1, copies)
+        prepare_first_group(1)
+        quantise_x(0, 1)
+        transpose_x(1, 0, copies)
+        quantise_first_group(1)
+        project(0, (0,))
+        quantise_x(1, 0)
+        transpose_x(1, 1, (nc.scalar.copy, nc.vector.tensor_copy))
+        quantise_x(1, 1)
+        nc.gpsimd.tensor_copy(out=held[:], in_=x_scales[:, PASSES - 1, PHASES - 1, B * HALF - 1:B * HALF])
         regroup_on_gpsimd(1)
-        quantise(1)
-        for n in range(LEAD):
-            project(n)
+        project(0, (1,))
+        project(1)
         spread_parameters(0, lead)
         spread_parameters(lead + 1, PROJ * CONV_GROUPS)
         scalar_taps(0)
@@ -447,8 +484,7 @@ def tile_tranceptionblockattention_pa_kernel(
         for j in range(2, WG_BUFS):
             regroup_on_gpsimd(j)
         derive_parameters(lead + 1, PROJ * CONV_GROUPS, MAX_TAPS)
-        for j in range(WG_BUFS, 2 + WG_BUFS):
-            regroup_on_gpsimd(j)
+        regroup_on_gpsimd(WG_BUFS)
 
         for n in range(n_units):
             if n in plain_at:

@@ -22,7 +22,6 @@ PASSES = E // K_PASS
 PROJ = 3
 GROUPS = 4
 TAPS = (1, 3, 5, 7)
-MAX_TAPS = 7
 CONV_GROUPS = GROUPS - 1
 GROUP_COLS = E // GROUPS
 TILES = GROUP_COLS // P
@@ -33,10 +32,10 @@ HEADS = P // D
 SLOT = 16
 HALO = 8
 CONV_ORDER = (3, 2, 1)
-LAST_ORDER = (3, 1, 2)
-SCALAR_SIDES = (0, 1, 1, 2)
+LAST_ORDER = (3, 2, 1)
+SCALAR_SIDES = ((2, 2, 2, 1, 1, 0), (2, 2, 2, 1, 1, 0), (2, 2, 2, 1, 1, 0))
+PLAIN_UNITS = ((4, 5, 5, 8), (9, 10, 11, 11), (14, 15, 16, 16))
 WG_BUFS = 4
-PLAIN_FIRST = (4, 2, 0)
 LEAD = 2
 
 FLOPS = 2 * B * S * E * PROJ * E + 2 * B * S * PROJ * GROUP_COLS * sum(TAPS[1:])
@@ -65,22 +64,24 @@ def tile_tranceptionblockattention_pa_kernel(
         for b in range(B):
             for blk in range(BLOCKS):
                 plain_units.append((pr, b, blk))
+    plain_units_done = []
     plain_at = {}
     for pr in range(PROJ):
-        for i in range(B * BLOCKS):
-            plain_at[pr * n_units // PROJ + PLAIN_FIRST[pr] + i] = len(plain_at)
+        for n in PLAIN_UNITS[pr]:
+            plain_at.setdefault(n, []).append(len(plain_units_done))
+            plain_units_done.append(n)
     group_seq = []
-    needed = []
-    for pr in range(PROJ):
-        uses = [(units.index((pr, g, 0)) - LEAD, g) for g in (LAST_ORDER if pr == PROJ - 1 else CONV_ORDER)]
-        uses.append((min(n for n in plain_at if plain_at[n] >= pr * B * BLOCKS) - LEAD, 0))
-        for n, g in sorted(uses):
-            group_seq.append((pr, g))
-            needed.append(n)
     quantise_at = {}
-    for j in range(1, len(group_seq)):
-        early = 1 if group_seq[j][1] == 0 and group_seq[j][0] > 0 else 0
-        quantise_at.setdefault(needed[j] - early, []).append(j)
+    for pr in range(PROJ):
+        first, second, third = LAST_ORDER if pr == PROJ - 1 else CONV_ORDER
+        start = pr * n_units // PROJ
+        places = ((start - LEAD, first), (start - 1, second), (start - 1, 0), (start + LEAD, third))
+        if pr == 0:
+            places = ((None, first), (0, second), (LEAD, 0), (LEAD, third))
+        for n, g in places:
+            if n is not None:
+                quantise_at.setdefault(n, []).append(len(group_seq))
+            group_seq.append((pr, g))
 
     with tc.tile_pool(name="keep", bufs=1) as keep, \
             tc.tile_pool(name="wg_pool", bufs=WG_BUFS) as wg_pool, \
@@ -104,7 +105,7 @@ def tile_tranceptionblockattention_pa_kernel(
             return pr * CONV_GROUPS + g - 1
 
         def load_parameters(pr, g):
-            nc.sync.dma_start(out=par_in[0:D, block(pr, g), 0, MAX_TAPS - TAPS[g]:MAX_TAPS], in_=conv_w[pr][g - 1])
+            nc.sync.dma_start(out=par_in[0:D, block(pr, g), 0, 0:TAPS[g]], in_=conv_w[pr][g - 1])
             nc.sync.dma_start(out=par_in[0:D, block(pr, g), 1, 0:1], in_=conv_b[pr][g - 1].rearrange("(d o) -> d o", o=1))
 
         w_raw = []
@@ -134,9 +135,9 @@ def tile_tranceptionblockattention_pa_kernel(
         nc.sync.dma_start(out=bias_rows[0:PROJ * E // P, :], in_=c_attn_b.rearrange("(n m) -> n m", m=P))
         load_parameters(0, CONV_ORDER[0])
         load_x(0, 0)
-        load_x(0, 1)
-        load_w(0, first_col, GROUP_COLS, (1,))
         load_x(1, 0)
+        load_w(0, first_col, GROUP_COLS, (1,))
+        load_x(0, 1)
         load_x(1, 1)
         for g in CONV_ORDER[1:]:
             load_parameters(0, g)
@@ -190,22 +191,24 @@ def tile_tranceptionblockattention_pa_kernel(
         conv_bias = keep.tile([P, PROJ * CONV_GROUPS, TILES], F32)
         plain_bias = keep.tile([P, PROJ * TILES, P], F32)
         par = keep.tile([P, PROJ * CONV_GROUPS, 2, SLOT], F32)
-        total = keep.tile([P, PROJ * CONV_GROUPS], F32)
-        short = keep.tile([P, PROJ * CONV_GROUPS, HALO], F32)
+        sums = keep.tile([P, PROJ * CONV_GROUPS, 2, SLOT], F32)
+        starts = keep.tile([P, PROJ * CONV_GROUPS, 2, SLOT], F32)
         beta = keep.tile([P, PROJ * CONV_GROUPS, TILES], F32)
-        far = [None]
-        for g in range(1, GROUPS):
+        edge_beta = keep.tile([P, PROJ, TILES, PHASES], F32)
+        far = [None, None]
+        for g in range(2, GROUPS):
             far_g = []
             for f in range(TILES):
                 far_gf = keep.tile([P, PHASES, B, HALO + HALF], F32, name="far%d%d" % (g, f))
                 far_g.append(far_gf)
             far.append(far_g)
         near = []
-        for f in range(TILES):
-            near_f = keep.tile([P, PHASES + 1, B, HALO + HALF], F32, name="near%d" % f)
-            near.append(near_f)
-            nc.vector.memset(near_f[:, :, :, 0:HALO], 0.0)
-        nc.vector.memset(short[:], 0.0)
+        for i in range(2 * LEAD):
+            near_i = keep.tile([P, PHASES, B, HALO + HALF], F32, name="near%d" % i)
+            near.append(near_i)
+            nc.vector.memset(near_i[:, :, :, 0:HALO], 0.0)
+        nc.vector.memset(starts[:], 1.0)
+        nc.vector.memset(starts[:, :, :, 0:1], 0.0)
 
         def spread_attn_bias():
             bias_ps = psum.tile([P, P], F32, name="bias_ps", tag="z")
@@ -237,43 +240,45 @@ def tile_tranceptionblockattention_pa_kernel(
         def take_parameters(lo, hi):
             nc.scalar.copy(out=par[:, lo:hi].rearrange("p n k i -> p (n k i)"), in_=par_ps[lo][:, 0:(hi - lo) * 2 * SLOT])
 
-        def derive_parameters(lo, hi, n_taps):
-            n = hi - lo
-            last = MAX_TAPS - 1
-            for t in range(1, n_taps):
-                nc.gpsimd.tensor_tensor(
-                    out=short[:, lo:hi, 0:t], in0=short[:, lo:hi, 0:t],
-                    in1=par[:, lo:hi, 0, last - t:last - t + 1].to_broadcast([P, n, t]), op=SUB,
+        def derive_parameters(lo, hi):
+            nc.vector.tensor_tensor_scan(
+                out=sums[:, lo:hi].rearrange("p n k i -> p (n k i)"), data0=starts[:, lo:hi].rearrange("p n k i -> p (n k i)"),
+                data1=par[:, lo:hi].rearrange("p n k i -> p (n k i)"), initial=0.0, op0=MULT, op1=ADD,
+            )
+            for n in range(lo, hi):
+                pr, g = divmod(n, CONV_GROUPS)
+                nc.gpsimd.tensor_scalar(
+                    out=beta[:, n], in0=conv_bias[:, n], scalar1=sums[:, n, 0, SLOT - 1:SLOT], scalar2=par[:, n, 1, 0:1],
+                    op0=MULT, op1=ADD,
                 )
-            nc.gpsimd.tensor_tensor(
-                out=total[:, lo:hi].unsqueeze(2), in0=par[:, lo:hi, 0, last:last + 1], in1=short[:, lo:hi, 0:1], op=SUB,
-            )
-            nc.gpsimd.tensor_tensor(
-                out=beta[:, lo:hi], in0=conv_bias[:, lo:hi], in1=total[:, lo:hi].unsqueeze(2).to_broadcast([P, n, TILES]), op=MULT,
-            )
-            nc.gpsimd.tensor_tensor(
-                out=beta[:, lo:hi], in0=beta[:, lo:hi], in1=par[:, lo:hi, 1, 0:1].to_broadcast([P, n, TILES]), op=ADD,
-            )
+                if g + 1 == 1:
+                    for f in range(TILES):
+                        nc.gpsimd.tensor_scalar(
+                            out=edge_beta[:, pr, f], in0=sums[:, n, 0, 0:PHASES][:, ::-1], scalar1=conv_bias[:, n, f:f + 1],
+                            scalar2=beta[:, n, f:f + 1], op0=MULT, op1=SUB,
+                        )
+                        nc.gpsimd.tensor_scalar(
+                            out=edge_beta[:, pr, f], in0=edge_beta[:, pr, f], scalar1=-1.0, scalar2=0.0, op0=MULT, op1=ADD,
+                        )
 
         def correct_edge(pr, g):
+            n = block(pr, g)
             u = (TAPS[g] - 1) // PHASES
+            missing = sums[:, n, 0, 0:TAPS[g] - 1][:, ::-1].rearrange("p (i a) -> p a i", a=PHASES)
             for f in range(TILES):
-                nc.gpsimd.tensor_tensor(
-                    out=far[g][f][:, :, :, HALO - u:HALO],
-                    in0=short[:, block(pr, g), 0:PHASES * u].rearrange("p (i a) -> p a i", a=PHASES)
-                    .unsqueeze(2).to_broadcast([P, PHASES, B, u]),
-                    in1=conv_bias[:, block(pr, g), f:f + 1].unsqueeze(2).unsqueeze(3).to_broadcast([P, PHASES, B, u]), op=MULT,
+                nc.gpsimd.tensor_scalar(
+                    out=far[g][f][:, :, :, HALO - u:HALO], in0=missing.unsqueeze(2).to_broadcast([P, PHASES, B, u]),
+                    scalar1=conv_bias[:, n, f:f + 1], scalar2=-1.0, op0=MULT, op1=MULT,
                 )
 
         def weight(pr, g, t):
-            return par[:, block(pr, g), 0, MAX_TAPS - 1 - t:MAX_TAPS - t]
+            return par[:, block(pr, g), 0, TAPS[g] - 1 - t:TAPS[g] - t]
 
         x_words = x_raw[:].bitcast(F32)
         x_grouped = []
         for c in range(PASSES):
             x_grouped_c = keep.tile([P, PHASES, B, HALF, PACK], BF16, name="x_grouped%d" % c, align_bytes=64)
             x_grouped.append(x_grouped_c)
-        held = keep.tile([P, 1], U8)
         x_codes = keep.tile([P, PASSES, PHASES, B * HALF], U32, align_bytes=64)
         x_scales = keep.tile([P, PASSES, PHASES, B * HALF], U8, align_bytes=64)
         words = K_PASS // 2
@@ -310,80 +315,98 @@ def tile_tranceptionblockattention_pa_kernel(
             src = (ph - t) % PHASES
             return src, (t + src - ph) // PHASES
 
-        def busy(n):
-            return (1 if n in plain_at else 0) + len(quantise_at.get(n, [])) >= 2
+        def side_taps(n):
+            place = n % (n_units // PROJ)
+            n_taps = TAPS[units[n][1]]
+            return range(n_taps - SCALAR_SIDES[units[n][0]][place], n_taps)
 
         def sides(n):
-            g = units[n][1]
-            pairs = [(t, ph) for t in range(TAPS[g] - SCALAR_SIDES[g], TAPS[g]) for ph in range(PHASES)]
-            if g > 1 and busy(n):
-                pairs.append((TAPS[g] - SCALAR_SIDES[g] - 1, 0))
-            return pairs
-
-        def vector_sides(n):
-            if units[n][1] != 1:
-                return ()
-            return (1,) if busy(n) else (0, 1)
+            return [(t, ph) for t in side_taps(n) for ph in range(PHASES)]
 
         def side(n, t, ph):
             pr, g, f = units[n]
-            if t == TAPS[g] - 1:
+            if g > 1 and t == TAPS[g] - 1:
                 return far[g][f][:, ph]
-            return near[f][:, ph if t >= TAPS[g] - SCALAR_SIDES[g] else PHASES]
+            return near[n % (2 * LEAD)][:, ph]
 
-        def project(n, phases=range(PHASES)):
+        def multiply(n, ph, out, first, count):
             pr, g, f = units[n]
             pg = pr * GROUPS + g
             cols = slice(f * P, (f + 1) * P)
-            for ph in phases:
+            steps = slice(first * HALF, (first + count) * HALF)
+            for c in range(PASSES):
+                nc.tensor.matmul_mx(
+                    out=out[:].rearrange("p b i -> p (b i)"),
+                    lhsT=w_codes[:, pg, c, cols].bitcast(FP8X4), lhsT_scale=w_scales[:, pg, c, cols],
+                    rhs=x_codes[:, c, ph, steps].bitcast(FP8X4), rhs_scale=x_scales[:, c, ph, steps],
+                    start=(c == 0), stop=(c == PASSES - 1),
+                )
+
+        def project(n):
+            for ph in range(PHASES):
                 x_ps[(n, ph)] = psum.tile([P, B, HALF], F32, name="x_b", tag="x", bufs=LEAD * PHASES)
-                for c in range(PASSES):
-                    nc.tensor.matmul_mx(
-                        out=x_ps[(n, ph)][:].rearrange("p b i -> p (b i)"),
-                        lhsT=w_codes[:, pg, c, cols].bitcast(FP8X4), lhsT_scale=w_scales[:, pg, c, cols],
-                        rhs=x_codes[:, c, ph, :].bitcast(FP8X4), rhs_scale=x_scales[:, c, ph, :],
-                        start=(c == 0), stop=(c == PASSES - 1),
+                multiply(n, ph, x_ps[(n, ph)], 0, B)
+
+        def project_first(b):
+            for ph in range(PHASES):
+                if b == 0:
+                    x_first = psum.tile([P, 1, HALF], F32, name="x_first0", tag="x", bufs=LEAD * PHASES)
+                else:
+                    x_first = psum.tile([P, 1, HALF], F32, name="x_first1", tag="y")
+                x_ps[(0, ph, b)] = x_first
+                multiply(0, ph, x_first, b, 1)
+
+        def products(n, src, b):
+            return x_ps[(n, src)][:] if b is None else x_ps[(n, src, b)][:]
+
+        def entries(b):
+            return slice(0, B) if b is None else slice(b, b + 1)
+
+        def first_tap(n, src, b=None):
+            pr, g, f = units[n]
+            if b in (None, 0):
+                acc[(n, src)] = acc_pool.tile([P, B, HALF], F32, name="acc")
+            first = 0
+            if g == 1:
+                first = 1
+                nc.scalar.activation(
+                    out=acc[(n, src)][:, :, 0:first], in_=products(n, src, b)[:, :, 0:first], func=IDENTITY,
+                    scale=weight(pr, g, 0), bias=edge_beta[:, pr, f, src:src + 1],
+                )
+            nc.scalar.activation(
+                out=acc[(n, src)][:, entries(b), first:], in_=products(n, src, b)[:, :, first:], func=IDENTITY,
+                scale=weight(pr, g, 0), bias=beta[:, block(pr, g), f:f + 1],
+            )
+
+        def scalar_sides(n, src, b=None):
+            pr, g, f = units[n]
+            for t, ph in sides(n):
+                if source(ph, t)[0] == src:
+                    nc.scalar.activation(
+                        out=side(n, t, ph)[:, entries(b), HALO:], in_=products(n, src, b), func=COPY, scale=weight(pr, g, t),
                     )
 
         def scalar_taps(n):
-            pr, g, f = units[n]
             for src in range(PHASES):
-                acc[(n, src)] = acc_pool.tile([P, B, HALF], F32, name="acc")
-                nc.scalar.activation(
-                    out=acc[(n, src)][:], in_=x_ps[(n, src)][:], func=IDENTITY,
-                    scale=weight(pr, g, 0), bias=beta[:, block(pr, g), f:f + 1],
-                )
-                for t, ph in sides(n):
-                    if source(ph, t)[0] == src and ph not in vector_sides(n):
-                        nc.scalar.activation(
-                            out=side(n, t, ph)[:, :, HALO:], in_=x_ps[(n, src)][:], func=COPY, scale=weight(pr, g, t),
-                        )
+                first_tap(n, src)
+                scalar_sides(n, src)
 
-        def vector_taps(n, src):
+        def vector_taps(n, src, b=None):
             pr, g, f = units[n]
             by_phase = [
                 [t for t in range(1, TAPS[g]) if source(ph, t)[0] == src and (t, ph) not in sides(n)] for ph in range(PHASES)]
             order = (1, 0) if len(by_phase[1]) > len(by_phase[0]) else (0, 1)
-            if (n, src) == (0, 0):
-                turns = [(i, ph) for ph in order for i in range(max(len(taps) for taps in by_phase))]
-            else:
-                turns = [(i, ph) for i in range(max(len(taps) for taps in by_phase)) for ph in order]
-            for i, ph in turns:
-                if i < len(by_phase[ph]):
-                    vector_tap(n, by_phase[ph][i], ph)
-            t = TAPS[g] - 1
-            for ph in vector_sides(n):
-                if source(ph, t)[0] == src:
-                    nc.vector.tensor_scalar(
-                        out=side(n, t, ph)[:, :, HALO:], in0=x_ps[(n, src)][:], scalar1=weight(pr, g, t), scalar2=None, op0=MULT,
-                    )
+            for i in range(max(len(taps) for taps in by_phase)):
+                for ph in order:
+                    if i < len(by_phase[ph]):
+                        vector_tap(n, by_phase[ph][i], ph, b)
 
-        def vector_tap(n, t, ph):
+        def vector_tap(n, t, ph, b):
             pr, g, f = units[n]
             src, u = source(ph, t)
             nc.vector.scalar_tensor_tensor(
-                out=acc[(n, ph)][:, :, u:], in0=x_ps[(n, src)][:, :, 0:HALF - u], scalar=weight(pr, g, t),
-                in1=acc[(n, ph)][:, :, u:], op0=MULT, op1=ADD,
+                out=acc[(n, ph)][:, entries(b), u:], in0=products(n, src, b)[:, :, 0:HALF - u], scalar=weight(pr, g, t),
+                in1=acc[(n, ph)][:, entries(b), u:], op0=MULT, op1=ADD,
             )
 
         def transposes(n):
@@ -447,64 +470,89 @@ def tile_tranceptionblockattention_pa_kernel(
                 in_=o_plain[:].rearrange("p h a d -> p h (a d)"),
             )
 
+        def quantise_for(n):
+            for j in quantise_at.get(n, []):
+                quantise(j)
+
+        def regroup_for(n):
+            for j in quantise_at.get(n, []):
+                if j + WG_BUFS < len(group_seq):
+                    regroup_on_gpsimd(j + WG_BUFS)
+
+        def finish_unit(n):
+            for k in plain_at.get(n + 1, []):
+                finish_plain(k)
+            if n + LEAD < n_units:
+                project(n + LEAD)
+            for k in plain_at.get(n + LEAD, []):
+                project_plain(k)
+            if n >= 1:
+                evacuate(n - 1)
+            transposes(n)
+            if n >= LEAD:
+                pr, g, f = units[n - LEAD]
+                if g > 1 and f == TILES - 1 and pr + 1 < PROJ:
+                    correct_edge(pr + 1, g)
+            if n == 0:
+                spread_parameters(lead + 1, PROJ * CONV_GROUPS)
+            if n + LEAD < n_units:
+                scalar_taps(n + LEAD)
+            if n == LEAD - 1:
+                take_parameters(lead + 1, PROJ * CONV_GROUPS)
+
         spread_attn_bias()
         first_g = CONV_ORDER[0]
         lead = block(0, first_g)
         spread_parameters(lead, lead + 1)
         take_parameters(lead, lead + 1)
-        derive_parameters(lead, lead + 1, TAPS[first_g])
-        correct_edge(0, first_g)
         prepare_first_group(0)
+        derive_parameters(lead, lead + 1)
+        correct_edge(0, first_g)
         copies = (nc.scalar.copy, nc.scalar.copy)
         transpose_x(0, 0, copies)
         quantise_first_group(0)
         quantise_x(0, 0)
-        transpose_x(0, 1, copies)
-        prepare_first_group(1)
-        quantise_x(0, 1)
         transpose_x(1, 0, copies)
-        quantise_first_group(1)
-        project(0, (0,))
+        prepare_first_group(1)
         quantise_x(1, 0)
-        transpose_x(1, 1, (nc.scalar.copy, nc.vector.tensor_copy))
+        quantise_first_group(1)
+        transpose_x(0, 1, (nc.vector.tensor_copy, nc.vector.tensor_copy))
+        quantise_x(0, 1)
+        project_first(0)
+        for src in range(PHASES):
+            first_tap(0, src, 0)
+        transpose_x(1, 1, copies)
+        vector_taps(0, 0, 0)
         quantise_x(1, 1)
-        nc.gpsimd.tensor_copy(out=held[:], in_=x_scales[:, PASSES - 1, PHASES - 1, B * HALF - 1:B * HALF])
         regroup_on_gpsimd(1)
-        project(0, (1,))
+        vector_taps(0, 1, 0)
+        project_first(1)
         project(1)
         spread_parameters(0, lead)
-        spread_parameters(lead + 1, PROJ * CONV_GROUPS)
-        scalar_taps(0)
+        for src in range(PHASES):
+            first_tap(0, src, 1)
+        for src in range(PHASES):
+            scalar_sides(0, src, 0)
         take_parameters(0, lead)
-        derive_parameters(0, lead, TAPS[first_g - 1])
-        for g in range(1, first_g):
-            correct_edge(0, g)
         scalar_taps(1)
-        take_parameters(lead + 1, PROJ * CONV_GROUPS)
-        for j in range(2, WG_BUFS):
+        vector_taps(0, 0, 1)
+        derive_parameters(0, lead)
+        correct_edge(0, 2)
+        for j in range(2, WG_BUFS + 1):
             regroup_on_gpsimd(j)
-        derive_parameters(lead + 1, PROJ * CONV_GROUPS, MAX_TAPS)
-        regroup_on_gpsimd(WG_BUFS)
+        quantise_for(0)
+        regroup_for(0)
+        vector_taps(0, 1, 1)
+        for src in range(PHASES):
+            scalar_sides(0, src, 1)
+        finish_unit(0)
 
-        for n in range(n_units):
-            if n in plain_at:
-                finish_plain(plain_at[n])
+        for n in range(1, n_units):
             vector_taps(n, 0)
-            for j in quantise_at.get(n, []):
-                quantise(j)
-                if j + WG_BUFS < len(group_seq):
-                    regroup_on_gpsimd(j + WG_BUFS)
+            quantise_for(n)
             vector_taps(n, 1)
-            if n + LEAD < n_units:
-                project(n + LEAD)
-            if n + LEAD in plain_at:
-                project_plain(plain_at[n + LEAD])
-            if n >= 1:
-                evacuate(n - 1)
-            transposes(n)
-            pr, g, f = units[n]
-            if f == TILES - 1 and pr + 1 < PROJ:
-                correct_edge(pr + 1, g)
-            if n + LEAD < n_units:
-                scalar_taps(n + LEAD)
+            if n == LEAD:
+                derive_parameters(lead + 1, PROJ * CONV_GROUPS)
+            regroup_for(n)
+            finish_unit(n)
         evacuate(n_units - 1)

@@ -7,7 +7,6 @@ U32 = mybir.dt.uint32
 U8 = mybir.dt.uint8
 FP8X4 = mybir.dt.float8_e4m3fn_x4
 ADD = mybir.AluOpType.add
-SUB = mybir.AluOpType.subtract
 MULT = mybir.AluOpType.mult
 IDENTITY = mybir.ActivationFunctionType.Identity
 COPY = mybir.ActivationFunctionType.Copy
@@ -36,6 +35,7 @@ LAST_ORDER = (3, 2, 1)
 SCALAR_SIDES = ((2, 2, 2, 1, 1, 0), (2, 2, 2, 1, 1, 0), (2, 2, 2, 1, 1, 0))
 PLAIN_UNITS = ((4, 5, 5, 8), (9, 10, 11, 11), (14, 15, 16, 16))
 WG_BUFS = 4
+REGROUP_COLS = 128
 LEAD = 2
 
 FLOPS = 2 * B * S * E * PROJ * E + 2 * B * S * PROJ * GROUP_COLS * sum(TAPS[1:])
@@ -174,11 +174,12 @@ def tile_tranceptionblockattention_pa_kernel(
             pr, g = group_seq[j]
             wg[j] = wg_pool.tile([P, PASSES, GROUP_COLS, PACK], BF16, name="wg", align_bytes=64)
             for c in range(PASSES):
-                nc.gpsimd.tensor_scalar(
-                    out=wg[j][:, c],
-                    in0=w_raw[pr][:, c, :, g * GROUP_COLS:(g + 1) * GROUP_COLS].rearrange("p j n -> p n j"),
-                    scalar1=1.0, scalar2=0.0, op0=MULT, op1=ADD,
-                )
+                for first in range(0, GROUP_COLS, REGROUP_COLS):
+                    cols = slice(g * GROUP_COLS + first, g * GROUP_COLS + first + REGROUP_COLS)
+                    nc.gpsimd.tensor_scalar(
+                        out=wg[j][:, c, first:first + REGROUP_COLS], in0=w_raw[pr][:, c, :, cols].rearrange("p j n -> p n j"),
+                        scalar1=1.0, scalar2=0.0, op0=MULT, op1=ADD,
+                    )
 
         def quantise(j):
             pr, g = group_seq[j]
@@ -188,13 +189,14 @@ def tile_tranceptionblockattention_pa_kernel(
                 in_=wg[j][:].rearrange("p c n j -> p (c n j)"),
             )
 
+        minus_bias = keep.tile([P, PROJ * CONV_GROUPS, TILES], F32)
         conv_bias = keep.tile([P, PROJ * CONV_GROUPS, TILES], F32)
         plain_bias = keep.tile([P, PROJ * TILES, P], F32)
         par = keep.tile([P, PROJ * CONV_GROUPS, 2, SLOT], F32)
         sums = keep.tile([P, PROJ * CONV_GROUPS, 2, SLOT], F32)
         starts = keep.tile([P, PROJ * CONV_GROUPS, 2, SLOT], F32)
         beta = keep.tile([P, PROJ * CONV_GROUPS, TILES], F32)
-        edge_beta = keep.tile([P, PROJ, TILES, PHASES], F32)
+        edge_beta = keep.tile([P, PROJ * CONV_GROUPS, TILES, PHASES], F32)
         far = [None, None]
         for g in range(2, GROUPS):
             far_g = []
@@ -216,6 +218,10 @@ def tile_tranceptionblockattention_pa_kernel(
             nc.scalar.copy(
                 out=conv_bias[:].rearrange("p (r g) f -> p r (g f)", r=PROJ),
                 in_=bias_ps[:, 0:PROJ * GROUPS * TILES].rearrange("p (r g) -> p r g", r=PROJ)[:, :, TILES:],
+            )
+            nc.scalar.activation(
+                out=minus_bias[:].rearrange("p (r g) f -> p r (g f)", r=PROJ),
+                in_=bias_ps[:, 0:PROJ * GROUPS * TILES].rearrange("p (r g) -> p r g", r=PROJ)[:, :, TILES:], func=COPY, scale=-1.0,
             )
             for first in range(0, PROJ * TILES, 4):
                 n_rows = min(4, PROJ * TILES - first)
@@ -245,30 +251,34 @@ def tile_tranceptionblockattention_pa_kernel(
                 out=sums[:, lo:hi].rearrange("p n k i -> p (n k i)"), data0=starts[:, lo:hi].rearrange("p n k i -> p (n k i)"),
                 data1=par[:, lo:hi].rearrange("p n k i -> p (n k i)"), initial=0.0, op0=MULT, op1=ADD,
             )
-            for n in range(lo, hi):
-                pr, g = divmod(n, CONV_GROUPS)
-                nc.gpsimd.tensor_scalar(
-                    out=beta[:, n], in0=conv_bias[:, n], scalar1=sums[:, n, 0, SLOT - 1:SLOT], scalar2=par[:, n, 1, 0:1],
-                    op0=MULT, op1=ADD,
-                )
-                if g + 1 == 1:
-                    for f in range(TILES):
-                        nc.gpsimd.tensor_scalar(
-                            out=edge_beta[:, pr, f], in0=sums[:, n, 0, 0:PHASES][:, ::-1], scalar1=conv_bias[:, n, f:f + 1],
-                            scalar2=beta[:, n, f:f + 1], op0=MULT, op1=SUB,
-                        )
-                        nc.gpsimd.tensor_scalar(
-                            out=edge_beta[:, pr, f], in0=edge_beta[:, pr, f], scalar1=-1.0, scalar2=0.0, op0=MULT, op1=ADD,
-                        )
+            n = hi - lo
+            nc.gpsimd.tensor_tensor(
+                out=beta[:, lo:hi], in0=conv_bias[:, lo:hi],
+                in1=sums[:, lo:hi, 0, SLOT - 1:SLOT].to_broadcast([P, n, TILES]), op=MULT,
+            )
+            nc.gpsimd.tensor_tensor(
+                out=beta[:, lo:hi], in0=beta[:, lo:hi], in1=par[:, lo:hi, 1, 0:1].to_broadcast([P, n, TILES]), op=ADD,
+            )
+            for ph in range(PHASES):
+                g1 = slice(lo + -lo % CONV_GROUPS, hi, CONV_GROUPS)
+                n_g1 = len(range(lo, hi)[-lo % CONV_GROUPS::CONV_GROUPS])
+                if n_g1 > 0:
+                    nc.gpsimd.tensor_tensor(
+                        out=edge_beta[:, g1, :, ph], in0=minus_bias[:, g1],
+                        in1=sums[:, g1, 0, PHASES - 1 - ph:PHASES - ph].to_broadcast([P, n_g1, TILES]), op=MULT,
+                    )
+                    nc.gpsimd.tensor_tensor(
+                        out=edge_beta[:, g1, :, ph], in0=edge_beta[:, g1, :, ph], in1=beta[:, g1], op=ADD,
+                    )
 
         def correct_edge(pr, g):
             n = block(pr, g)
             u = (TAPS[g] - 1) // PHASES
             missing = sums[:, n, 0, 0:TAPS[g] - 1][:, ::-1].rearrange("p (i a) -> p a i", a=PHASES)
             for f in range(TILES):
-                nc.gpsimd.tensor_scalar(
+                nc.gpsimd.tensor_tensor(
                     out=far[g][f][:, :, :, HALO - u:HALO], in0=missing.unsqueeze(2).to_broadcast([P, PHASES, B, u]),
-                    scalar1=conv_bias[:, n, f:f + 1], scalar2=-1.0, op0=MULT, op1=MULT,
+                    in1=minus_bias[:, n, f:f + 1].unsqueeze(2).unsqueeze(3).to_broadcast([P, PHASES, B, u]), op=MULT,
                 )
 
         def weight(pr, g, t):
@@ -371,7 +381,7 @@ def tile_tranceptionblockattention_pa_kernel(
                 first = 1
                 nc.scalar.activation(
                     out=acc[(n, src)][:, :, 0:first], in_=products(n, src, b)[:, :, 0:first], func=IDENTITY,
-                    scale=weight(pr, g, 0), bias=edge_beta[:, pr, f, src:src + 1],
+                    scale=weight(pr, g, 0), bias=edge_beta[:, block(pr, g), f, src:src + 1],
                 )
             nc.scalar.activation(
                 out=acc[(n, src)][:, entries(b), first:], in_=products(n, src, b)[:, :, first:], func=IDENTITY,
@@ -495,10 +505,10 @@ def tile_tranceptionblockattention_pa_kernel(
                     correct_edge(pr + 1, g)
             if n == 0:
                 spread_parameters(lead + 1, PROJ * CONV_GROUPS)
-            if n + LEAD < n_units:
-                scalar_taps(n + LEAD)
             if n == LEAD - 1:
                 take_parameters(lead + 1, PROJ * CONV_GROUPS)
+            if n + LEAD < n_units:
+                scalar_taps(n + LEAD)
 
         spread_attn_bias()
         first_g = CONV_ORDER[0]

@@ -33,9 +33,9 @@ HALO = 8
 CONV_ORDER = (3, 2, 1)
 LAST_ORDER = (3, 2, 1)
 SCALAR_SIDES = ((2, 2, 2, 1, 1, 0), (2, 2, 2, 1, 1, 0), (2, 2, 2, 1, 1, 0))
-PLAIN_UNITS = ((4, 5, 5, 8), (9, 10, 11, 11), (14, 15, 16, 16))
+PLAIN_UNITS = ((5, 5, 8, 9), (10, 11, 11, 14), (14, 15, 15, 16))
 WG_BUFS = 4
-REGROUP_COLS = 128
+REGROUP_COLS = 256
 LEAD = 2
 
 FLOPS = 2 * B * S * E * PROJ * E + 2 * B * S * PROJ * GROUP_COLS * sum(TAPS[1:])
@@ -75,9 +75,9 @@ def tile_tranceptionblockattention_pa_kernel(
     for pr in range(PROJ):
         first, second, third = LAST_ORDER if pr == PROJ - 1 else CONV_ORDER
         start = pr * n_units // PROJ
-        places = ((start - LEAD, first), (start - 1, second), (start - 1, 0), (start + LEAD, third))
+        places = ((start - LEAD, first), (start - 1, second), (PLAIN_UNITS[pr][0] - LEAD, 0), (start + LEAD, third))
         if pr == 0:
-            places = ((None, first), (0, second), (LEAD, 0), (LEAD, third))
+            places = ((None, first), (0, second), (LEAD, third), (LEAD + 1, 0))
         for n, g in places:
             if n is not None:
                 quantise_at.setdefault(n, []).append(len(group_seq))
@@ -142,11 +142,11 @@ def tile_tranceptionblockattention_pa_kernel(
         for g in CONV_ORDER[1:]:
             load_parameters(0, g)
         load_w(0, CONV_ORDER[1] * GROUP_COLS, GROUP_COLS)
-        load_w(0, 0, GROUP_COLS)
+        load_w(0, CONV_ORDER[2] * GROUP_COLS, GROUP_COLS)
         for pr in range(1, PROJ):
             for g in CONV_ORDER:
                 load_parameters(pr, g)
-        load_w(0, CONV_ORDER[2] * GROUP_COLS, GROUP_COLS)
+        load_w(0, 0, GROUP_COLS)
         load_w(1, 0, E)
         load_w(2, 0, E)
 
@@ -246,29 +246,22 @@ def tile_tranceptionblockattention_pa_kernel(
         def take_parameters(lo, hi):
             nc.scalar.copy(out=par[:, lo:hi].rearrange("p n k i -> p (n k i)"), in_=par_ps[lo][:, 0:(hi - lo) * 2 * SLOT])
 
-        def derive_parameters(lo, hi):
+        def sum_taps(lo, hi):
             nc.vector.tensor_tensor_scan(
                 out=sums[:, lo:hi].rearrange("p n k i -> p (n k i)"), data0=starts[:, lo:hi].rearrange("p n k i -> p (n k i)"),
                 data1=par[:, lo:hi].rearrange("p n k i -> p (n k i)"), initial=0.0, op0=MULT, op1=ADD,
             )
-            n = hi - lo
-            nc.gpsimd.tensor_tensor(
-                out=beta[:, lo:hi], in0=conv_bias[:, lo:hi],
-                in1=sums[:, lo:hi, 0, SLOT - 1:SLOT].to_broadcast([P, n, TILES]), op=MULT,
+
+        def derive_biases(pr, g):
+            n = block(pr, g)
+            nc.scalar.activation(
+                out=beta[:, n], in_=conv_bias[:, n], func=IDENTITY, scale=sums[:, n, 0, SLOT - 1:SLOT], bias=par[:, n, 1, 0:1],
             )
-            nc.gpsimd.tensor_tensor(
-                out=beta[:, lo:hi], in0=beta[:, lo:hi], in1=par[:, lo:hi, 1, 0:1].to_broadcast([P, n, TILES]), op=ADD,
-            )
-            for ph in range(PHASES):
-                g1 = slice(lo + -lo % CONV_GROUPS, hi, CONV_GROUPS)
-                n_g1 = len(range(lo, hi)[-lo % CONV_GROUPS::CONV_GROUPS])
-                if n_g1 > 0:
-                    nc.gpsimd.tensor_tensor(
-                        out=edge_beta[:, g1, :, ph], in0=minus_bias[:, g1],
-                        in1=sums[:, g1, 0, PHASES - 1 - ph:PHASES - ph].to_broadcast([P, n_g1, TILES]), op=MULT,
-                    )
-                    nc.gpsimd.tensor_tensor(
-                        out=edge_beta[:, g1, :, ph], in0=edge_beta[:, g1, :, ph], in1=beta[:, g1], op=ADD,
+            if g == 1:
+                for f in range(TILES):
+                    nc.scalar.activation(
+                        out=edge_beta[:, n, f], in_=sums[:, n, 0, 0:PHASES][:, ::-1], func=IDENTITY,
+                        scale=minus_bias[:, n, f:f + 1], bias=beta[:, n, f:f + 1],
                     )
 
         def correct_edge(pr, g):
@@ -276,9 +269,9 @@ def tile_tranceptionblockattention_pa_kernel(
             u = (TAPS[g] - 1) // PHASES
             missing = sums[:, n, 0, 0:TAPS[g] - 1][:, ::-1].rearrange("p (i a) -> p a i", a=PHASES)
             for f in range(TILES):
-                nc.gpsimd.tensor_tensor(
-                    out=far[g][f][:, :, :, HALO - u:HALO], in0=missing.unsqueeze(2).to_broadcast([P, PHASES, B, u]),
-                    in1=minus_bias[:, n, f:f + 1].unsqueeze(2).unsqueeze(3).to_broadcast([P, PHASES, B, u]), op=MULT,
+                nc.scalar.activation(
+                    out=far[g][f][:, :, :, HALO - u:HALO], in_=missing.unsqueeze(2).to_broadcast([P, PHASES, B, u]), func=COPY,
+                    scale=minus_bias[:, n, f:f + 1],
                 )
 
         def weight(pr, g, t):
@@ -289,6 +282,7 @@ def tile_tranceptionblockattention_pa_kernel(
         for c in range(PASSES):
             x_grouped_c = keep.tile([P, PHASES, B, HALF, PACK], BF16, name="x_grouped%d" % c, align_bytes=64)
             x_grouped.append(x_grouped_c)
+        held = keep.tile([P, 1], U8)
         x_codes = keep.tile([P, PASSES, PHASES, B * HALF], U32, align_bytes=64)
         x_scales = keep.tile([P, PASSES, PHASES, B * HALF], U8, align_bytes=64)
         words = K_PASS // 2
@@ -367,7 +361,9 @@ def tile_tranceptionblockattention_pa_kernel(
                 multiply(0, ph, x_first, b, 1)
 
         def products(n, src, b):
-            return x_ps[(n, src)][:] if b is None else x_ps[(n, src, b)][:]
+            if n == 0:
+                return x_ps[(n, src, b)][:]
+            return x_ps[(n, src)][:, entries(b)]
 
         def entries(b):
             return slice(0, B) if b is None else slice(b, b + 1)
@@ -419,35 +415,55 @@ def tile_tranceptionblockattention_pa_kernel(
                 in1=acc[(n, ph)][:, entries(b), u:], op0=MULT, op1=ADD,
             )
 
+        def transpose_blocks(n, ph, b, out):
+            for blk in range(BLOCKS):
+                parts = [acc[(n, ph)][:, b, blk * P:(blk + 1) * P]]
+                for t, to in sides(n):
+                    if to == ph:
+                        first = HALO + blk * P - source(ph, t)[1]
+                        parts.append(side(n, t, ph)[:, b, first:first + P])
+                for k in range(len(parts)):
+                    nc.tensor.matmul(
+                        out=out[:, blk, :], lhsT=parts[k], rhs=ident_f32[:], is_transpose=True,
+                        start=(k == 0), stop=(k == len(parts) - 1),
+                    )
+
         def transposes(n):
-            pr, g, f = units[n]
             for ph in range(PHASES):
-                y_ps[(n, ph)] = psum.tile([P, B * BLOCKS, P], F32, name="y_b", tag="y")
+                y_ps[(n, ph)] = psum.tile([P, B, BLOCKS, P], F32, name="y_b", tag="y")
                 for b in range(B):
-                    for blk in range(BLOCKS):
-                        parts = [acc[(n, ph)][:, b, blk * P:(blk + 1) * P]]
-                        for t, to in sides(n):
-                            if to == ph:
-                                first = HALO + blk * P - source(ph, t)[1]
-                                parts.append(side(n, t, ph)[:, b, first:first + P])
-                        for k in range(len(parts)):
-                            nc.tensor.matmul(
-                                out=y_ps[(n, ph)][:, b * BLOCKS + blk, :], lhsT=parts[k], rhs=ident_f32[:], is_transpose=True,
-                                start=(k == 0), stop=(k == len(parts) - 1),
-                            )
+                    transpose_blocks(n, ph, b, y_ps[(n, ph)][:, b])
+
+        def store(n, b, o_sb):
+            pr, g, f = units[n]
+            for h in range(HEADS):
+                nc.sync.dma_start(
+                    out=outs[pr][b, (g * TILES + f) * HEADS + h].rearrange("(k p a) d -> p k (a d)", p=P, a=PHASES),
+                    in_=o_sb[:, :, h].rearrange("p k a d -> p k (a d)"),
+                )
 
         def evacuate(n):
-            pr, g, f = units[n]
-            o_sb = out_pool.tile([P, B * BLOCKS, HEADS, PHASES, D], F32, name="o_sb")
+            o_sb = out_pool.tile([P, B, BLOCKS, HEADS, PHASES, D], F32, name="o_sb")
             for ph in range(PHASES):
-                copy_out = nc.vector.tensor_copy if n == n_units - 1 and ph == 1 else nc.scalar.copy
-                copy_out(out=o_sb[:, :, :, ph, :], in_=y_ps[(n, ph)][:].rearrange("p k (h d) -> p k h d", d=D))
+                nc.scalar.copy(
+                    out=o_sb[:, :, :, :, ph, :].rearrange("p b k h d -> p (b k) h d"),
+                    in_=y_ps[(n, ph)][:].rearrange("p b k (h d) -> p (b k) h d", d=D),
+                )
             for b in range(B):
-                for h in range(HEADS):
-                    nc.sync.dma_start(
-                        out=outs[pr][b, (g * TILES + f) * HEADS + h].rearrange("(k p a) d -> p k (a d)", p=P, a=PHASES),
-                        in_=o_sb[:, b * BLOCKS:(b + 1) * BLOCKS, h].rearrange("p k a d -> p k (a d)"),
-                    )
+                store(n, b, o_sb[:, b])
+
+        def finish_last(b):
+            n = n_units - 1
+            o_last = out_pool.tile([P, BLOCKS, HEADS, PHASES, D], F32, name="o_last")
+            for ph in range(PHASES):
+                if b == 0:
+                    y_last = psum.tile([P, BLOCKS, P], F32, name="y_last0", tag="z")
+                else:
+                    y_last = psum.tile([P, BLOCKS, P], F32, name="y_last1", tag="x", bufs=LEAD * PHASES)
+                transpose_blocks(n, ph, b, y_last[:])
+                copy_out = nc.vector.tensor_copy if (b, ph) == (1, 1) else nc.scalar.copy
+                copy_out(out=o_last[:, :, :, ph, :], in_=y_last[:].rearrange("p k (h d) -> p k h d", d=D))
+            store(n, b, o_last[:])
 
         z_ps = {}
 
@@ -484,10 +500,16 @@ def tile_tranceptionblockattention_pa_kernel(
             for j in quantise_at.get(n, []):
                 quantise(j)
 
+        def hold_gpsimd(scales):
+            nc.gpsimd.tensor_copy(out=held[:], in_=scales)
+
         def regroup_for(n):
-            for j in quantise_at.get(n, []):
-                if j + WG_BUFS < len(group_seq):
-                    regroup_on_gpsimd(j + WG_BUFS)
+            coming = [j + 2 for j in quantise_at.get(n, []) if WG_BUFS <= j + 2 < len(group_seq)]
+            if coming:
+                pr, g = group_seq[coming[-1] - 2]
+                hold_gpsimd(w_scales[:, pr * GROUPS + g, PASSES - 1, GROUP_COLS - 1:GROUP_COLS])
+                for j in coming:
+                    regroup_on_gpsimd(j)
 
         def finish_unit(n):
             for k in plain_at.get(n + 1, []):
@@ -501,8 +523,10 @@ def tile_tranceptionblockattention_pa_kernel(
             transposes(n)
             if n >= LEAD:
                 pr, g, f = units[n - LEAD]
-                if g > 1 and f == TILES - 1 and pr + 1 < PROJ:
-                    correct_edge(pr + 1, g)
+                if f == TILES - 1 and pr + 1 < PROJ:
+                    derive_biases(pr + 1, g)
+                    if g > 1:
+                        correct_edge(pr + 1, g)
             if n == 0:
                 spread_parameters(lead + 1, PROJ * CONV_GROUPS)
             if n == LEAD - 1:
@@ -516,8 +540,7 @@ def tile_tranceptionblockattention_pa_kernel(
         spread_parameters(lead, lead + 1)
         take_parameters(lead, lead + 1)
         prepare_first_group(0)
-        derive_parameters(lead, lead + 1)
-        correct_edge(0, first_g)
+        sum_taps(lead, lead + 1)
         copies = (nc.scalar.copy, nc.scalar.copy)
         transpose_x(0, 0, copies)
         quantise_first_group(0)
@@ -528,13 +551,17 @@ def tile_tranceptionblockattention_pa_kernel(
         quantise_first_group(1)
         transpose_x(0, 1, (nc.vector.tensor_copy, nc.vector.tensor_copy))
         quantise_x(0, 1)
+        derive_biases(0, first_g)
+        correct_edge(0, first_g)
         project_first(0)
         for src in range(PHASES):
             first_tap(0, src, 0)
         transpose_x(1, 1, copies)
         vector_taps(0, 0, 0)
         quantise_x(1, 1)
-        regroup_on_gpsimd(1)
+        hold_gpsimd(x_scales[:, PASSES - 1, PHASES - 1, B * HALF - 1:B * HALF])
+        for j in range(1, WG_BUFS):
+            regroup_on_gpsimd(j)
         vector_taps(0, 1, 0)
         project_first(1)
         project(1)
@@ -546,23 +573,26 @@ def tile_tranceptionblockattention_pa_kernel(
         take_parameters(0, lead)
         scalar_taps(1)
         vector_taps(0, 0, 1)
-        derive_parameters(0, lead)
-        correct_edge(0, 2)
-        for j in range(2, WG_BUFS + 1):
-            regroup_on_gpsimd(j)
-        quantise_for(0)
-        regroup_for(0)
+        sum_taps(0, lead)
         vector_taps(0, 1, 1)
+        quantise_for(0)
         for src in range(PHASES):
             scalar_sides(0, src, 1)
+        for g in (2, 1):
+            derive_biases(0, g)
+        correct_edge(0, 2)
         finish_unit(0)
 
-        for n in range(1, n_units):
+        for n in range(1, n_units - 1):
             vector_taps(n, 0)
             quantise_for(n)
             vector_taps(n, 1)
             if n == LEAD:
-                derive_parameters(lead + 1, PROJ * CONV_GROUPS)
+                sum_taps(lead + 1, PROJ * CONV_GROUPS)
             regroup_for(n)
             finish_unit(n)
-        evacuate(n_units - 1)
+        evacuate(n_units - 2)
+        for b in range(B):
+            for src in range(PHASES):
+                vector_taps(n_units - 1, src, b)
+            finish_last(b)

@@ -35,7 +35,7 @@ LAST_ORDER = (3, 2, 1)
 SCALAR_SIDES = ((2, 2, 2, 1, 1, 0), (2, 2, 2, 1, 1, 0), (2, 2, 2, 1, 1, 0))
 PLAIN_UNITS = ((5, 5, 8, 9), (10, 11, 11, 14), (14, 15, 15, 16))
 WG_BUFS = 4
-REGROUP_COLS = 256
+REGROUP_AFTER = {1: (2, 3), 2: (4,), 4: (5,), 5: (6, 7, 8), 7: (9,), 8: (10,), 9: (11,)}
 LEAD = 2
 
 FLOPS = 2 * B * S * E * PROJ * E + 2 * B * S * PROJ * GROUP_COLS * sum(TAPS[1:])
@@ -97,7 +97,7 @@ def tile_tranceptionblockattention_pa_kernel(
         ident_f32 = keep.tile([P, P], F32)
         make_identity(nc, ident_f32[:])
         ident_bf = keep.tile([P, P], BF16)
-        make_identity(nc, ident_bf[:])
+        nc.vector.tensor_copy(out=ident_bf[:], in_=ident_f32[:])
         twice = keep.tile([P, 2, D], BF16)
         nc.vector.tensor_copy(out=twice[:], in_=ident_bf[:, 0:D].unsqueeze(1).to_broadcast([P, 2, D]))
 
@@ -173,13 +173,10 @@ def tile_tranceptionblockattention_pa_kernel(
         def regroup_on_gpsimd(j):
             pr, g = group_seq[j]
             wg[j] = wg_pool.tile([P, PASSES, GROUP_COLS, PACK], BF16, name="wg", align_bytes=64)
-            for c in range(PASSES):
-                for first in range(0, GROUP_COLS, REGROUP_COLS):
-                    cols = slice(g * GROUP_COLS + first, g * GROUP_COLS + first + REGROUP_COLS)
-                    nc.gpsimd.tensor_scalar(
-                        out=wg[j][:, c, first:first + REGROUP_COLS], in0=w_raw[pr][:, c, :, cols].rearrange("p j n -> p n j"),
-                        scalar1=1.0, scalar2=0.0, op0=MULT, op1=ADD,
-                    )
+            nc.gpsimd.tensor_scalar(
+                out=wg[j][:], in0=w_raw[pr][:, :, :, g * GROUP_COLS:(g + 1) * GROUP_COLS].rearrange("p c j n -> p c n j"),
+                scalar1=1.0, scalar2=0.0, op0=MULT, op1=ADD,
+            )
 
         def quantise(j):
             pr, g = group_seq[j]
@@ -504,12 +501,12 @@ def tile_tranceptionblockattention_pa_kernel(
             nc.gpsimd.tensor_copy(out=held[:], in_=scales)
 
         def regroup_for(n):
-            coming = [j + 2 for j in quantise_at.get(n, []) if WG_BUFS <= j + 2 < len(group_seq)]
-            if coming:
-                pr, g = group_seq[coming[-1] - 2]
-                hold_gpsimd(w_scales[:, pr * GROUPS + g, PASSES - 1, GROUP_COLS - 1:GROUP_COLS])
-                for j in coming:
-                    regroup_on_gpsimd(j)
+            for j in quantise_at.get(n, []):
+                if j in REGROUP_AFTER:
+                    pr, g = group_seq[j]
+                    hold_gpsimd(w_scales[:, pr * GROUPS + g, PASSES - 1, GROUP_COLS - 1:GROUP_COLS])
+                    for coming in REGROUP_AFTER[j]:
+                        regroup_on_gpsimd(coming)
 
         def finish_unit(n):
             for k in plain_at.get(n + 1, []):
@@ -560,22 +557,22 @@ def tile_tranceptionblockattention_pa_kernel(
         vector_taps(0, 0, 0)
         quantise_x(1, 1)
         hold_gpsimd(x_scales[:, PASSES - 1, PHASES - 1, B * HALF - 1:B * HALF])
-        for j in range(1, WG_BUFS):
-            regroup_on_gpsimd(j)
+        regroup_on_gpsimd(1)
         vector_taps(0, 1, 0)
+        spread_parameters(0, lead)
         project_first(1)
         project(1)
-        spread_parameters(0, lead)
         for src in range(PHASES):
             first_tap(0, src, 1)
+        take_parameters(0, lead)
         for src in range(PHASES):
             scalar_sides(0, src, 0)
-        take_parameters(0, lead)
         scalar_taps(1)
         vector_taps(0, 0, 1)
-        sum_taps(0, lead)
         vector_taps(0, 1, 1)
+        sum_taps(0, lead)
         quantise_for(0)
+        regroup_for(0)
         for src in range(PHASES):
             scalar_sides(0, src, 1)
         for g in (2, 1):
@@ -585,8 +582,8 @@ def tile_tranceptionblockattention_pa_kernel(
 
         for n in range(1, n_units - 1):
             vector_taps(n, 0)
-            quantise_for(n)
             vector_taps(n, 1)
+            quantise_for(n)
             if n == LEAD:
                 sum_taps(lead + 1, PROJ * CONV_GROUPS)
             regroup_for(n)

@@ -317,9 +317,11 @@ def tile_tranceptionblockattention_pa_kernel(
             return src, (t + src - ph) // PHASES
 
         def side_taps(n):
-            place = n % (n_units // PROJ)
-            n_taps = TAPS[units[n][1]]
-            return range(n_taps - SCALAR_SIDES[units[n][0]][place], n_taps)
+            g = units[n][1]
+            count = SCALAR_SIDES[units[n][0]][n % (n_units // PROJ)]
+            if g == 1:
+                return list(range(1, 1 + count))
+            return [TAPS[g] - 1] + list(range(1, count))
 
         def sides(n):
             return [(t, ph) for t in side_taps(n) for ph in range(PHASES)]
@@ -394,23 +396,31 @@ def tile_tranceptionblockattention_pa_kernel(
                 first_tap(n, src)
                 scalar_sides(n, src)
 
+        def partial_sum(n, ph, t, b, u):
+            if t == 0:
+                return acc[(n, ph)][:, entries(b), u:]
+            shift = source(ph, t)[1]
+            return side(n, t, ph)[:, entries(b), HALO + u - shift:HALO + HALF - shift]
+
         def vector_taps(n, src, b=None):
             pr, g, f = units[n]
-            by_phase = [
-                [t for t in range(1, TAPS[g]) if source(ph, t)[0] == src and (t, ph) not in sides(n)] for ph in range(PHASES)]
-            order = (1, 0) if len(by_phase[1]) > len(by_phase[0]) else (0, 1)
-            for i in range(max(len(taps) for taps in by_phase)):
+            begun = [[0] + side_taps(n) if n > 0 else [0] for ph in range(PHASES)]
+            taps = []
+            for ph in range(PHASES):
+                sums = [t for t in begun[ph] if source(ph, t)[0] == src] or begun[ph]
+                others = [t for t in range(1, TAPS[g]) if source(ph, t)[0] == src and (t, ph) not in sides(n)]
+                taps.append([(t, ph, sums[i % len(sums)]) for i, t in enumerate(others)])
+            order = (1 - src, src) if n > 0 and (len(taps[0]) != len(taps[1]) or 1 in side_taps(n)) else (0, 1)
+            for i in range(max(len(taps[0]), len(taps[1]))):
                 for ph in order:
-                    if i < len(by_phase[ph]):
-                        vector_tap(n, by_phase[ph][i], ph, b)
-
-        def vector_tap(n, t, ph, b):
-            pr, g, f = units[n]
-            src, u = source(ph, t)
-            nc.vector.scalar_tensor_tensor(
-                out=acc[(n, ph)][:, entries(b), u:], in0=products(n, src, b)[:, :, 0:HALF - u], scalar=weight(pr, g, t),
-                in1=acc[(n, ph)][:, entries(b), u:], op0=MULT, op1=ADD,
-            )
+                    if i < len(taps[ph]):
+                        t, ph, begin = taps[ph][i]
+                        u = source(ph, t)[1]
+                        total = partial_sum(n, ph, begin, b, u)
+                        nc.vector.scalar_tensor_tensor(
+                            out=total, in0=products(n, src, b)[:, :, 0:HALF - u], scalar=weight(pr, g, t), in1=total,
+                            op0=MULT, op1=ADD,
+                        )
 
         def transpose_blocks(n, ph, b, out):
             for blk in range(BLOCKS):

@@ -35,6 +35,8 @@ LAST_ORDER = (3, 2, 1)
 SCALAR_SIDES = ((2, 2, 2, 1, 1, 0), (2, 2, 2, 1, 1, 0), (2, 2, 2, 1, 1, 0))
 PLAIN_UNITS = ((5, 5, 8, 9), (10, 11, 11, 14), (14, 15, 15, 16))
 WG_BUFS = 4
+WARM_UP = 20
+Y_BANKS = 4
 REGROUP_AFTER = {1: (2, 3), 2: (4,), 4: (5,), 5: (6, 7, 8), 7: (9,), 8: (10,), 9: (11,)}
 LEAD = 2
 
@@ -210,7 +212,7 @@ def tile_tranceptionblockattention_pa_kernel(
         nc.vector.memset(starts[:, :, :, 0:1], 0.0)
 
         def spread_attn_bias():
-            bias_ps = psum.tile([P, P], F32, name="bias_ps", tag="z")
+            bias_ps = psum.tile([P, P], F32, name="bias_ps", tag="y", bufs=Y_BANKS)
             nc.tensor.matmul(out=bias_ps[:], lhsT=bias_rows[:], rhs=ident_bf[:], start=True, stop=True)
             nc.scalar.copy(
                 out=conv_bias[:].rearrange("p (r g) f -> p r (g f)", r=PROJ),
@@ -222,7 +224,7 @@ def tile_tranceptionblockattention_pa_kernel(
             )
             for first in range(0, PROJ * TILES, 4):
                 n_rows = min(4, PROJ * TILES - first)
-                rows_ps = psum.tile([P, 4, P], F32, name="rows_ps", tag="z")
+                rows_ps = psum.tile([P, 4, P], F32, name="rows_ps", tag="y", bufs=Y_BANKS)
                 for i in range(n_rows):
                     r = ((first + i) // TILES) * GROUPS * TILES + (first + i) % TILES
                     nc.tensor.matmul(
@@ -234,7 +236,7 @@ def tile_tranceptionblockattention_pa_kernel(
         par_ps = {}
 
         def spread_parameters(lo, hi):
-            par_ps[lo] = psum.tile([P, PROJ * CONV_GROUPS * 2 * SLOT], F32, name="par_b", tag="z")
+            par_ps[lo] = psum.tile([P, PROJ * CONV_GROUPS * 2 * SLOT], F32, name="par_b", tag="y", bufs=Y_BANKS)
             nc.tensor.matmul(
                 out=par_ps[lo][:, 0:(hi - lo) * 2 * SLOT], lhsT=twice[:].rearrange("p a d -> p (a d)"),
                 rhs=par_in[:, lo:hi].rearrange("p n k i -> p (n k i)"), start=True, stop=True,
@@ -288,7 +290,7 @@ def tile_tranceptionblockattention_pa_kernel(
             last = (ph, b) == (PHASES - 1, B - 1)
             for c in range(PASSES):
                 if last:
-                    xt = psum.tile([P, BLOCKS, 2, P], F32, name="xt_last", tag="y")
+                    xt = psum.tile([P, BLOCKS, 2, P], F32, name="xt_last", tag="y", bufs=Y_BANKS)
                 else:
                     xt = psum.tile([P, BLOCKS, 2, P], F32, name="xt", tag="x", bufs=LEAD * PHASES)
                 for blk in range(BLOCKS):
@@ -355,7 +357,7 @@ def tile_tranceptionblockattention_pa_kernel(
                 if b == 0:
                     x_first = psum.tile([P, 1, HALF], F32, name="x_first0", tag="x", bufs=LEAD * PHASES)
                 else:
-                    x_first = psum.tile([P, 1, HALF], F32, name="x_first1", tag="y")
+                    x_first = psum.tile([P, 1, HALF], F32, name="x_first1", tag="y", bufs=Y_BANKS)
                 x_ps[(0, ph, b)] = x_first
                 multiply(0, ph, x_first, b, 1)
 
@@ -431,45 +433,46 @@ def tile_tranceptionblockattention_pa_kernel(
                         parts.append(side(n, t, ph)[:, b, first:first + P])
                 for k in range(len(parts)):
                     nc.tensor.matmul(
-                        out=out[:, blk, :], lhsT=parts[k], rhs=ident_f32[:], is_transpose=True,
+                        out=out[:, :, blk, :], lhsT=parts[k], rhs=ident_f32[:].rearrange("p (h d) -> p h d", d=D), is_transpose=True,
                         start=(k == 0), stop=(k == len(parts) - 1),
                     )
 
         def transposes(n):
             for ph in range(PHASES):
-                y_ps[(n, ph)] = psum.tile([P, B, BLOCKS, P], F32, name="y_b", tag="y")
+                y_ps[(n, ph)] = psum.tile([P, B, HEADS, BLOCKS, D], F32, name="y_b", tag="y", bufs=Y_BANKS)
                 for b in range(B):
                     transpose_blocks(n, ph, b, y_ps[(n, ph)][:, b])
 
         def store(n, b, o_sb):
             pr, g, f = units[n]
-            for h in range(HEADS):
-                nc.sync.dma_start(
-                    out=outs[pr][b, (g * TILES + f) * HEADS + h].rearrange("(k p a) d -> p k (a d)", p=P, a=PHASES),
-                    in_=o_sb[:, :, h].rearrange("p k a d -> p k (a d)"),
-                )
+            first = (g * TILES + f) * HEADS
+            nc.sync.dma_start(
+                out=outs[pr][b, first:first + HEADS].rearrange("h (k p a) d -> p (h k) (a d)", p=P, a=PHASES),
+                in_=o_sb.rearrange("p h k a d -> p (h k) (a d)"),
+            )
 
         def evacuate(n):
-            o_sb = out_pool.tile([P, B, BLOCKS, HEADS, PHASES, D], F32, name="o_sb")
+            o_sb = out_pool.tile([P, B, HEADS, BLOCKS, PHASES, D], F32, name="o_sb")
             for ph in range(PHASES):
                 nc.scalar.copy(
-                    out=o_sb[:, :, :, :, ph, :].rearrange("p b k h d -> p (b k) h d"),
-                    in_=y_ps[(n, ph)][:].rearrange("p b k (h d) -> p (b k) h d", d=D),
+                    out=o_sb[:, :, :, :, ph, :].rearrange("p b h k d -> p (b h k) d"),
+                    in_=y_ps[(n, ph)][:].rearrange("p b h k d -> p (b h k) d"),
                 )
             for b in range(B):
                 store(n, b, o_sb[:, b])
 
         def finish_last(b):
             n = n_units - 1
-            o_last = out_pool.tile([P, BLOCKS, HEADS, PHASES, D], F32, name="o_last")
+            o_last = out_pool.tile([P, HEADS, BLOCKS, PHASES, D], F32, name="o_last")
             for ph in range(PHASES):
                 if b == 0:
-                    y_last = psum.tile([P, BLOCKS, P], F32, name="y_last0", tag="z")
+                    y_last = psum.tile([P, HEADS, BLOCKS, D], F32, name="y_last0", tag="y", bufs=Y_BANKS)
                 else:
-                    y_last = psum.tile([P, BLOCKS, P], F32, name="y_last1", tag="x", bufs=LEAD * PHASES)
+                    y_last = psum.tile([P, HEADS, BLOCKS, D], F32, name="y_last1", tag="x", bufs=LEAD * PHASES)
                 transpose_blocks(n, ph, b, y_last[:])
                 copy_out = nc.vector.tensor_copy if (b, ph) == (1, 1) else nc.scalar.copy
-                copy_out(out=o_last[:, :, :, ph, :], in_=y_last[:].rearrange("p k (h d) -> p k h d", d=D))
+                copy_out(
+                    out=o_last[:, :, :, ph, :].rearrange("p h k d -> p (h k) d"), in_=y_last[:].rearrange("p h k d -> p (h k) d"))
             store(n, b, o_last[:])
 
         z_ps = {}
@@ -477,7 +480,7 @@ def tile_tranceptionblockattention_pa_kernel(
         def project_plain(k):
             pr, b, blk = plain_units[k]
             pg = pr * GROUPS
-            z_ps[k] = psum.tile([P, PHASES, GROUP_COLS], F32, name="z_b", tag="z")
+            z_ps[k] = psum.tile([P, PHASES, GROUP_COLS], F32, name="z_b", tag="y", bufs=Y_BANKS)
             first = b * HALF + blk * P
             for ph in range(PHASES):
                 for c in range(PASSES):
@@ -541,6 +544,10 @@ def tile_tranceptionblockattention_pa_kernel(
             if n + LEAD < n_units:
                 scalar_taps(n + LEAD)
 
+        for i in range(WARM_UP):
+            if i % 4 == 0:
+                warm_ps = psum.tile([P, 4, P], F32, name="warm_ps", tag="y", bufs=Y_BANKS)
+            nc.tensor.matmul(out=warm_ps[:, i % 4, :], lhsT=ident_bf[:], rhs=ident_bf[:], start=True, stop=True)
         spread_attn_bias()
         first_g = CONV_ORDER[0]
         lead = block(0, first_g)

@@ -563,7 +563,7 @@ def tile_tranceptionblockattention_pa_kernel(
         prepare_first_group(1)
         quantise_x(1, 0)
         quantise_first_group(1)
-        transpose_x(0, 1, (nc.vector.tensor_copy, nc.vector.tensor_copy))
+        transpose_x(0, 1, (nc.scalar.copy, nc.vector.tensor_copy))
         quantise_x(0, 1)
         derive_biases(0, first_g)
         correct_edge(0, first_g)

import concourse.mybir as mybir
from concourse.masks import make_identity

F32 = mybir.dt.float32
BF16 = mybir.dt.bfloat16
U32 = mybir.dt.uint32
U8 = mybir.dt.uint8
FP8X4 = mybir.dt.float8_e4m3fn_x4
ADD = mybir.AluOpType.add
MULT = mybir.AluOpType.mult
IDENTITY = mybir.ActivationFunctionType.Identity
COPY = mybir.ActivationFunctionType.Copy

P = 128
PACK = 4
PAIR = 2
WORDS = PACK // PAIR
K_PASS = P * PACK
B, S, E, D = 2, 512, 1024, 64
PASSES = E // K_PASS
PROJ = 3
GROUPS = 4
TAPS = (1, 3, 5, 7)
CONV_GROUPS = GROUPS - 1
GROUP_COLS = E // GROUPS
TILES = GROUP_COLS // P
PHASES = 2
HALF = S // PHASES
BLOCKS = HALF // P
HEADS = P // D
SLOT = 16
HALO = 8
CONV_ORDER = (3, 2, 1)
LAST_ORDER = (3, 2, 1)
SCALAR_SIDES = ((2, 2, 2, 1, 1, 0), (2, 2, 2, 1, 1, 0), (2, 2, 2, 1, 1, 0))
PLAIN_UNITS = ((5, 5, 8, 9), (10, 11, 11, 14), (14, 15, 15, 16))
WG_BUFS = 4
WARM_UP = 20
Y_BANKS = 4
REGROUP_AFTER = {1: (2, 3), 2: (4,), 4: (5,), 5: (6, 7, 8), 7: (9,), 8: (10,), 9: (11,)}
LEAD = 2

FLOPS = 2 * B * S * E * PROJ * E + 2 * B * S * PROJ * GROUP_COLS * sum(TAPS[1:])


def tile_tranceptionblockattention_pa_kernel(
    tc, hidden_states, c_attn_w, c_attn_b,
    qw3, qb3, qw5, qb5, qw7, qb7,
    kw3, kb3, kw5, kb5, kw7, kb7,
    vw3, vb3, vw5, vb5, vw7, vb7,
    out_0, out_1, out_2,
):
    nc = tc.nc
    conv_w = ((qw3, qw5, qw7), (kw3, kw5, kw7), (vw3, vw5, vw7))
    conv_b = ((qb3, qb5, qb7), (kb3, kb5, kb7), (vb3, vb5, vb7))
    outs = (out_0, out_1, out_2)

    units = []
    for pr in range(PROJ):
        for g in (LAST_ORDER if pr == PROJ - 1 else CONV_ORDER):
            for f in range(TILES):
                units.append((pr, g, f))
    n_units = len(units)
    plain_units = []
    for pr in range(PROJ):
        for b in range(B):
            for blk in range(BLOCKS):
                plain_units.append((pr, b, blk))
    plain_units_done = []
    plain_at = {}
    for pr in range(PROJ):
        for n in PLAIN_UNITS[pr]:
            plain_at.setdefault(n, []).append(len(plain_units_done))
            plain_units_done.append(n)
    group_seq = []
    quantise_at = {}
    for pr in range(PROJ):
        first, second, third = LAST_ORDER if pr == PROJ - 1 else CONV_ORDER
        start = pr * n_units // PROJ
        places = ((start - LEAD, first), (start - 1, second), (PLAIN_UNITS[pr][0] - LEAD, 0), (start + LEAD, third))
        if pr == 0:
            places = ((None, first), (0, second), (LEAD, third), (LEAD + 1, 0))
        for n, g in places:
            if n is not None:
                quantise_at.setdefault(n, []).append(len(group_seq))
            group_seq.append((pr, g))

    with tc.tile_pool(name="keep", bufs=1) as keep, \
            tc.tile_pool(name="wg_pool", bufs=WG_BUFS) as wg_pool, \
            tc.tile_pool(name="acc_pool", bufs=6) as acc_pool, \
            tc.tile_pool(name="out_pool", bufs=5) as out_pool, \
            tc.psum_pool(name="psum", bufs=2) as psum, \
            tc.manual_schedule():

        bias_rows = keep.tile([P, P], BF16)
        nc.vector.memset(bias_rows[:], 0.0)
        par_in = keep.tile([P, PROJ * CONV_GROUPS, 2, SLOT], BF16)
        nc.vector.memset(par_in[:], 0.0)
        ident_f32 = keep.tile([P, P], F32)
        make_identity(nc, ident_f32[:])
        ident_bf = keep.tile([P, P], BF16)
        nc.vector.tensor_copy(out=ident_bf[:], in_=ident_f32[:])
        twice = keep.tile([P, 2, D], BF16)
        nc.vector.tensor_copy(out=twice[:], in_=ident_bf[:, 0:D].unsqueeze(1).to_broadcast([P, 2, D]))

        def block(pr, g):
            return pr * CONV_GROUPS + g - 1

        def load_parameters(pr, g):
            nc.sync.dma_start(out=par_in[0:D, block(pr, g), 0, 0:TAPS[g]], in_=conv_w[pr][g - 1])
            nc.sync.dma_start(out=par_in[0:D, block(pr, g), 1, 0:1], in_=conv_b[pr][g - 1].rearrange("(d o) -> d o", o=1))

        w_raw = []
        for pr in range(PROJ):
            w_raw_pr = keep.tile([P, PASSES, PACK, E], BF16, name="w_raw%d" % pr)
            w_raw.append(w_raw_pr)

        def load_w(pr, first_col, n_cols, passes=range(PASSES)):
            for c in passes:
                for u in range(WORDS):
                    first_row = c * K_PASS + u * K_PASS // WORDS
                    nc.sync.dma_start(
                        out=w_raw[pr][:, c, u * PAIR:(u + 1) * PAIR, first_col:first_col + n_cols],
                        in_=c_attn_w[first_row:first_row + K_PASS // WORDS, pr * E + first_col:pr * E + first_col + n_cols]
                        .rearrange("(p e) n -> p e n", e=PAIR),
                    )

        def load_x(ph, b):
            nc.sync.dma_start(
                out=x_raw[:, ph, b],
                in_=hidden_states[b].rearrange("(k p a) e -> p a k e", p=P, a=PHASES)[:, ph],
            )

        x_raw = keep.tile([P, PHASES, B, BLOCKS, E], BF16)
        first_col = CONV_ORDER[0] * GROUP_COLS
        load_w(0, first_col, GROUP_COLS, (0,))
        nc.sync.dma_start(out=bias_rows[0:PROJ * E // P, :], in_=c_attn_b.rearrange("(n m) -> n m", m=P))
        load_parameters(0, CONV_ORDER[0])
        load_x(0, 0)
        load_x(1, 0)
        load_w(0, first_col, GROUP_COLS, (1,))
        load_x(0, 1)
        load_x(1, 1)
        for g in CONV_ORDER[1:]:
            load_parameters(0, g)
        load_w(0, CONV_ORDER[1] * GROUP_COLS, GROUP_COLS)
        load_w(0, CONV_ORDER[2] * GROUP_COLS, GROUP_COLS)
        for pr in range(1, PROJ):
            for g in CONV_ORDER:
                load_parameters(pr, g)
        load_w(0, 0, GROUP_COLS)
        load_w(1, 0, E)
        load_w(2, 0, E)

        w_codes = keep.tile([P, PROJ * GROUPS, PASSES, GROUP_COLS], U32, align_bytes=64)
        w_scales = keep.tile([P, PROJ * GROUPS, PASSES, GROUP_COLS], U8, align_bytes=64)
        wg = {}

        def prepare_first_group(c):
            pr, g = group_seq[0]
            if c == 0:
                wg[0] = wg_pool.tile([P, PASSES, GROUP_COLS, PACK], BF16, name="wg", align_bytes=64)
            nc.vector.tensor_copy(
                out=wg[0][:, c].rearrange("p (n i) j -> p n j i", i=4),
                in_=w_raw[pr][:, c, :, g * GROUP_COLS:(g + 1) * GROUP_COLS].rearrange("p j (n i) -> p n j i", i=4),
            )

        def quantise_first_group(c):
            pr, g = group_seq[0]
            nc.vector.quantize_mx(
                out=w_codes[:, pr * GROUPS + g, c].bitcast(FP8X4), scales=w_scales[:, pr * GROUPS + g, c],
                in_=wg[0][:, c].rearrange("p n j -> p (n j)"),
            )

        def regroup_on_gpsimd(j):
            pr, g = group_seq[j]
            wg[j] = wg_pool.tile([P, PASSES, GROUP_COLS, PACK], BF16, name="wg", align_bytes=64)
            nc.gpsimd.tensor_scalar(
                out=wg[j][:], in0=w_raw[pr][:, :, :, g * GROUP_COLS:(g + 1) * GROUP_COLS].rearrange("p c j n -> p c n j"),
                scalar1=1.0, scalar2=0.0, op0=MULT, op1=ADD,
            )

        def quantise(j):
            pr, g = group_seq[j]
            nc.vector.quantize_mx(
                out=w_codes[:, pr * GROUPS + g].rearrange("p c n -> p (c n)").bitcast(FP8X4),
                scales=w_scales[:, pr * GROUPS + g].rearrange("p c n -> p (c n)"),
                in_=wg[j][:].rearrange("p c n j -> p (c n j)"),
            )

        minus_bias = keep.tile([P, PROJ * CONV_GROUPS, TILES], F32)
        conv_bias = keep.tile([P, PROJ * CONV_GROUPS, TILES], F32)
        plain_bias = keep.tile([P, PROJ * TILES, P], F32)
        par = keep.tile([P, PROJ * CONV_GROUPS, 2, SLOT], F32)
        sums = keep.tile([P, PROJ * CONV_GROUPS, 2, SLOT], F32)
        starts = keep.tile([P, PROJ * CONV_GROUPS, 2, SLOT], F32)
        beta = keep.tile([P, PROJ * CONV_GROUPS, TILES], F32)
        edge_beta = keep.tile([P, PROJ * CONV_GROUPS, TILES, PHASES], F32)
        far = [None, None]
        for g in range(2, GROUPS):
            far_g = []
            for f in range(TILES):
                far_gf = keep.tile([P, PHASES, B, HALO + HALF], F32, name="far%d%d" % (g, f))
                far_g.append(far_gf)
            far.append(far_g)
        near = []
        for i in range(2 * LEAD):
            near_i = keep.tile([P, PHASES, B, HALO + HALF], F32, name="near%d" % i)
            near.append(near_i)
            nc.vector.memset(near_i[:, :, :, 0:HALO], 0.0)
        nc.vector.memset(starts[:], 1.0)
        nc.vector.memset(starts[:, :, :, 0:1], 0.0)

        def spread_attn_bias():
            bias_ps = psum.tile([P, P], F32, name="bias_ps", tag="y", bufs=Y_BANKS)
            nc.tensor.matmul(out=bias_ps[:], lhsT=bias_rows[:], rhs=ident_bf[:], start=True, stop=True)
            nc.scalar.copy(
                out=conv_bias[:].rearrange("p (r g) f -> p r (g f)", r=PROJ),
                in_=bias_ps[:, 0:PROJ * GROUPS * TILES].rearrange("p (r g) -> p r g", r=PROJ)[:, :, TILES:],
            )
            nc.scalar.activation(
                out=minus_bias[:].rearrange("p (r g) f -> p r (g f)", r=PROJ),
                in_=bias_ps[:, 0:PROJ * GROUPS * TILES].rearrange("p (r g) -> p r g", r=PROJ)[:, :, TILES:], func=COPY, scale=-1.0,
            )
            for first in range(0, PROJ * TILES, 4):
                n_rows = min(4, PROJ * TILES - first)
                rows_ps = psum.tile([P, 4, P], F32, name="rows_ps", tag="y", bufs=Y_BANKS)
                for i in range(n_rows):
                    r = ((first + i) // TILES) * GROUPS * TILES + (first + i) % TILES
                    nc.tensor.matmul(
                        out=rows_ps[:, i, :], lhsT=ident_bf[:, r:r + 1].to_broadcast([P, P]), rhs=bias_rows[:],
                        start=True, stop=True,
                    )
                nc.scalar.copy(out=plain_bias[:, first:first + n_rows, :], in_=rows_ps[:, 0:n_rows, :])

        par_ps = {}

        def spread_parameters(lo, hi):
            par_ps[lo] = psum.tile([P, PROJ * CONV_GROUPS * 2 * SLOT], F32, name="par_b", tag="y", bufs=Y_BANKS)
            nc.tensor.matmul(
                out=par_ps[lo][:, 0:(hi - lo) * 2 * SLOT], lhsT=twice[:].rearrange("p a d -> p (a d)"),
                rhs=par_in[:, lo:hi].rearrange("p n k i -> p (n k i)"), start=True, stop=True,
            )

        def take_parameters(lo, hi):
            nc.scalar.copy(out=par[:, lo:hi].rearrange("p n k i -> p (n k i)"), in_=par_ps[lo][:, 0:(hi - lo) * 2 * SLOT])

        def sum_taps(lo, hi):
            nc.vector.tensor_tensor_scan(
                out=sums[:, lo:hi].rearrange("p n k i -> p (n k i)"), data0=starts[:, lo:hi].rearrange("p n k i -> p (n k i)"),
                data1=par[:, lo:hi].rearrange("p n k i -> p (n k i)"), initial=0.0, op0=MULT, op1=ADD,
            )

        def derive_biases(pr, g):
            n = block(pr, g)
            nc.scalar.activation(
                out=beta[:, n], in_=conv_bias[:, n], func=IDENTITY, scale=sums[:, n, 0, SLOT - 1:SLOT], bias=par[:, n, 1, 0:1],
            )
            if g == 1:
                for f in range(TILES):
                    nc.scalar.activation(
                        out=edge_beta[:, n, f], in_=sums[:, n, 0, 0:PHASES][:, ::-1], func=IDENTITY,
                        scale=minus_bias[:, n, f:f + 1], bias=beta[:, n, f:f + 1],
                    )

        def correct_edge(pr, g):
            n = block(pr, g)
            u = (TAPS[g] - 1) // PHASES
            missing = sums[:, n, 0, 0:TAPS[g] - 1][:, ::-1].rearrange("p (i a) -> p a i", a=PHASES)
            for f in range(TILES):
                nc.scalar.activation(
                    out=far[g][f][:, :, :, HALO - u:HALO], in_=missing.unsqueeze(2).to_broadcast([P, PHASES, B, u]), func=COPY,
                    scale=minus_bias[:, n, f:f + 1],
                )

        def weight(pr, g, t):
            return par[:, block(pr, g), 0, TAPS[g] - 1 - t:TAPS[g] - t]

        x_words = x_raw[:].bitcast(F32)
        x_grouped = []
        for c in range(PASSES):
            x_grouped_c = keep.tile([P, PHASES, B, HALF, PACK], BF16, name="x_grouped%d" % c, align_bytes=64)
            x_grouped.append(x_grouped_c)
        held = keep.tile([P, 1], U8)
        x_codes = keep.tile([P, PASSES, PHASES, B * HALF], U32, align_bytes=64)
        x_scales = keep.tile([P, PASSES, PHASES, B * HALF], U8, align_bytes=64)
        words = K_PASS // 2

        def transpose_x(ph, b, copy_out):
            last = (ph, b) == (PHASES - 1, B - 1)
            for c in range(PASSES):
                if last:
                    xt = psum.tile([P, BLOCKS, 2, P], F32, name="xt_last", tag="y", bufs=Y_BANKS)
                else:
                    xt = psum.tile([P, BLOCKS, 2, P], F32, name="xt", tag="x", bufs=LEAD * PHASES)
                for blk in range(BLOCKS):
                    for u in range(2):
                        nc.tensor.transpose(
                            xt[:, blk, u, :], x_words[:, ph, b, blk, c * words + u * P:c * words + (u + 1) * P], ident_f32[:])
                copy_out[c](
                    out=x_grouped[c][:].bitcast(F32)[:, ph, b].rearrange("p (k t) u -> p k t u", t=P),
                    in_=xt[:].rearrange("p k u t -> p k t u"),
                )

        def quantise_x(ph, b):
            for c in range(PASSES):
                nc.vector.quantize_mx(
                    out=x_codes[:, c, ph, b * HALF:(b + 1) * HALF].bitcast(FP8X4),
                    scales=x_scales[:, c, ph, b * HALF:(b + 1) * HALF],
                    in_=x_grouped[c][:, ph, b].rearrange("p t j -> p (t j)"),
                )

        x_ps = {}
        acc = {}
        y_ps = {}

        def source(ph, t):
            src = (ph - t) % PHASES
            return src, (t + src - ph) // PHASES

        def side_taps(n):
            g = units[n][1]
            count = SCALAR_SIDES[units[n][0]][n % (n_units // PROJ)]
            if g == 1:
                return list(range(1, 1 + count))
            return [TAPS[g] - 1] + list(range(1, count))

        def sides(n):
            return [(t, ph) for t in side_taps(n) for ph in range(PHASES)]

        def side(n, t, ph):
            pr, g, f = units[n]
            if g > 1 and t == TAPS[g] - 1:
                return far[g][f][:, ph]
            return near[n % (2 * LEAD)][:, ph]

        def multiply(n, ph, out, first, count):
            pr, g, f = units[n]
            pg = pr * GROUPS + g
            cols = slice(f * P, (f + 1) * P)
            steps = slice(first * HALF, (first + count) * HALF)
            for c in range(PASSES):
                nc.tensor.matmul_mx(
                    out=out[:].rearrange("p b i -> p (b i)"),
                    lhsT=w_codes[:, pg, c, cols].bitcast(FP8X4), lhsT_scale=w_scales[:, pg, c, cols],
                    rhs=x_codes[:, c, ph, steps].bitcast(FP8X4), rhs_scale=x_scales[:, c, ph, steps],
                    start=(c == 0), stop=(c == PASSES - 1),
                )

        def project(n):
            for ph in range(PHASES):
                x_ps[(n, ph)] = psum.tile([P, B, HALF], F32, name="x_b", tag="x", bufs=LEAD * PHASES)
                multiply(n, ph, x_ps[(n, ph)], 0, B)

        def project_first(b):
            for ph in range(PHASES):
                if b == 0:
                    x_first = psum.tile([P, 1, HALF], F32, name="x_first0", tag="x", bufs=LEAD * PHASES)
                else:
                    x_first = psum.tile([P, 1, HALF], F32, name="x_first1", tag="y", bufs=Y_BANKS)
                x_ps[(0, ph, b)] = x_first
                multiply(0, ph, x_first, b, 1)

        def products(n, src, b):
            if n == 0:
                return x_ps[(n, src, b)][:]
            return x_ps[(n, src)][:, entries(b)]

        def entries(b):
            return slice(0, B) if b is None else slice(b, b + 1)

        def first_tap(n, src, b=None):
            pr, g, f = units[n]
            if b in (None, 0):
                acc[(n, src)] = acc_pool.tile([P, B, HALF], F32, name="acc")
            first = 0
            if g == 1:
                first = 1
                nc.scalar.activation(
                    out=acc[(n, src)][:, :, 0:first], in_=products(n, src, b)[:, :, 0:first], func=IDENTITY,
                    scale=weight(pr, g, 0), bias=edge_beta[:, block(pr, g), f, src:src + 1],
                )
            nc.scalar.activation(
                out=acc[(n, src)][:, entries(b), first:], in_=products(n, src, b)[:, :, first:], func=IDENTITY,
                scale=weight(pr, g, 0), bias=beta[:, block(pr, g), f:f + 1],
            )

        def scalar_sides(n, src, b=None):
            pr, g, f = units[n]
            for t, ph in sides(n):
                if source(ph, t)[0] == src:
                    nc.scalar.activation(
                        out=side(n, t, ph)[:, entries(b), HALO:], in_=products(n, src, b), func=COPY, scale=weight(pr, g, t),
                    )

        def scalar_taps(n):
            for src in range(PHASES):
                first_tap(n, src)
                scalar_sides(n, src)

        def partial_sum(n, ph, t, b, u):
            if t == 0:
                return acc[(n, ph)][:, entries(b), u:]
            shift = source(ph, t)[1]
            return side(n, t, ph)[:, entries(b), HALO + u - shift:HALO + HALF - shift]

        def vector_taps(n, src, b=None):
            pr, g, f = units[n]
            begun = [[0] + side_taps(n) if n > 0 else [0] for ph in range(PHASES)]
            taps = []
            for ph in range(PHASES):
                sums = [t for t in begun[ph] if source(ph, t)[0] == src] or begun[ph]
                others = [t for t in range(1, TAPS[g]) if source(ph, t)[0] == src and (t, ph) not in sides(n)]
                taps.append([(t, ph, sums[i % len(sums)]) for i, t in enumerate(others)])
            order = (1 - src, src) if n > 0 and (len(taps[0]) != len(taps[1]) or 1 in side_taps(n)) else (0, 1)
            for i in range(max(len(taps[0]), len(taps[1]))):
                for ph in order:
                    if i < len(taps[ph]):
                        t, ph, begin = taps[ph][i]
                        u = source(ph, t)[1]
                        total = partial_sum(n, ph, begin, b, u)
                        nc.vector.scalar_tensor_tensor(
                            out=total, in0=products(n, src, b)[:, :, 0:HALF - u], scalar=weight(pr, g, t), in1=total,
                            op0=MULT, op1=ADD,
                        )

        def transpose_blocks(n, ph, b, out):
            for blk in range(BLOCKS):
                parts = [acc[(n, ph)][:, b, blk * P:(blk + 1) * P]]
                for t, to in sides(n):
                    if to == ph:
                        first = HALO + blk * P - source(ph, t)[1]
                        parts.append(side(n, t, ph)[:, b, first:first + P])
                for k in range(len(parts)):
                    nc.tensor.matmul(
                        out=out[:, :, blk, :], lhsT=parts[k], rhs=ident_f32[:].rearrange("p (h d) -> p h d", d=D), is_transpose=True,
                        start=(k == 0), stop=(k == len(parts) - 1),
                    )

        def transposes(n):
            for ph in range(PHASES):
                y_ps[(n, ph)] = psum.tile([P, B, HEADS, BLOCKS, D], F32, name="y_b", tag="y", bufs=Y_BANKS)
                for b in range(B):
                    transpose_blocks(n, ph, b, y_ps[(n, ph)][:, b])

        def store(n, b, o_sb):
            pr, g, f = units[n]
            first = (g * TILES + f) * HEADS
            nc.sync.dma_start(
                out=outs[pr][b, first:first + HEADS].rearrange("h (k p a) d -> p (h k) (a d)", p=P, a=PHASES),
                in_=o_sb.rearrange("p h k a d -> p (h k) (a d)"),
            )

        def evacuate(n):
            o_sb = out_pool.tile([P, B, HEADS, BLOCKS, PHASES, D], F32, name="o_sb")
            for ph in range(PHASES):
                nc.scalar.copy(
                    out=o_sb[:, :, :, :, ph, :].rearrange("p b h k d -> p (b h k) d"),
                    in_=y_ps[(n, ph)][:].rearrange("p b h k d -> p (b h k) d"),
                )
            for b in range(B):
                store(n, b, o_sb[:, b])

        def finish_last(b):
            n = n_units - 1
            o_last = out_pool.tile([P, HEADS, BLOCKS, PHASES, D], F32, name="o_last")
            for ph in range(PHASES):
                if b == 0:
                    y_last = psum.tile([P, HEADS, BLOCKS, D], F32, name="y_last0", tag="y", bufs=Y_BANKS)
                else:
                    y_last = psum.tile([P, HEADS, BLOCKS, D], F32, name="y_last1", tag="x", bufs=LEAD * PHASES)
                transpose_blocks(n, ph, b, y_last[:])
                copy_out = nc.vector.tensor_copy if (b, ph) == (1, 1) else nc.scalar.copy
                copy_out(
                    out=o_last[:, :, :, ph, :].rearrange("p h k d -> p (h k) d"), in_=y_last[:].rearrange("p h k d -> p (h k) d"))
            store(n, b, o_last[:])

        z_ps = {}

        def project_plain(k):
            pr, b, blk = plain_units[k]
            pg = pr * GROUPS
            z_ps[k] = psum.tile([P, PHASES, GROUP_COLS], F32, name="z_b", tag="y", bufs=Y_BANKS)
            first = b * HALF + blk * P
            for ph in range(PHASES):
                for c in range(PASSES):
                    nc.tensor.matmul_mx(
                        out=z_ps[k][:, ph, :],
                        lhsT=x_codes[:, c, ph, first:first + P].bitcast(FP8X4), lhsT_scale=x_scales[:, c, ph, first:first + P],
                        rhs=w_codes[:, pg, c, :].bitcast(FP8X4), rhs_scale=w_scales[:, pg, c, :],
                        start=(c == 0), stop=(c == PASSES - 1),
                    )

        def finish_plain(k):
            pr, b, blk = plain_units[k]
            o_plain = out_pool.tile([P, GROUP_COLS // D, PHASES, D], F32, name="o_plain")
            nc.vector.tensor_tensor(
                out=o_plain[:].rearrange("p h a d -> p a h d"), in0=z_ps[k][:].rearrange("p a (h d) -> p a h d", d=D),
                in1=plain_bias[:, pr * TILES:(pr + 1) * TILES, :].rearrange("p f (h d) -> p (f h) d", d=D)
                .unsqueeze(1).to_broadcast([P, PHASES, GROUP_COLS // D, D]),
                op=ADD,
            )
            nc.sync.dma_start(
                out=outs[pr][b, 0:GROUP_COLS // D, blk * P * PHASES:(blk + 1) * P * PHASES, :]
                .rearrange("h (p a) d -> p h (a d)", a=PHASES),
                in_=o_plain[:].rearrange("p h a d -> p h (a d)"),
            )

        def quantise_for(n):
            for j in quantise_at.get(n, []):
                quantise(j)

        def hold_gpsimd(scales):
            nc.gpsimd.tensor_copy(out=held[:], in_=scales)

        def regroup_for(n):
            for j in quantise_at.get(n, []):
                if j in REGROUP_AFTER:
                    pr, g = group_seq[j]
                    hold_gpsimd(w_scales[:, pr * GROUPS + g, PASSES - 1, GROUP_COLS - 1:GROUP_COLS])
                    for coming in REGROUP_AFTER[j]:
                        regroup_on_gpsimd(coming)

        def finish_unit(n):
            for k in plain_at.get(n + 1, []):
                finish_plain(k)
            if n + LEAD < n_units:
                project(n + LEAD)
            for k in plain_at.get(n + LEAD, []):
                project_plain(k)
            if n >= 1:
                evacuate(n - 1)
            transposes(n)
            if n >= LEAD:
                pr, g, f = units[n - LEAD]
                if f == TILES - 1 and pr + 1 < PROJ:
                    derive_biases(pr + 1, g)
                    if g > 1:
                        correct_edge(pr + 1, g)
            if n == 0:
                spread_parameters(lead + 1, PROJ * CONV_GROUPS)
            if n == LEAD - 1:
                take_parameters(lead + 1, PROJ * CONV_GROUPS)
            if n + LEAD < n_units:
                scalar_taps(n + LEAD)

        for i in range(WARM_UP):
            if i % 4 == 0:
                warm_ps = psum.tile([P, 4, P], F32, name="warm_ps", tag="y", bufs=Y_BANKS)
            nc.tensor.matmul(out=warm_ps[:, i % 4, :], lhsT=ident_bf[:], rhs=ident_bf[:], start=True, stop=True)
        spread_attn_bias()
        first_g = CONV_ORDER[0]
        lead = block(0, first_g)
        spread_parameters(lead, lead + 1)
        take_parameters(lead, lead + 1)
        prepare_first_group(0)
        sum_taps(lead, lead + 1)
        copies = (nc.scalar.copy, nc.scalar.copy)
        transpose_x(0, 0, copies)
        quantise_first_group(0)
        quantise_x(0, 0)
        transpose_x(1, 0, copies)
        prepare_first_group(1)
        quantise_x(1, 0)
        quantise_first_group(1)
        transpose_x(0, 1, (nc.scalar.copy, nc.vector.tensor_copy))
        quantise_x(0, 1)
        derive_biases(0, first_g)
        correct_edge(0, first_g)
        project_first(0)
        for src in range(PHASES):
            first_tap(0, src, 0)
        transpose_x(1, 1, copies)
        vector_taps(0, 0, 0)
        quantise_x(1, 1)
        hold_gpsimd(x_scales[:, PASSES - 1, PHASES - 1, B * HALF - 1:B * HALF])
        regroup_on_gpsimd(1)
        vector_taps(0, 1, 0)
        spread_parameters(0, lead)
        project_first(1)
        project(1)
        for src in range(PHASES):
            first_tap(0, src, 1)
        take_parameters(0, lead)
        for src in range(PHASES):
            scalar_sides(0, src, 0)
        scalar_taps(1)
        vector_taps(0, 0, 1)
        vector_taps(0, 1, 1)
        sum_taps(0, lead)
        quantise_for(0)
        regroup_for(0)
        for src in range(PHASES):
            scalar_sides(0, src, 1)
        for g in (2, 1):
            derive_biases(0, g)
        correct_edge(0, 2)
        finish_unit(0)

        for n in range(1, n_units - 1):
            vector_taps(n, 0)
            vector_taps(n, 1)
            quantise_for(n)
            if n == LEAD:
                sum_taps(lead + 1, PROJ * CONV_GROUPS)
            regroup_for(n)
            finish_unit(n)
        evacuate(n_units - 2)
        for b in range(B):
            for src in range(PHASES):
                vector_taps(n_units - 1, src, b)
            finish_last(b)
